import numpy as np
import ml_dtypes


def mxq(x, axis, fmt="e4m3"):
    dtype, down = {"e4m3": (ml_dtypes.float8_e4m3fn, 7), "e5m2": (ml_dtypes.float8_e5m2, 14)}[fmt]
    v = np.moveaxis(np.asarray(x, np.float32).astype(ml_dtypes.bfloat16).astype(np.float64), axis, -1)
    blocks = v.reshape(v.shape[:-1] + (-1, 32))
    amax = np.abs(blocks).max(-1, keepdims=True)
    byte = np.maximum(np.where(amax > 0, np.frexp(amax)[1] - 1 + 127, 0) - down, 1)
    scale = np.exp2(byte - 127.0)
    codes = (blocks / scale).astype(np.float32).astype(dtype).astype(np.float64)
    return np.moveaxis((codes * scale).reshape(v.shape), -1, axis)


WIDE = False


def mx_kscale(k):
    if not WIDE:
        return np.ones(k)
    levels = np.array([18, -18])
    if k % 512:
        return np.exp2(np.random.permutation(np.resize(levels, k // 32))).repeat(32)
    a = np.empty((k // 512, 16))
    for p in range(k // 512):
        a[p, :8] = np.random.permutation(np.resize(levels, 8))
        for g in range(8):
            far = levels[np.abs(levels - a[p, g]) >= 10]
            a[p, g + 8] = far[np.random.randint(len(far))]
    return np.exp2(a.ravel()).repeat(32)


BF16 = ml_dtypes.bfloat16


def bf(x):
    return np.asarray(x, np.float32).astype(BF16)


def f64(x):
    return np.asarray(x).astype(np.float64)


B, S, D, H, DH, DL, DR = 2, 512, 2048, 16, 128, 512, 64
ROPE_BASE = 10000.0
T = B * S
J = H * (DH + DR)


def rope_tables():
    inv_freq = 1.0 / ROPE_BASE ** (np.arange(0, DR, 2) / DR)
    freqs = np.arange(S)[:, None] * inv_freq[None, :]
    emb = np.concatenate([freqs, freqs], axis=-1)
    return np.cos(emb), np.sin(emb)


def rotate_half(u):
    u1, u2 = np.split(u, 2, axis=-1)
    return np.concatenate([-u2, u1], axis=-1)


def rotate_half_back(u):
    u1, u2 = np.split(u, 2, axis=-1)
    return np.concatenate([u2, -u1], axis=-1)


def setup_inputs():
    s = mx_kscale(T)
    v = mx_kscale(DL)
    u = np.array(mx_kscale(J)).reshape(H, DH + DR)
    u[:, DH + DR // 2:] = u[:, DH:DH + DR // 2]
    x0 = bf(np.random.standard_normal((B, S, D)))
    wd0 = bf(np.random.standard_normal((D, DL)) / np.sqrt(D))
    wu0 = bf(np.random.standard_normal((DL, J)) / np.sqrt(DL))
    g = bf(np.random.standard_normal((B, S, H, DH + DR)) * np.exp2(np.random.randint(-6, 1, (B, S, 1, 1))) / s.reshape(B, S, 1, 1) * u)
    cos, sin = rope_tables()
    return {"x": bf(f64(x0) * s.reshape(B, S, 1)),
            "W_q_down": bf(f64(wd0) / v),
            "W_q_up": bf(f64(wu0) * v[:, None] / u.reshape(J)),
            "rope_cos": np.asarray(cos, np.float32),
            "rope_sin": np.asarray(sin, np.float32),
            "grad_out": g}


def reference(x, W_q_down, W_q_up, rope_cos, rope_sin, grad_out):
    g = f64(grad_out)
    cos, sin = f64(rope_cos)[None, :, None, :], f64(rope_sin)[None, :, None, :]
    gr = g[..., DH:]
    dr = gr * cos + rotate_half_back(gr * sin)
    dz2 = np.concatenate([g[..., :DH], dr], axis=-1).reshape(T, J)
    dz1 = mxq(dz2, 1, "e5m2") @ mxq(f64(W_q_up), 1, "e4m3").T
    dx = mxq(dz1, 1, "e5m2") @ mxq(f64(W_q_down), 1, "e4m3").T
    dw = mxq(f64(x).reshape(T, D), 0, "e4m3").T @ mxq(dz1, 0, "e5m2")
    return dx.reshape(B, S, D), dw

@@ -1,0 +1,467 @@
+from contextlib import ExitStack
+
+import concourse.mybir as mybir
+from concourse.masks import make_identity
+
+B, S, D, H, DH, DL, DR = 2, 512, 2048, 16, 128, 512, 64
+T = B * S
+J = H * (DH + DR)
+FLOPS = 2 * T * J * DL + 2 * T * DL * D + 2 * D * T * DL
+
+F32 = mybir.dt.float32
+BF16 = mybir.dt.bfloat16
+U32 = mybir.dt.uint32
+U8 = mybir.dt.uint8
+E4M3 = mybir.dt.float8_e4m3fn_x4
+E5M2 = mybir.dt.float8_e5m2_x4
+MULT = mybir.AluOpType.mult
+ADD = mybir.AluOpType.add
+SUB = mybir.AluOpType.subtract
+
+P = 128
+PASSES = J // 512
+TILES = T // P
+GTILES = S // P
+HF = DH + DR
+
+
+def tile_multilatentattention_pb_v_kernel(tc, x, wd, wu, rope_cos, rope_sin, g, out_0, out_1):
+    nc = tc.nc
+
+    g_view = g.rearrange("b (p j) h f -> b p j (h f)", j=4)
+    x_view = x.rearrange("b (p j) d -> b p j d", j=4)
+    wu_view = wu.rearrange("(p u e) f -> p u e f", u=2, e=2)
+    wd_view = wd.rearrange("(n p i) l -> p n i l", p=P, i=4)
+    cos_view = rope_cos.rearrange("(p j) r -> p j r", j=4)
+    sin_view = rope_sin.rearrange("(p j) r -> p j r", j=4)
+    out0_view = out_0.rearrange("b (p j) d -> b p j d", j=4)
+    out1_view = out_1.rearrange("(n h p i) l -> p n h i l", h=2, p=P, i=2)
+
+    with ExitStack() as ctx:
+        keep = ctx.enter_context(tc.tile_pool(name="keep", bufs=1))
+        raw = ctx.enter_context(tc.tile_pool(name="raw", bufs=7))
+        work = ctx.enter_context(tc.tile_pool(name="work", bufs=2))
+        psum = ctx.enter_context(tc.psum_pool(name="psum", bufs=8))
+
+        ident = keep.tile([P, P], F32, align_bytes=64)
+        make_identity(nc, ident[:])
+        warm = keep.tile([P, 16], F32, align_bytes=64)
+        nc.vector.memset(warm[:], 0.0)
+        warm2 = keep.tile([P, 16], F32, align_bytes=64)
+
+        cos_t = keep.tile([P, 4, DR], F32, align_bytes=64)
+        sin_t = keep.tile([P, 4, DR], F32, align_bytes=64)
+        wu_codes = keep.tile([P, PASSES, DL], U32, align_bytes=64)
+        wu_scales = keep.tile([P, PASSES, DL], U8, align_bytes=64)
+        wd_codes = keep.tile([P, D], U32, align_bytes=64)
+        wd_scales = keep.tile([P, D], U8, align_bytes=64)
+        x_codes = keep.tile([P, B, D], U32, align_bytes=64)
+        x_scales = keep.tile([P, B, D], U8, align_bytes=64)
+
+        zeros = keep.tile([P, 512], BF16, align_bytes=64)
+        nc.vector.memset(zeros[:], 0.0)
+
+        with tc.manual_schedule():
+            nc.scalar.copy(out=warm2[:], in_=warm[:])
+
+            def load_g(k):
+                t = raw.tile([P, H, HF], BF16, name="g_raw", tag="rawa", align_bytes=64)
+                nc.sync.dma_start(out=t[:], in_=g[k // 4].rearrange("(p j) h f -> p j h f", j=4)[:, k % 4])
+                return t
+
+            def load_wu(u, half):
+                t = raw.tile([P, 2, J // 2], BF16, name="wu_raw", tag="rawa", align_bytes=64)
+                nc.sync.dma_start(out=t[:], in_=wu_view[:, u, :, half * (J // 2) : (half + 1) * (J // 2)])
+                return t
+
+            def load_wd(c):
+                t = raw.tile([P, 4, DL], BF16, name="wd_raw", tag="rawa", align_bytes=64)
+                nc.sync.dma_start(out=t[:], in_=wd_view[:, c])
+                return t
+
+            def load_x(b):
+                t = keep.tile([P, 4, D], BF16, name=f"x_raw{b}", align_bytes=64)
+                nc.sync.dma_start(out=t[:], in_=x_view[b])
+                return t
+
+            wu_raw = {}
+            g_raw = {}
+            wd_raw = {}
+            x_raw = {}
+            g0_parts = []
+
+            def load_g0(half):
+                t = keep.tile([P, H // 2, HF], BF16, name=f"g0_{half}", align_bytes=64)
+                nc.sync.dma_start(out=t[:], in_=g[0].rearrange("(p j) h f -> p j h f", j=4)[:, 0, half * 8 : half * 8 + 8])
+                g0_parts.append(t)
+
+            nc.sync.dma_start(out=cos_t[:, 0:1, :], in_=cos_view[:, 0:1, :])
+            nc.sync.dma_start(out=sin_t[:, 0:1, :], in_=sin_view[:, 0:1, :])
+            wu_raw[0, 0] = load_wu(0, 0)
+            load_g0(0)
+            load_g0(1)
+            wu_raw[1, 0] = load_wu(1, 0)
+            nc.sync.dma_start(out=cos_t[:, 1:4, :], in_=cos_view[:, 1:4, :])
+            nc.sync.dma_start(out=sin_t[:, 1:4, :], in_=sin_view[:, 1:4, :])
+            g_raw[1] = load_g(1)
+            wu_raw[0, 1] = load_wu(0, 1)
+            wu_raw[1, 1] = load_wu(1, 1)
+            for c in range(2):
+                g_raw[2 + c] = load_g(2 + c)
+                wd_raw[2 * c] = load_wd(2 * c)
+                wd_raw[2 * c + 1] = load_wd(2 * c + 1)
+            for k in range(4, TILES):
+                g_raw[k] = load_g(k)
+            for b in range(B):
+                x_raw[b] = load_x(b)
+
+            def copy_out(engine, out, in_):
+                if engine == "v":
+                    nc.vector.tensor_copy(out=out, in_=in_)
+                else:
+                    nc.scalar.copy(out=out, in_=in_)
+
+            def new_bank(warm=0):
+                bank = psum.tile([P, 512], F32, name="bank", tag="bank")
+                for i in range(warm):
+                    nc.tensor.matmul(bank[:], lhsT=zeros[:, :P], rhs=zeros[:], start=True, stop=True)
+                return bank
+
+            grp = {}
+            ropes = {}
+
+            def rope_mul(parts, k):
+                res = []
+                for t in parts:
+                    heads = t.shape[1]
+                    gr = t[:, :, DH:HF]
+                    pc = work.tile([P, H, DR], F32, name="pc", tag="pc", bufs=2, align_bytes=64)
+                    ps = work.tile([P, H, DR], F32, name="ps", tag="ps", bufs=2, align_bytes=64)
+                    shape = [P, heads, DR]
+                    nc.vector.tensor_tensor(out=pc[:, :heads], in0=gr, in1=cos_t[:, k % 4, :].unsqueeze(1).to_broadcast(shape), op=MULT)
+                    nc.vector.tensor_tensor(out=ps[:, :heads], in0=gr, in1=sin_t[:, k % 4, :].unsqueeze(1).to_broadcast(shape), op=MULT)
+                    res.append((t, pc, ps, heads))
+                return res
+
+            def rope_add(items, k):
+                for t, pc, ps, n in items:
+                    nc.vector.tensor_tensor(out=t[:, :, DH : DH + 32], in0=pc[:, :n, 0:32], in1=ps[:, :n, 32:64], op=ADD)
+                    nc.vector.tensor_tensor(out=t[:, :, DH + 32 : HF], in0=pc[:, :n, 32:64], in1=ps[:, :n, 0:32], op=SUB)
+
+            def wu_bank(u, s, warm=0):
+                src = wu_raw[u, s // 3]
+                bank = new_bank(warm)
+                for e in range(2):
+                    words = src[:, e, (s % 3) * 512 : (s % 3 + 1) * 512].bitcast(F32)
+                    for w in range(2):
+                        q = 2 * e + w
+                        nc.tensor.transpose(bank[:, q * P : (q + 1) * P], words[:, w:256:2], ident[:])
+                grouped = work.tile([P, 1024], BF16, name="wu_grp", tag="wgrp", bufs=3, align_bytes=64)
+                nc.scalar.copy(
+                    out=grouped[:].bitcast(F32).rearrange("p (m e w) -> p m e w", e=2, w=2),
+                    in_=bank[:].rearrange("p (e w m) -> p m e w", e=2, w=2),
+                )
+                return u, s, grouped
+
+            def wu_quant(item):
+                u, s, grouped = item
+                nc.vector.quantize_mx(
+                    out=wu_codes[:, s, 256 * u : 256 * u + 256].bitcast(E4M3),
+                    scales=wu_scales[:, s, 256 * u : 256 * u + 256],
+                    in_=grouped[:],
+                )
+
+            wd_grp = {}
+
+            def wd_bank(n, warm=0):
+                c, half = n // 2, n % 2
+                if half == 0:
+                    wd_grp[c] = work.tile([P, 512, 4], BF16, name="wd_grp", tag="xgrp", bufs=3, align_bytes=64)
+                bank = new_bank(warm)
+                for i in range(2):
+                    words = wd_raw[c][:, 2 * half + i, :].bitcast(F32)
+                    for w in range(2):
+                        q = 2 * i + w
+                        nc.tensor.transpose(bank[:, q * P : (q + 1) * P], words[:, w:256:2], ident[:])
+                nc.scalar.copy(
+                    out=wd_grp[c][:].rearrange("p c t -> p (c t)").bitcast(F32).rearrange("p (m i w) -> p m i w", i=4, w=2)[:, :, 2 * half : 2 * half + 2, :],
+                    in_=bank[:].rearrange("p (i w m) -> p m i w", i=2, w=2),
+                )
+
+            def wd_quant(c):
+                nc.vector.quantize_mx(
+                    out=wd_codes[:, 512 * c : 512 * c + 512].bitcast(E4M3),
+                    scales=wd_scales[:, 512 * c : 512 * c + 512],
+                    in_=wd_grp[c][:].rearrange("p c t -> p (c t)"),
+                )
+
+            def g_words(k, s):
+                if k == 0:
+                    flat = g0_parts[s // 3][:].rearrange("p h f -> p (h f)")
+                    s = s % 3
+                else:
+                    flat = g_raw[k][:].rearrange("p h f -> p (h f)")
+                return flat[:, 512 * s : 512 * s + 512].bitcast(F32)
+
+            def dz2_bank(k, c, warm=0):
+                if c == 0:
+                    grp[k] = work.tile([P, J], BF16, name="g_grp", tag="ggrp", bufs=2, align_bytes=64)
+                bank = new_bank(warm)
+                for i in range(2):
+                    words = g_words(k, 2 * c + i)
+                    for w in range(2):
+                        q = 2 * i + w
+                        nc.tensor.transpose(bank[:, q * P : (q + 1) * P], words[:, w:256:2], ident[:])
+                return bank
+
+            def dz2_copy(k, c, bank):
+                nc.scalar.copy(
+                    out=grp[k][:, 1024 * c : 1024 * c + 1024].bitcast(F32).rearrange("p (i r w) -> p i r w", i=2, w=2),
+                    in_=bank[:].rearrange("p (i w r) -> p i r w", i=2, w=2),
+                )
+
+            dz2 = {}
+
+            def dz2_quant(k, grouped):
+                codes = work.tile([P, PASSES, P], U32, name="dz2_codes", tag="dz2c", bufs=3, align_bytes=64)
+                scales = work.tile([P, PASSES, P], U8, name="dz2_scales", tag="dz2s", bufs=3, align_bytes=64)
+                for a, b in ((0, 4), (4, 6)):
+                    nc.vector.quantize_mx(
+                        out=codes[:, a:b, :].rearrange("p s r -> p (s r)").bitcast(E5M2),
+                        scales=scales[:, a:b, :].rearrange("p s r -> p (s r)"),
+                        in_=grouped[:, 512 * a : 512 * b],
+                    )
+                dz2[k] = (codes, scales)
+
+            dz1_tok = {}
+            acc = {}
+
+            def stage1(k, lo=0, hi=PASSES):
+                codes, scales = dz2[k]
+                if lo == 0:
+                    acc[k] = new_bank()
+                for s in range(lo, hi):
+                    nc.tensor.matmul_mx(
+                        out=acc[k][:],
+                        lhsT=codes[:, s, :].bitcast(E5M2),
+                        lhsT_scale=scales[:, s, :],
+                        rhs=wu_codes[:, s, :].bitcast(E4M3),
+                        rhs_scale=wu_scales[:, s, :],
+                        start=(s == 0),
+                        stop=(s == PASSES - 1),
+                    )
+
+            def stage1_copy(k):
+                if k % GTILES == 0:
+                    dz1_tok[k // GTILES] = work.tile([P, GTILES, DL], BF16, name="dz1_tok", tag="dz1t", bufs=2, align_bytes=64)
+                nc.scalar.copy(out=dz1_tok[k // GTILES][:, k % GTILES, :], in_=acc[k][:])
+
+            dz1f_grp = {}
+
+            def dz1_transpose(k):
+                words = dz1_tok[k // GTILES][:, k % GTILES, :].bitcast(F32)
+                bank = new_bank()
+                for u in range(2):
+                    nc.tensor.transpose(bank[:, u * P : (u + 1) * P], words[:, u * P : (u + 1) * P], ident[:])
+                grouped = work.tile([P, DL], BF16, name="dz1f_grp", tag="dz1fg", bufs=2, align_bytes=64)
+                nc.scalar.copy(
+                    out=grouped[:].bitcast(F32).rearrange("p (r u) -> p r u", u=2),
+                    in_=bank[:, : 2 * P].rearrange("p (u r) -> p r u", u=2),
+                )
+                dz1f_grp[k] = grouped
+
+            dz1f = {}
+
+            def dz1f_quant(k):
+                codes = work.tile([P, P], U32, name="dz1f_codes", tag="dz1fc", bufs=3, align_bytes=64)
+                scales = work.tile([P, P], U8, name="dz1f_scales", tag="dz1fs", bufs=3, align_bytes=64)
+                nc.vector.quantize_mx(out=codes[:].bitcast(E5M2), scales=scales[:], in_=dz1f_grp[k][:])
+                dz1f[k] = (codes, scales)
+
+            res0 = {}
+
+            def out0_part(k, n, engine):
+                codes, scales = dz1f[k]
+                if n == 0:
+                    res0[k] = work.tile([P, D], F32, name="res0", tag="res0", bufs=2, align_bytes=64)
+                bank = new_bank()
+                nc.tensor.matmul_mx(
+                    out=bank[:],
+                    lhsT=codes[:].bitcast(E5M2),
+                    lhsT_scale=scales[:],
+                    rhs=wd_codes[:, 512 * n : 512 * n + 512].bitcast(E4M3),
+                    rhs_scale=wd_scales[:, 512 * n : 512 * n + 512],
+                    start=True,
+                    stop=True,
+                )
+                copy_out(engine, res0[k][:, 512 * n : 512 * n + 512], bank[:])
+                if n % 2 == 1:
+                    lo = 1024 * (n // 2)
+                    nc.sync.dma_start(out=out0_view[k // GTILES][:, k % GTILES, lo : lo + 1024], in_=res0[k][:, lo : lo + 1024])
+
+            dz1 = {}
+            dz1_grp = {}
+
+            def dz1_interleave(b, engine, lo, hi):
+                if lo == 0:
+                    dz1_grp[b] = work.tile([P, DL, 4], BF16, name="dz1_grp", tag="xgrp", bufs=3, align_bytes=64)
+                copy_out(
+                    engine,
+                    dz1_grp[b][:, lo:hi, :].rearrange("p (g l) t -> p g t l", l=4),
+                    dz1_tok[b][:, :, lo:hi].rearrange("p t (g l) -> p g t l", l=4),
+                )
+
+            def dz1_quant(b):
+                codes = keep.tile([P, DL], U32, name=f"dz1_codes{b}", align_bytes=64)
+                scales = keep.tile([P, DL], U8, name=f"dz1_scales{b}", align_bytes=64)
+                nc.vector.quantize_mx(
+                    out=codes[:].bitcast(E5M2), scales=scales[:], in_=dz1_grp[b][:].rearrange("p c t -> p (c t)")
+                )
+                dz1[b] = (codes, scales)
+
+            x_grp = {}
+
+            def x_interleave(n, b):
+                grouped = work.tile([P, 512, 4], BF16, name="x_grp", tag="xgrp", bufs=3, align_bytes=64)
+                for i in range(2):
+                    nc.vector.tensor_copy(
+                        out=grouped[:, 256 * i : 256 * i + 256, :].rearrange("p (g l) t -> p g t l", l=4),
+                        in_=x_raw[b][:, :, 512 * n + i : 512 * n + 512 : 2].rearrange("p t (g l) -> p g t l", l=4),
+                    )
+                x_grp[n, b] = grouped
+
+            def x_quant(n, b):
+                nc.vector.quantize_mx(
+                    out=x_codes[:, b, 512 * n : 512 * n + 512].bitcast(E4M3),
+                    scales=x_scales[:, b, 512 * n : 512 * n + 512],
+                    in_=x_grp[n, b][:].rearrange("p c t -> p (c t)"),
+                )
+
+            res1 = {}
+            acc1 = {}
+
+            def out1_pass(j, b):
+                n, h, i = j // 4, j // 2 % 2, j % 2
+                a = 4 * n + 2 * i + h
+                codes, scales = dz1[b]
+                if b == 0:
+                    acc1[j] = new_bank()
+                nc.tensor.matmul_mx(
+                    out=acc1[j][:],
+                    lhsT=x_codes[:, b, P * a : P * a + P].bitcast(E4M3),
+                    lhsT_scale=x_scales[:, b, P * a : P * a + P],
+                    rhs=codes[:].bitcast(E5M2),
+                    rhs_scale=scales[:],
+                    start=(b == 0),
+                    stop=(b == B - 1),
+                )
+
+            def out1_copy(j, engine):
+                n, h, i = j // 4, j // 2 % 2, j % 2
+                if i == 0:
+                    res1[j // 2] = work.tile([P, 2, DL], F32, name="res1", tag="res1", bufs=4, align_bytes=64)
+                copy_out(
+                    engine,
+                    res1[j // 2][:, i, :].rearrange("p (m u e) -> p m u e", u=2, e=2),
+                    acc1[j][:].rearrange("p (u m e) -> p m u e", u=2, e=2),
+                )
+                if i == 1:
+                    nc.sync.dma_start(out=out1_view[:, n, h], in_=res1[j // 2][:])
+
+            def rope(k):
+                rope_add(rope_mul([g_raw[k]], k), k)
+
+            def dz2_step(k, cs, warm=0):
+                for c in cs:
+                    dz2_copy(k, c, dz2_bank(k, c, warm if c == cs[0] else 0))
+
+            xs = [(n, b) for n in range(4) for b in range(B)]
+            pend = []
+
+            def x_step():
+                xu = xs.pop(0)
+                x_interleave(*xu)
+                if pend:
+                    x_quant(*pend.pop())
+                pend.append(xu)
+
+            w00 = [wu_bank(0, s, 10 if s == 0 else 0) for s in range(3)]
+            rope_add(rope_mul(g0_parts[:1], 0), 0)
+            w10 = []
+            for s in range(3):
+                wu_quant(w00[s])
+                w10.append(wu_bank(1, s, 4 if s == 0 else 0))
+            dz2_step(0, (0,), 2)
+            rope_add(rope_mul(g0_parts[1:], 0), 0)
+            for item in w10:
+                wu_quant(item)
+            dz2_step(0, (1, 2))
+            rope(1)
+            w01 = [wu_bank(0, s, 2 if s == 3 else 0) for s in range(3, 6)]
+            dz2_quant(0, grp[0])
+            w11 = []
+            for s in range(3):
+                wu_quant(w01[s])
+                w11.append(wu_bank(1, 3 + s, 2 if s == 0 else 0))
+            for item in w11:
+                wu_quant(item)
+            ropes_at = {0: (2,), 1: (3, 4), 2: (5,), 3: (6,), 4: (7,)}
+            left = None
+            for k in range(TILES):
+                if k + 1 < TILES:
+                    dz2_step(k + 1, (0, 1), 2 if k == 0 else 0)
+                if k >= 2:
+                    for n in range(4):
+                        out0_part(k - 2, n, "v" if n == 3 and k in (5, 7) else "s")
+                if k + 1 < TILES:
+                    bank = dz2_bank(k + 1, 2)
+                if k >= 1:
+                    dz1_transpose(k - 1)
+                if k + 1 < TILES:
+                    dz2_copy(k + 1, 2, bank)
+                for j in ropes_at.get(k, ())[:1]:
+                    rope(j)
+                if k == 6:
+                    x_step()
+                    x_step()
+                if k >= 1:
+                    dz1f_quant(k - 1)
+                for j in ropes_at.get(k, ())[1:]:
+                    rope(j)
+                if k >= 1:
+                    stage1(k)
+                    stage1_copy(k)
+                if k < 2:
+                    for n in range(4 * k, 4 * k + 4):
+                        wd_bank(n, (2, 0, 1, 0, 0, 0, 2, 0)[n])
+                    wd_quant(2 * k)
+                if k == 0:
+                    stage1(k)
+                    stage1_copy(k)
+                if k + 1 < TILES:
+                    dz2_quant(k + 1, grp[k + 1])
+                if k < 2:
+                    wd_quant(2 * k + 1)
+                if k == 4:
+                    dz1_interleave(0, "v", 0, DL)
+                if k in (4, 6):
+                    x_step()
+                if k == 4:
+                    dz1_quant(0)
+            for n in range(4):
+                out0_part(6, n, "s")
+                if n == 1:
+                    dz1_transpose(7)
+            dz1_interleave(1, "v", 0, DL)
+            dz1f_quant(7)
+            dz1_quant(1)
+            for n in range(4):
+                out0_part(7, n, "s")
+            for j in range(16):
+                while len(xs) > 0 and xs[0][0] <= (j + 4) // 4:
+                    x_step()
+                if len(pend) > 0 and (pend[0][0] <= j // 4 or len(xs) == 0):
+                    x_quant(*pend.pop())
+                out1_pass(j, 0)
+                out1_pass(j, 1)
+                out1_copy(j, "v" if j in (11, 12, 14) else "s")

@@ -58,8 +58,6 @@ def tile_multilatentattention_pb_v_kernel(tc, x, wd, wu, rope_cos, rope_sin, g, 
         x_codes = keep.tile([P, B, D], U32, align_bytes=64)
         x_scales = keep.tile([P, B, D], U8, align_bytes=64)
 
-        zeros = keep.tile([P, 512], BF16, align_bytes=64)
-        nc.vector.memset(zeros[:], 0.0)
 
         with tc.manual_schedule():
             nc.scalar.copy(out=warm2[:], in_=warm[:])
@@ -123,8 +121,6 @@ def tile_multilatentattention_pb_v_kernel(tc, x, wd, wu, rope_cos, rope_sin, g, 
 
             def new_bank(warm=0):
                 bank = psum.tile([P, 512], F32, name="bank", tag="bank")
-                for i in range(warm):
-                    nc.tensor.matmul(bank[:], lhsT=zeros[:, :P], rhs=zeros[:], start=True, stop=True)
                 return bank
 
             grp = {}

@@ -23,14 +23,16 @@ PASSES = J // 512
 TILES = T // P
 GTILES = S // P
 HF = DH + DR
+KIB = 1024
+SORTED = ()
 
 
 def tile_multilatentattention_pb_v_kernel(tc, x, wd, wu, rope_cos, rope_sin, g, out_0, out_1):
     nc = tc.nc
 
-    g_view = g.rearrange("b (p j) h f -> b p j (h f)", j=4)
+    g_view = g.rearrange("b (p j) h f -> b p j h f", j=4)
     x_view = x.rearrange("b (p j) d -> b p j d", j=4)
-    wu_view = wu.rearrange("(p u e) f -> p u e f", u=2, e=2)
+    wu_view = wu.rearrange("(p r) f -> p r f", r=4)
     wd_view = wd.rearrange("(n p i) l -> p n i l", p=P, i=4)
     cos_view = rope_cos.rearrange("(p j) r -> p j r", j=4)
     sin_view = rope_sin.rearrange("(p j) r -> p j r", j=4)
@@ -39,79 +41,63 @@ def tile_multilatentattention_pb_v_kernel(tc, x, wd, wu, rope_cos, rope_sin, g, 
 
     with ExitStack() as ctx:
         keep = ctx.enter_context(tc.tile_pool(name="keep", bufs=1))
-        raw = ctx.enter_context(tc.tile_pool(name="raw", bufs=7))
+        arena = ctx.enter_context(tc.tile_pool(name="arena", bufs=1))
         work = ctx.enter_context(tc.tile_pool(name="work", bufs=2))
         psum = ctx.enter_context(tc.psum_pool(name="psum", bufs=8))
 
-        ident = keep.tile([P, P], F32, align_bytes=64)
+        ident = keep.tile([P, P], F32, name="ident", align_bytes=64)
         make_identity(nc, ident[:])
-        warm = keep.tile([P, 16], F32, align_bytes=64)
+        warm = keep.tile([P, 16], F32, name="warm", align_bytes=64)
         nc.vector.memset(warm[:], 0.0)
-        warm2 = keep.tile([P, 16], F32, align_bytes=64)
+        warm2 = keep.tile([P, 16], F32, name="warm2", align_bytes=64)
 
-        cos_t = keep.tile([P, 4, DR], F32, align_bytes=64)
-        sin_t = keep.tile([P, 4, DR], F32, align_bytes=64)
-        wu_codes = keep.tile([P, PASSES, DL], U32, align_bytes=64)
-        wu_scales = keep.tile([P, PASSES, DL], U8, align_bytes=64)
-        wd_codes = keep.tile([P, D], U32, align_bytes=64)
-        wd_scales = keep.tile([P, D], U8, align_bytes=64)
-        x_codes = keep.tile([P, B, D], U32, align_bytes=64)
-        x_scales = keep.tile([P, B, D], U8, align_bytes=64)
-
+        cos_t = keep.tile([P, 4, DR], F32, name="cos_t", align_bytes=64)
+        sin_t = keep.tile([P, 4, DR], F32, name="sin_t", align_bytes=64)
+        wu_codes = keep.tile([P, PASSES, DL], U32, name="wu_codes", align_bytes=64)
+        wu_scales = keep.tile([P, PASSES, DL], U8, name="wu_scales", align_bytes=64)
+        wd_codes = keep.tile([P, D], U32, name="wd_codes", align_bytes=64)
+        wd_scales = keep.tile([P, D], U8, name="wd_scales", align_bytes=64)
+        x_codes = keep.tile([P, B, D], U32, name="x_codes", align_bytes=64)
+        x_scales = keep.tile([P, B, D], U8, name="x_scales", align_bytes=64)
 
         with tc.manual_schedule():
             nc.scalar.copy(out=warm2[:], in_=warm[:])
 
-            def load_g(k):
-                t = raw.tile([P, H, HF], BF16, name="g_raw", tag="rawa", align_bytes=64)
-                nc.sync.dma_start(out=t[:], in_=g[k // 4].rearrange("(p j) h f -> p j h f", j=4)[:, k % 4])
-                return t
+            wu_raw, g_raw, wd_raw, x_raw = {}, {}, {}, {}
 
-            def load_wu(u, half):
-                t = raw.tile([P, 2, J // 2], BF16, name="wu_raw", tag="rawa", align_bytes=64)
-                nc.sync.dma_start(out=t[:], in_=wu_view[:, u, :, half * (J // 2) : (half + 1) * (J // 2)])
-                return t
+            def load_tables(lo, hi):
+                nc.sync.dma_start(out=cos_t[:, lo:hi, :], in_=cos_view[:, lo:hi, :])
+                nc.sync.dma_start(out=sin_t[:, lo:hi, :], in_=sin_view[:, lo:hi, :])
+
+            def load_g(k, parts=1):
+                heads = H // parts
+                if parts == 1:
+                    g_raw[k] = [work.tile([P, H, HF], BF16, name=f"g{k}", tag="g", bufs=5, align_bytes=64)]
+                else:
+                    g_raw[k] = [keep.tile([P, heads, HF], BF16, name=f"g{k}_{i}", align_bytes=64) for i in range(parts)]
+
+            def issue_g(k, i=0):
+                if k not in g_raw:
+                    load_g(k)
+                t = g_raw[k][i]
+                heads = t.shape[1]
+                nc.sync.dma_start(out=t[:], in_=g_view[k // GTILES][:, k % GTILES, i * heads : (i + 1) * heads])
+
+            def load_wu(r, lo=0, hi=PASSES):
+                t = arena.tile([P, 512 * (hi - lo)], BF16, name=f"wu{r}_{lo}", offset=KIB * (PASSES * r + lo), align_bytes=64)
+                nc.sync.dma_start(out=t[:], in_=wu_view[:, r, 512 * lo : 512 * hi])
+                for s in range(lo, hi):
+                    wu_raw[r, s] = t[:, 512 * (s - lo) : 512 * (s - lo + 1)]
 
             def load_wd(c):
-                t = raw.tile([P, 4, DL], BF16, name="wd_raw", tag="rawa", align_bytes=64)
+                t = arena.tile([P, 4, DL], BF16, name=f"wd{c}", offset=4 * KIB * (PASSES + c), align_bytes=64)
                 nc.sync.dma_start(out=t[:], in_=wd_view[:, c])
-                return t
+                wd_raw[c] = t
 
             def load_x(b):
-                t = keep.tile([P, 4, D], BF16, name=f"x_raw{b}", align_bytes=64)
+                t = keep.tile([P, 4, D], BF16, name=f"x{b}", align_bytes=64)
                 nc.sync.dma_start(out=t[:], in_=x_view[b])
-                return t
-
-            wu_raw = {}
-            g_raw = {}
-            wd_raw = {}
-            x_raw = {}
-            g0_parts = []
-
-            def load_g0(half):
-                t = keep.tile([P, H // 2, HF], BF16, name=f"g0_{half}", align_bytes=64)
-                nc.sync.dma_start(out=t[:], in_=g[0].rearrange("(p j) h f -> p j h f", j=4)[:, 0, half * 8 : half * 8 + 8])
-                g0_parts.append(t)
-
-            nc.sync.dma_start(out=cos_t[:, 0:1, :], in_=cos_view[:, 0:1, :])
-            nc.sync.dma_start(out=sin_t[:, 0:1, :], in_=sin_view[:, 0:1, :])
-            wu_raw[0, 0] = load_wu(0, 0)
-            load_g0(0)
-            load_g0(1)
-            wu_raw[1, 0] = load_wu(1, 0)
-            nc.sync.dma_start(out=cos_t[:, 1:4, :], in_=cos_view[:, 1:4, :])
-            nc.sync.dma_start(out=sin_t[:, 1:4, :], in_=sin_view[:, 1:4, :])
-            g_raw[1] = load_g(1)
-            wu_raw[0, 1] = load_wu(0, 1)
-            wu_raw[1, 1] = load_wu(1, 1)
-            for c in range(2):
-                g_raw[2 + c] = load_g(2 + c)
-                wd_raw[2 * c] = load_wd(2 * c)
-                wd_raw[2 * c + 1] = load_wd(2 * c + 1)
-            for k in range(4, TILES):
-                g_raw[k] = load_g(k)
-            for b in range(B):
-                x_raw[b] = load_x(b)
+                x_raw[b] = t
 
             def copy_out(engine, out, in_):
                 if engine == "v":
@@ -119,68 +105,107 @@ def tile_multilatentattention_pb_v_kernel(tc, x, wd, wu, rope_cos, rope_sin, g, 
                 else:
                     nc.scalar.copy(out=out, in_=in_)
 
-            def new_bank(warm=0):
-                bank = psum.tile([P, 512], F32, name="bank", tag="bank")
-                return bank
+            def new_bank():
+                return psum.tile([P, 512], F32, name="bank", tag="bank")
 
-            grp = {}
-            ropes = {}
-
-            def rope_mul(parts, k):
-                res = []
-                for t in parts:
-                    heads = t.shape[1]
-                    gr = t[:, :, DH:HF]
-                    pc = work.tile([P, H, DR], F32, name="pc", tag="pc", bufs=2, align_bytes=64)
-                    ps = work.tile([P, H, DR], F32, name="ps", tag="ps", bufs=2, align_bytes=64)
-                    shape = [P, heads, DR]
-                    nc.vector.tensor_tensor(out=pc[:, :heads], in0=gr, in1=cos_t[:, k % 4, :].unsqueeze(1).to_broadcast(shape), op=MULT)
-                    nc.vector.tensor_tensor(out=ps[:, :heads], in0=gr, in1=sin_t[:, k % 4, :].unsqueeze(1).to_broadcast(shape), op=MULT)
-                    res.append((t, pc, ps, heads))
-                return res
-
-            def rope_add(items, k):
-                for t, pc, ps, n in items:
-                    nc.vector.tensor_tensor(out=t[:, :, DH : DH + 32], in0=pc[:, :n, 0:32], in1=ps[:, :n, 32:64], op=ADD)
-                    nc.vector.tensor_tensor(out=t[:, :, DH + 32 : HF], in0=pc[:, :n, 32:64], in1=ps[:, :n, 0:32], op=SUB)
-
-            def wu_bank(u, s, warm=0):
-                src = wu_raw[u, s // 3]
-                bank = new_bank(warm)
-                for e in range(2):
-                    words = src[:, e, (s % 3) * 512 : (s % 3 + 1) * 512].bitcast(F32)
-                    for w in range(2):
-                        q = 2 * e + w
-                        nc.tensor.transpose(bank[:, q * P : (q + 1) * P], words[:, w:256:2], ident[:])
-                grouped = work.tile([P, 1024], BF16, name="wu_grp", tag="wgrp", bufs=3, align_bytes=64)
-                nc.scalar.copy(
-                    out=grouped[:].bitcast(F32).rearrange("p (m e w) -> p m e w", e=2, w=2),
-                    in_=bank[:].rearrange("p (e w m) -> p m e w", e=2, w=2),
-                )
-                return u, s, grouped
-
-            def wu_quant(item):
-                u, s, grouped = item
-                nc.vector.quantize_mx(
-                    out=wu_codes[:, s, 256 * u : 256 * u + 256].bitcast(E4M3),
-                    scales=wu_scales[:, s, 256 * u : 256 * u + 256],
-                    in_=grouped[:],
-                )
-
-            wd_grp = {}
-
-            def wd_bank(n, warm=0):
-                c, half = n // 2, n % 2
-                if half == 0:
-                    wd_grp[c] = work.tile([P, 512, 4], BF16, name="wd_grp", tag="xgrp", bufs=3, align_bytes=64)
-                bank = new_bank(warm)
+            def transpose_pairs(bank, rows):
                 for i in range(2):
-                    words = wd_raw[c][:, 2 * half + i, :].bitcast(F32)
+                    words = rows[i].bitcast(F32)
                     for w in range(2):
                         q = 2 * i + w
                         nc.tensor.transpose(bank[:, q * P : (q + 1) * P], words[:, w:256:2], ident[:])
+
+            prods = {}
+
+            def rope_cos(k, half):
+                parts = g_raw[k]
+                gr = parts[half][:, :, DH:HF] if len(parts) == 2 else parts[0][:, 8 * half : 8 * half + 8, DH:HF]
+                pc = work.tile([P, 8, DR], F32, name="pc", tag="pc", bufs=2, align_bytes=64)
+                ps = work.tile([P, 8, DR], F32, name="ps", tag="ps", bufs=2, align_bytes=64)
+                prods[k, half] = (gr, pc, ps)
+                nc.vector.tensor_tensor(out=pc[:], in0=gr, in1=cos_t[:, k % 4, :].unsqueeze(1).to_broadcast([P, 8, DR]), op=MULT)
+
+            def rope_sin(k, half):
+                gr, pc, ps = prods[k, half]
+                nc.vector.tensor_tensor(out=ps[:], in0=gr, in1=sin_t[:, k % 4, :].unsqueeze(1).to_broadcast([P, 8, DR]), op=MULT)
+
+            def rope_mul(k, half):
+                rope_cos(k, half)
+                rope_sin(k, half)
+
+            sorted_words = {}
+
+            def sort_content(k, engine="v"):
+                if k not in SORTED:
+                    return
+                t = work.tile([P, 2, H, HF // 4], F32, name="sorted", tag="sorted", bufs=2, align_bytes=64)
+                sorted_words[k] = t
+                words = g_raw[k][0][:].bitcast(F32)
+                copy_out(engine, t[:, :, :, : DH // 4], words[:, :, : DH // 2].rearrange("p h (m u) -> p u h m", u=2))
+
+            def rope_add(k, half):
+                gr, pc, ps = prods[k, half]
+                if k not in SORTED:
+                    nc.vector.tensor_tensor(out=gr[:, :, 0:32], in0=pc[:, :, 0:32], in1=ps[:, :, 32:64], op=ADD)
+                    nc.vector.tensor_tensor(out=gr[:, :, 32:64], in0=pc[:, :, 32:64], in1=ps[:, :, 0:32], op=SUB)
+                    return
+                dst = sorted_words[k][:].bitcast(BF16)
+                pc4 = pc[:].rearrange("p h (a m u e) -> p h a m u e", a=2, u=2, e=2)
+                ps4 = ps[:].rearrange("p h (a m u e) -> p h a m u e", a=2, u=2, e=2)
+                for u in range(2):
+                    for a, op in ((0, ADD), (1, SUB)):
+                        lo = DH // 2 + 16 * a
+                        nc.vector.tensor_tensor(
+                            out=dst[:, u, 8 * half : 8 * half + 8, lo : lo + 16].rearrange("p h (m e) -> p h m e", e=2),
+                            in0=pc4[:, :, a, :, u, :],
+                            in1=ps4[:, :, 1 - a, :, u, :],
+                            op=op,
+                        )
+
+            def rope(k):
+                rope_mul(k, 0)
+                rope_mul(k, 1)
+                if k in SORTED:
+                    sort_content(k)
+                rope_add(k, 0)
+                rope_add(k, 1)
+
+            wu_grp = {}
+
+            def wu_bank(r, c):
+                grouped = work.tile([P, 2, 512], BF16, name="wu_grp", tag="wug", bufs=4, align_bytes=64)
+                bank = new_bank()
+                transpose_pairs(bank, [wu_raw[r, 2 * c + i] for i in range(2)])
                 nc.scalar.copy(
-                    out=wd_grp[c][:].rearrange("p c t -> p (c t)").bitcast(F32).rearrange("p (m i w) -> p m i w", i=4, w=2)[:, :, 2 * half : 2 * half + 2, :],
+                    out=grouped[:].rearrange("p i c -> p (i c)").bitcast(F32).rearrange("p (i m w) -> p i m w", i=2, w=2),
+                    in_=bank[:].rearrange("p (i w m) -> p i m w", i=2, w=2),
+                )
+                wu_grp[r, c] = grouped
+
+            def wu_row(r):
+                for c in range(3):
+                    wu_bank(r, c)
+
+            def wu_quant(r, cs=(0, 1, 2)):
+                for c in cs:
+                    for i in range(2):
+                        s = 2 * c + i
+                        nc.vector.quantize_mx(
+                            out=wu_codes[:, s, P * r : P * r + P].bitcast(E4M3),
+                            scales=wu_scales[:, s, P * r : P * r + P],
+                            in_=wu_grp[r, c][:, i, :],
+                        )
+
+            wd_grp = {}
+
+            def wd_bank(n):
+                c, half = n // 2, n % 2
+                if half == 0:
+                    wd_grp[c] = work.tile([P, 2048], BF16, name="wd_grp", tag="xgrp", bufs=3, align_bytes=64)
+                bank = new_bank()
+                transpose_pairs(bank, [wd_raw[c][:, 2 * half + i, :] for i in range(2)])
+                nc.scalar.copy(
+                    out=wd_grp[c][:].bitcast(F32).rearrange("p (m i w) -> p m i w", i=4, w=2)[:, :, 2 * half : 2 * half + 2, :],
                     in_=bank[:].rearrange("p (i w m) -> p m i w", i=2, w=2),
                 )
 
@@ -188,46 +213,47 @@ def tile_multilatentattention_pb_v_kernel(tc, x, wd, wu, rope_cos, rope_sin, g, 
                 nc.vector.quantize_mx(
                     out=wd_codes[:, 512 * c : 512 * c + 512].bitcast(E4M3),
                     scales=wd_scales[:, 512 * c : 512 * c + 512],
-                    in_=wd_grp[c][:].rearrange("p c t -> p (c t)"),
+                    in_=wd_grp[c][:],
                 )
 
-            def g_words(k, s):
-                if k == 0:
-                    flat = g0_parts[s // 3][:].rearrange("p h f -> p (h f)")
-                    s = s % 3
-                else:
-                    flat = g_raw[k][:].rearrange("p h f -> p (h f)")
-                return flat[:, 512 * s : 512 * s + 512].bitcast(F32)
+            def g_pass(k, s):
+                parts = g_raw[k]
+                per = PASSES // len(parts)
+                flat = parts[s // per][:].rearrange("p h f -> p (h f)")
+                return flat[:, 512 * (s % per) : 512 * (s % per) + 512]
 
-            def dz2_bank(k, c, warm=0):
+            dz2_grp = {}
+
+            def dz2_bank(k, c):
                 if c == 0:
-                    grp[k] = work.tile([P, J], BF16, name="g_grp", tag="ggrp", bufs=2, align_bytes=64)
-                bank = new_bank(warm)
-                for i in range(2):
-                    words = g_words(k, 2 * c + i)
-                    for w in range(2):
-                        q = 2 * i + w
-                        nc.tensor.transpose(bank[:, q * P : (q + 1) * P], words[:, w:256:2], ident[:])
-                return bank
-
-            def dz2_copy(k, c, bank):
+                    dz2_grp[k] = work.tile([P, J], BF16, name="dz2_grp", tag="dz2g", bufs=2, align_bytes=64)
+                bank = new_bank()
+                if k in SORTED:
+                    flat = sorted_words[k][:].rearrange("p u h m -> p u (h m)")
+                    for i in range(2):
+                        for w in range(2):
+                            q, s = 2 * i + w, 2 * c + i
+                            nc.tensor.transpose(bank[:, q * P : (q + 1) * P], flat[:, w, P * s : P * s + P], ident[:])
+                else:
+                    transpose_pairs(bank, [g_pass(k, 2 * c + i) for i in range(2)])
                 nc.scalar.copy(
-                    out=grp[k][:, 1024 * c : 1024 * c + 1024].bitcast(F32).rearrange("p (i r w) -> p i r w", i=2, w=2),
+                    out=dz2_grp[k][:, 1024 * c : 1024 * c + 1024].bitcast(F32).rearrange("p (i r w) -> p i r w", i=2, w=2),
                     in_=bank[:].rearrange("p (i w r) -> p i r w", i=2, w=2),
                 )
 
             dz2 = {}
 
-            def dz2_quant(k, grouped):
-                codes = work.tile([P, PASSES, P], U32, name="dz2_codes", tag="dz2c", bufs=3, align_bytes=64)
-                scales = work.tile([P, PASSES, P], U8, name="dz2_scales", tag="dz2s", bufs=3, align_bytes=64)
-                for a, b in ((0, 4), (4, 6)):
-                    nc.vector.quantize_mx(
-                        out=codes[:, a:b, :].rearrange("p s r -> p (s r)").bitcast(E5M2),
-                        scales=scales[:, a:b, :].rearrange("p s r -> p (s r)"),
-                        in_=grouped[:, 512 * a : 512 * b],
-                    )
-                dz2[k] = (codes, scales)
+            def dz2_quant(k, a, b):
+                if a == 0:
+                    codes = work.tile([P, PASSES, P], U32, name="dz2_codes", tag="dz2c", bufs=3, align_bytes=64)
+                    scales = work.tile([P, PASSES, P], U8, name="dz2_scales", tag="dz2s", bufs=3, align_bytes=64)
+                    dz2[k] = (codes, scales)
+                codes, scales = dz2[k]
+                nc.vector.quantize_mx(
+                    out=codes[:, a:b, :].rearrange("p s r -> p (s r)").bitcast(E5M2),
+                    scales=scales[:, a:b, :].rearrange("p s r -> p (s r)"),
+                    in_=dz2_grp[k][:, 512 * a : 512 * b],
+                )
 
             dz1_tok = {}
             acc = {}
@@ -246,11 +272,13 @@ def tile_multilatentattention_pb_v_kernel(tc, x, wd, wu, rope_cos, rope_sin, g, 
                         start=(s == 0),
                         stop=(s == PASSES - 1),
                     )
-
-            def stage1_copy(k):
-                if k % GTILES == 0:
-                    dz1_tok[k // GTILES] = work.tile([P, GTILES, DL], BF16, name="dz1_tok", tag="dz1t", bufs=2, align_bytes=64)
-                nc.scalar.copy(out=dz1_tok[k // GTILES][:, k % GTILES, :], in_=acc[k][:])
+                if hi == PASSES:
+                    if k % GTILES == 0:
+                        dz1_tok[k // GTILES] = work.tile([P, GTILES, DL], BF16, name="dz1_tok", tag="dz1t", bufs=2, align_bytes=64)
+                    nc.scalar.copy(
+                        out=dz1_tok[k // GTILES][:, k % GTILES, :].rearrange("p (u m e) -> p u m e", u=2, e=2),
+                        in_=acc[k][:].rearrange("p (u e m) -> p u m e", u=2, e=2),
+                    )
 
             dz1f_grp = {}
 
@@ -274,15 +302,21 @@ def tile_multilatentattention_pb_v_kernel(tc, x, wd, wu, rope_cos, rope_sin, g, 
                 nc.vector.quantize_mx(out=codes[:].bitcast(E5M2), scales=scales[:], in_=dz1f_grp[k][:])
                 dz1f[k] = (codes, scales)
 
-            res0 = {}
+            results = []
 
-            def out0_part(k, n, engine):
+            def new_result():
+                slot = len(results) % 10
+                t = arena.tile([P, 2, 512], F32, name=f"res{len(results)}", offset=4 * KIB * slot, align_bytes=64)
+                results.append(t)
+                return t
+
+            acc0 = {}
+
+            def out0_pass(k, n):
                 codes, scales = dz1f[k]
-                if n == 0:
-                    res0[k] = work.tile([P, D], F32, name="res0", tag="res0", bufs=2, align_bytes=64)
-                bank = new_bank()
+                acc0[k, n] = new_bank()
                 nc.tensor.matmul_mx(
-                    out=bank[:],
+                    out=acc0[k, n][:],
                     lhsT=codes[:].bitcast(E5M2),
                     lhsT_scale=scales[:],
                     rhs=wd_codes[:, 512 * n : 512 * n + 512].bitcast(E4M3),
@@ -290,21 +324,38 @@ def tile_multilatentattention_pb_v_kernel(tc, x, wd, wu, rope_cos, rope_sin, g, 
                     start=True,
                     stop=True,
                 )
-                copy_out(engine, res0[k][:, 512 * n : 512 * n + 512], bank[:])
-                if n % 2 == 1:
-                    lo = 1024 * (n // 2)
-                    nc.sync.dma_start(out=out0_view[k // GTILES][:, k % GTILES, lo : lo + 1024], in_=res0[k][:, lo : lo + 1024])
+
+            res0 = {}
+
+            def out0_copy(k, n, engine="s"):
+                half, i = n // 2, n % 2
+                if i == 0:
+                    res0[k, half] = new_result()
+                res = res0[k, half]
+                copy_out(engine, res[:, i, :], acc0[k, n][:])
+                if i == 1:
+                    nc.sync.dma_start(
+                        out=out0_view[k // GTILES][:, k % GTILES, 1024 * half : 1024 * half + 1024],
+                        in_=res[:].rearrange("p i c -> p (i c)"),
+                    )
+
+            def out0_half(k, half, engines="ss"):
+                for i in range(2):
+                    out0_pass(k, 2 * half + i)
+                    out0_copy(k, 2 * half + i, engines[i])
+
+            def out0(k):
+                out0_half(k, 0)
+                out0_half(k, 1)
 
             dz1 = {}
             dz1_grp = {}
 
-            def dz1_interleave(b, engine, lo, hi):
-                if lo == 0:
-                    dz1_grp[b] = work.tile([P, DL, 4], BF16, name="dz1_grp", tag="xgrp", bufs=3, align_bytes=64)
-                copy_out(
-                    engine,
-                    dz1_grp[b][:, lo:hi, :].rearrange("p (g l) t -> p g t l", l=4),
-                    dz1_tok[b][:, :, lo:hi].rearrange("p t (g l) -> p g t l", l=4),
+            def dz1_interleave(b):
+                dz1_grp[b] = work.tile([P, DL, 4], BF16, name="dz1_grp", tag="xgrp", bufs=3, align_bytes=64)
+                nc.vector.tensor_copy(
+                    out=dz1_grp[b][:].rearrange("p (g l) t -> p g t l", l=4),
+                    in_=dz1_tok[b][:].rearrange("p t (g l) -> p g t l", l=4),
                 )
 
             def dz1_quant(b):
@@ -317,14 +368,16 @@ def tile_multilatentattention_pb_v_kernel(tc, x, wd, wu, rope_cos, rope_sin, g, 
 
             x_grp = {}
 
-            def x_interleave(n, b):
-                grouped = work.tile([P, 512, 4], BF16, name="x_grp", tag="xgrp", bufs=3, align_bytes=64)
-                for i in range(2):
+            def x_interleave(n, b, parts=(0, 1)):
+                if 0 in parts:
+                    x_grp[n, b] = work.tile([P, 512, 4], BF16, name="x_grp", tag="xgrp", bufs=3, align_bytes=64)
+                grouped = x_grp[n, b]
+                lo = 512 * n
+                for i in parts:
                     nc.vector.tensor_copy(
                         out=grouped[:, 256 * i : 256 * i + 256, :].rearrange("p (g l) t -> p g t l", l=4),
-                        in_=x_raw[b][:, :, 512 * n + i : 512 * n + 512 : 2].rearrange("p t (g l) -> p g t l", l=4),
+                        in_=x_raw[b][:, :, lo + i : lo + 512 : 2].rearrange("p t (g l) -> p g t l", l=4),
                     )
-                x_grp[n, b] = grouped
 
             def x_quant(n, b):
                 nc.vector.quantize_mx(
@@ -333,17 +386,15 @@ def tile_multilatentattention_pb_v_kernel(tc, x, wd, wu, rope_cos, rope_sin, g, 
                     in_=x_grp[n, b][:].rearrange("p c t -> p (c t)"),
                 )
 
-            res1 = {}
             acc1 = {}
 
-            def out1_pass(j, b):
-                n, h, i = j // 4, j // 2 % 2, j % 2
+            def out1_pass(n, h, i, b):
                 a = 4 * n + 2 * i + h
-                codes, scales = dz1[b]
                 if b == 0:
-                    acc1[j] = new_bank()
+                    acc1[a] = new_bank()
+                codes, scales = dz1[b]
                 nc.tensor.matmul_mx(
-                    out=acc1[j][:],
+                    out=acc1[a][:],
                     lhsT=x_codes[:, b, P * a : P * a + P].bitcast(E4M3),
                     lhsT_scale=x_scales[:, b, P * a : P * a + P],
                     rhs=codes[:].bitcast(E5M2),
@@ -352,112 +403,188 @@ def tile_multilatentattention_pb_v_kernel(tc, x, wd, wu, rope_cos, rope_sin, g, 
                     stop=(b == B - 1),
                 )
 
-            def out1_copy(j, engine):
-                n, h, i = j // 4, j // 2 % 2, j % 2
-                if i == 0:
-                    res1[j // 2] = work.tile([P, 2, DL], F32, name="res1", tag="res1", bufs=4, align_bytes=64)
-                copy_out(
-                    engine,
-                    res1[j // 2][:, i, :].rearrange("p (m u e) -> p m u e", u=2, e=2),
-                    acc1[j][:].rearrange("p (u m e) -> p m u e", u=2, e=2),
-                )
-                if i == 1:
-                    nc.sync.dma_start(out=out1_view[:, n, h], in_=res1[j // 2][:])
+            def out1_pair(n, h, engines="ss"):
+                res = new_result()
+                for i in range(2):
+                    a = 4 * n + 2 * i + h
+                    if a not in acc1:
+                        out1_pass(n, h, i, 0)
+                    out1_pass(n, h, i, 1)
+                    bank = acc1[a]
+                    copy_out(
+                        engines[i],
+                        res[:, i, :].rearrange("p (m u e) -> p m u e", u=2, e=2),
+                        bank[:].rearrange("p (u m e) -> p m u e", u=2, e=2),
+                    )
+                nc.sync.dma_start(out=out1_view[:, n, h], in_=res[:])
 
-            def rope(k):
-                rope_add(rope_mul([g_raw[k]], k), k)
+            load_g(0, 2)
+            load_wu(0, 0, 2)
+            load_tables(0, 1)
+            issue_g(0, 0)
+            issue_g(0, 1)
+            load_wu(0, 2, 6)
+            load_wu(1)
+            load_wu(2)
+            load_wu(3)
+            load_tables(1, 4)
+            issue_g(1)
+            load_wd(0)
+            load_wd(1)
+            issue_g(2)
+            load_wd(2)
+            load_wd(3)
+            for k in range(3, TILES):
+                issue_g(k)
+            load_x(0)
+            load_x(1)
 
-            def dz2_step(k, cs, warm=0):
-                for c in cs:
-                    dz2_copy(k, c, dz2_bank(k, c, warm if c == cs[0] else 0))
-
-            xs = [(n, b) for n in range(4) for b in range(B)]
-            pend = []
-
-            def x_step():
-                xu = xs.pop(0)
-                x_interleave(*xu)
-                if pend:
-                    x_quant(*pend.pop())
-                pend.append(xu)
-
-            w00 = [wu_bank(0, s, 10 if s == 0 else 0) for s in range(3)]
-            rope_add(rope_mul(g0_parts[:1], 0), 0)
-            w10 = []
-            for s in range(3):
-                wu_quant(w00[s])
-                w10.append(wu_bank(1, s, 4 if s == 0 else 0))
-            dz2_step(0, (0,), 2)
-            rope_add(rope_mul(g0_parts[1:], 0), 0)
-            for item in w10:
-                wu_quant(item)
-            dz2_step(0, (1, 2))
-            rope(1)
-            w01 = [wu_bank(0, s, 2 if s == 3 else 0) for s in range(3, 6)]
-            dz2_quant(0, grp[0])
-            w11 = []
-            for s in range(3):
-                wu_quant(w01[s])
-                w11.append(wu_bank(1, 3 + s, 2 if s == 0 else 0))
-            for item in w11:
-                wu_quant(item)
-            ropes_at = {0: (2,), 1: (3, 4), 2: (5,), 3: (6,), 4: (7,)}
-            left = None
-            for k in range(TILES):
-                if k + 1 < TILES:
-                    dz2_step(k + 1, (0, 1), 2 if k == 0 else 0)
-                if k >= 2:
-                    for n in range(4):
-                        out0_part(k - 2, n, "v" if n == 3 and k in (5, 7) else "s")
-                if k + 1 < TILES:
-                    bank = dz2_bank(k + 1, 2)
-                if k >= 1:
-                    dz1_transpose(k - 1)
-                if k + 1 < TILES:
-                    dz2_copy(k + 1, 2, bank)
-                for j in ropes_at.get(k, ())[:1]:
-                    rope(j)
-                if k == 6:
-                    x_step()
-                    x_step()
-                if k >= 1:
+            wu_bank(0, 0)
+            rope_mul(0, 0)
+            wu_quant(0, (0,))
+            rope_add(0, 0)
+            rope_mul(0, 1)
+            wu_bank(0, 1)
+            wu_bank(0, 2)
+            dz2_bank(0, 0)
+            wu_quant(0, (1,))
+            rope_add(0, 1)
+            wu_quant(0, (2,))
+            dz2_quant(0, 0, 2)
+            for r in range(1, 4):
+                wu_row(r)
+                wu_quant(r)
+            dz2_bank(0, 1)
+            dz2_bank(0, 2)
+            sort_content(1, "s")
+            rope_cos(1, 0)
+            dz2_quant(0, 2, 4)
+            rope_sin(1, 0)
+            dz2_quant(0, 4, 6)
+            rope_mul(1, 1)
+            rope_add(1, 0)
+            rope_add(1, 1)
+            stage1(0, 0, 3)
+            wd_bank(0)
+            wd_bank(1)
+            stage1(0, 3, 6)
+            sort_content(2, "s")
+            for c in range(3):
+                dz2_bank(1, c)
+            wd_bank(2)
+            wd_bank(3)
+            dz1_transpose(0)
+            rope_mul(2, 0)
+            wd_quant(0)
+            rope_cos(2, 1)
+            dz2_quant(1, 0, 4)
+            rope_sin(2, 1)
+            dz2_quant(1, 4, 6)
+            rope_add(2, 0)
+            rope_add(2, 1)
+            wd_quant(1)
+            dz1f_quant(0)
+            stage1(1, 0, 3)
+            wd_bank(4)
+            wd_bank(5)
+            sort_content(3, "s")
+            stage1(1, 3, 6)
+            rope_mul(3, 0)
+            wd_quant(2)
+            rope_mul(3, 1)
+            dz2_bank(2, 0)
+            dz2_bank(2, 1)
+            out0_half(0, 0)
+            dz2_bank(2, 2)
+            wd_bank(6)
+            dz1_transpose(1)
+            rope_add(3, 0)
+            dz2_quant(2, 0, 4)
+            rope_add(3, 1)
+            rope_cos(4, 0)
+            dz2_quant(2, 4, 6)
+            dz1f_quant(1)
+            stage1(2, 0, 3)
+            wd_bank(7)
+            dz2_bank(3, 0)
+            stage1(2, 3, 6)
+            rope_sin(4, 0)
+            rope_cos(4, 1)
+            wd_quant(3)
+            rope_sin(4, 1)
+            rope_add(4, 0)
+            rope_add(4, 1)
+            dz2_bank(3, 1)
+            dz2_bank(3, 2)
+            out0_half(0, 1)
+            rope_mul(5, 0)
+            dz2_quant(3, 0, 4)
+            dz2_quant(3, 4, 6)
+            rope_mul(5, 1)
+            rope_add(5, 0)
+            rope_add(5, 1)
+            for k in range(3, TILES):
+                nxt = k + 1 < TILES
+                if nxt:
+                    dz2_bank(k + 1, 0)
+                    dz2_bank(k + 1, 1)
+                for n in range(4):
+                    out0_pass(k - 2, n)
+                out0_copy(k - 2, 0)
+                out0_copy(k - 2, 1)
+                dz1_transpose(k - 1)
+                out0_copy(k - 2, 2)
+                out0_copy(k - 2, 3)
+                if nxt:
+                    dz2_bank(k + 1, 2)
+                stage1(k)
+                if k + 3 < TILES:
+                    dz2_quant(k + 1, 0, 4)
                     dz1f_quant(k - 1)
-                for j in ropes_at.get(k, ())[1:]:
-                    rope(j)
-                if k >= 1:
-                    stage1(k)
-                    stage1_copy(k)
-                if k < 2:
-                    for n in range(4 * k, 4 * k + 4):
-                        wd_bank(n, (2, 0, 1, 0, 0, 0, 2, 0)[n])
-                    wd_quant(2 * k)
-                if k == 0:
-                    stage1(k)
-                    stage1_copy(k)
-                if k + 1 < TILES:
-                    dz2_quant(k + 1, grp[k + 1])
-                if k < 2:
-                    wd_quant(2 * k + 1)
-                if k == 4:
-                    dz1_interleave(0, "v", 0, DL)
-                if k in (4, 6):
-                    x_step()
-                if k == 4:
+                    rope_mul(k + 3, 0)
+                    rope_mul(k + 3, 1)
+                    dz2_quant(k + 1, 4, 6)
+                    rope_add(k + 3, 0)
+                    rope_add(k + 3, 1)
+                if k == 5:
+                    dz1_interleave(0)
+                    dz2_quant(6, 0, 4)
+                    dz1f_quant(4)
                     dz1_quant(0)
+                    x_interleave(0, 0)
+                    dz2_quant(6, 4, 6)
+                    x_quant(0, 0)
+                    x_interleave(0, 1)
+                if k == 6:
+                    dz2_quant(7, 0, 4)
+                    dz1f_quant(5)
+                    x_quant(0, 1)
+                    x_interleave(1, 0)
+                    dz2_quant(7, 4, 6)
+                    x_quant(1, 0)
+                    x_interleave(1, 1, (0,))
+                if k == 7:
+                    dz1f_quant(6)
+                    x_interleave(1, 1, (1,))
+                    x_quant(1, 1)
             for n in range(4):
-                out0_part(6, n, "s")
-                if n == 1:
-                    dz1_transpose(7)
-            dz1_interleave(1, "v", 0, DL)
+                out0_pass(6, n)
+            out0_copy(6, 0, "v")
+            out0_copy(6, 1)
+            dz1_interleave(1)
+            dz1_transpose(7)
+            out0_copy(6, 2)
+            out0_copy(6, 3)
             dz1f_quant(7)
             dz1_quant(1)
+            for i in range(2):
+                out1_pass(0, 0, i, 0)
+            out0(7)
+            for n in (2, 3):
+                x_interleave(n, 0)
+                x_interleave(n, 1)
+                x_quant(n, 0)
+                x_quant(n, 1)
             for n in range(4):
-                out0_part(7, n, "s")
-            for j in range(16):
-                while len(xs) > 0 and xs[0][0] <= (j + 4) // 4:
-                    x_step()
-                if len(pend) > 0 and (pend[0][0] <= j // 4 or len(xs) == 0):
-                    x_quant(*pend.pop())
-                out1_pass(j, 0)
-                out1_pass(j, 1)
-                out1_copy(j, "v" if j in (11, 12, 14) else "s")
+                out1_pair(n, 0)
+                out1_pair(n, 1)

@@ -24,7 +24,8 @@ TILES = T // P
 GTILES = S // P
 HF = DH + DR
 KIB = 1024
-SORTED = ()
+FIRST_SHARED = 2
+OWN_HEADS = 4
 
 
 def tile_multilatentattention_pb_v_kernel(tc, x, wd, wu, rope_cos, rope_sin, g, out_0, out_1):
@@ -43,7 +44,8 @@ def tile_multilatentattention_pb_v_kernel(tc, x, wd, wu, rope_cos, rope_sin, g, 
         keep = ctx.enter_context(tc.tile_pool(name="keep", bufs=1))
         arena = ctx.enter_context(tc.tile_pool(name="arena", bufs=1))
         work = ctx.enter_context(tc.tile_pool(name="work", bufs=2))
-        psum = ctx.enter_context(tc.psum_pool(name="psum", bufs=8))
+        psum = ctx.enter_context(tc.psum_pool(name="psum", bufs=7))
+        psum_keep = ctx.enter_context(tc.psum_pool(name="psum_keep", bufs=1))
 
         ident = keep.tile([P, P], F32, name="ident", align_bytes=64)
         make_identity(nc, ident[:])
@@ -51,8 +53,10 @@ def tile_multilatentattention_pb_v_kernel(tc, x, wd, wu, rope_cos, rope_sin, g, 
         nc.vector.memset(warm[:], 0.0)
         warm2 = keep.tile([P, 16], F32, name="warm2", align_bytes=64)
 
-        cos_t = keep.tile([P, 4, DR], F32, name="cos_t", align_bytes=64)
+        tables = keep.tile([P, 4, 2, DR], F32, name="tables", align_bytes=64)
         sin_t = keep.tile([P, 4, DR], F32, name="sin_t", align_bytes=64)
+        tables_t = keep.tile([P, 4, P], F32, name="tables_t", align_bytes=64)
+        tables_psum = psum_keep.tile([P, 4, 2, DR], F32, name="tables_psum")
         wu_codes = keep.tile([P, PASSES, DL], U32, name="wu_codes", align_bytes=64)
         wu_scales = keep.tile([P, PASSES, DL], U8, name="wu_scales", align_bytes=64)
         wd_codes = keep.tile([P, D], U32, name="wd_codes", align_bytes=64)
@@ -66,13 +70,13 @@ def tile_multilatentattention_pb_v_kernel(tc, x, wd, wu, rope_cos, rope_sin, g, 
             wu_raw, g_raw, wd_raw, x_raw = {}, {}, {}, {}
 
             def load_tables(lo, hi):
-                nc.sync.dma_start(out=cos_t[:, lo:hi, :], in_=cos_view[:, lo:hi, :])
+                nc.sync.dma_start(out=tables[:, lo:hi, 0, :], in_=cos_view[:, lo:hi, :])
                 nc.sync.dma_start(out=sin_t[:, lo:hi, :], in_=sin_view[:, lo:hi, :])
 
             def load_g(k, parts=1):
                 heads = H // parts
                 if parts == 1:
-                    g_raw[k] = [work.tile([P, H, HF], BF16, name=f"g{k}", tag="g", bufs=5, align_bytes=64)]
+                    g_raw[k] = [work.tile([P, H, HF], BF16, name=f"g{k}", tag="g", bufs=6, align_bytes=64)]
                 else:
                     g_raw[k] = [keep.tile([P, heads, HF], BF16, name=f"g{k}_{i}", align_bytes=64) for i in range(parts)]
 
@@ -95,7 +99,7 @@ def tile_multilatentattention_pb_v_kernel(tc, x, wd, wu, rope_cos, rope_sin, g, 
                 wd_raw[c] = t
 
             def load_x(b):
-                t = keep.tile([P, 4, D], BF16, name=f"x{b}", align_bytes=64)
+                t = arena.tile([P, 4, D], BF16, name=f"x{b}", offset=KIB * (40 + 16 * b), align_bytes=64)
                 nc.sync.dma_start(out=t[:], in_=x_view[b])
                 x_raw[b] = t
 
@@ -115,85 +119,84 @@ def tile_multilatentattention_pb_v_kernel(tc, x, wd, wu, rope_cos, rope_sin, g, 
                         q = 2 * i + w
                         nc.tensor.transpose(bank[:, q * P : (q + 1) * P], words[:, w:256:2], ident[:])
 
+            def tables_sin(lo, hi):
+                nc.scalar.copy(out=tables[:, lo:hi, 1, 0:32], in_=sin_t[:, lo:hi, 32:64])
+                nc.scalar.mul(out=tables[:, lo:hi, 1, 32:64], in_=sin_t[:, lo:hi, 0:32], mul=-1.0)
+
+            def tables_turn():
+                bank = new_bank()
+                for j in range(4):
+                    nc.tensor.transpose(bank[:, j * P : (j + 1) * P], tables[:, j].rearrange("p a r -> p (a r)"), ident[:])
+                nc.scalar.copy(out=tables_t[:].rearrange("p j c -> p (j c)"), in_=bank[:])
+
+            def tables_back():
+                for j in range(4):
+                    nc.tensor.transpose(tables_psum[:, j].rearrange("p a r -> p (a r)"), tables_t[:, j, :], ident[:])
+
+            def rope_part(k, lo, hi):
+                parts = g_raw[k]
+                per = H // len(parts)
+                return parts[lo // per][:, lo % per : lo % per + hi - lo, DH:HF]
+
             prods = {}
 
-            def rope_cos(k, half):
-                parts = g_raw[k]
-                gr = parts[half][:, :, DH:HF] if len(parts) == 2 else parts[0][:, 8 * half : 8 * half + 8, DH:HF]
-                pc = work.tile([P, 8, DR], F32, name="pc", tag="pc", bufs=2, align_bytes=64)
-                ps = work.tile([P, 8, DR], F32, name="ps", tag="ps", bufs=2, align_bytes=64)
-                prods[k, half] = (gr, pc, ps)
-                nc.vector.tensor_tensor(out=pc[:], in0=gr, in1=cos_t[:, k % 4, :].unsqueeze(1).to_broadcast([P, 8, DR]), op=MULT)
+            def rope_cos(k, lo, hi, table):
+                if lo == 0:
+                    pc = work.tile([P, H, DR], F32, name="pc", tag="pc", bufs=2, align_bytes=64)
+                    ps = work.tile([P, H, DR], F32, name="ps", tag="ps", bufs=2, align_bytes=64)
+                    prods[k] = (pc, ps)
+                row = table[:, k % 4, 0, :].unsqueeze(1).to_broadcast([P, hi - lo, DR])
+                nc.vector.tensor_tensor(out=prods[k][0][:, lo:hi, :], in0=rope_part(k, lo, hi), in1=row, op=MULT)
 
-            def rope_sin(k, half):
-                gr, pc, ps = prods[k, half]
-                nc.vector.tensor_tensor(out=ps[:], in0=gr, in1=sin_t[:, k % 4, :].unsqueeze(1).to_broadcast([P, 8, DR]), op=MULT)
+            def rope_sin(k, lo, hi, table):
+                row = table[:, k % 4, 1, :].rearrange("p (a j) -> p a j", a=2).unsqueeze(1).to_broadcast([P, hi - lo, 2, 32])
+                nc.vector.tensor_tensor(
+                    out=prods[k][1][:, lo:hi, :].rearrange("p h (a j) -> p h a j", a=2),
+                    in0=rope_part(k, lo, hi).rearrange("p h (a j) -> p h a j", a=2)[:, :, ::-1, :],
+                    in1=row,
+                    op=MULT,
+                )
 
-            def rope_mul(k, half):
-                rope_cos(k, half)
-                rope_sin(k, half)
+            def rope_add(engine, k, lo, hi):
+                pc, ps = prods[k]
+                engine.tensor_tensor(out=rope_part(k, lo, hi), in0=pc[:, lo:hi, :], in1=ps[:, lo:hi, :], op=ADD)
 
-            sorted_words = {}
+            def rope_window(k):
+                if k - 1 >= FIRST_SHARED:
+                    rope_sin(k - 1, H - 1, H, tables_psum)
+                    rope_add(nc.gpsimd, k - 1, OWN_HEADS, H)
+                if k < TILES:
+                    rope_cos(k, 0, H, tables_psum)
+                    rope_sin(k, 0, H - 1, tables_psum)
 
-            def sort_content(k, engine="v"):
-                if k not in SORTED:
-                    return
-                t = work.tile([P, 2, H, HF // 4], F32, name="sorted", tag="sorted", bufs=2, align_bytes=64)
-                sorted_words[k] = t
-                words = g_raw[k][0][:].bitcast(F32)
-                copy_out(engine, t[:, :, :, : DH // 4], words[:, :, : DH // 2].rearrange("p h (m u) -> p u h m", u=2))
-
-            def rope_add(k, half):
-                gr, pc, ps = prods[k, half]
-                if k not in SORTED:
-                    nc.vector.tensor_tensor(out=gr[:, :, 0:32], in0=pc[:, :, 0:32], in1=ps[:, :, 32:64], op=ADD)
-                    nc.vector.tensor_tensor(out=gr[:, :, 32:64], in0=pc[:, :, 32:64], in1=ps[:, :, 0:32], op=SUB)
-                    return
-                dst = sorted_words[k][:].bitcast(BF16)
-                pc4 = pc[:].rearrange("p h (a m u e) -> p h a m u e", a=2, u=2, e=2)
-                ps4 = ps[:].rearrange("p h (a m u e) -> p h a m u e", a=2, u=2, e=2)
-                for u in range(2):
-                    for a, op in ((0, ADD), (1, SUB)):
-                        lo = DH // 2 + 16 * a
-                        nc.vector.tensor_tensor(
-                            out=dst[:, u, 8 * half : 8 * half + 8, lo : lo + 16].rearrange("p h (m e) -> p h m e", e=2),
-                            in0=pc4[:, :, a, :, u, :],
-                            in1=ps4[:, :, 1 - a, :, u, :],
-                            op=op,
-                        )
-
-            def rope(k):
-                rope_mul(k, 0)
-                rope_mul(k, 1)
-                if k in SORTED:
-                    sort_content(k)
-                rope_add(k, 0)
-                rope_add(k, 1)
+            def rope_own(k):
+                rope_add(nc.vector, k, 0, OWN_HEADS)
 
             wu_grp = {}
 
             def wu_bank(r, c):
-                grouped = work.tile([P, 2, 512], BF16, name="wu_grp", tag="wug", bufs=4, align_bytes=64)
+                if r % 2 == 0:
+                    wu_grp[r // 2, c] = arena.tile([P, 2, 2, 512], BF16, name=f"wu_grp{r}_{c}", offset=KIB * (40 + 4 * (3 * (r // 2) + c)), align_bytes=64)
+                grouped = wu_grp[r // 2, c]
                 bank = new_bank()
                 transpose_pairs(bank, [wu_raw[r, 2 * c + i] for i in range(2)])
                 nc.scalar.copy(
-                    out=grouped[:].rearrange("p i c -> p (i c)").bitcast(F32).rearrange("p (i m w) -> p i m w", i=2, w=2),
+                    out=grouped[:, :, r % 2, :].bitcast(F32).rearrange("p i (m w) -> p i m w", w=2),
                     in_=bank[:].rearrange("p (i w m) -> p i m w", i=2, w=2),
                 )
-                wu_grp[r, c] = grouped
 
             def wu_row(r):
                 for c in range(3):
                     wu_bank(r, c)
 
-            def wu_quant(r, cs=(0, 1, 2)):
+            def wu_quant(u, cs=(0, 1, 2)):
                 for c in cs:
                     for i in range(2):
                         s = 2 * c + i
                         nc.vector.quantize_mx(
-                            out=wu_codes[:, s, P * r : P * r + P].bitcast(E4M3),
-                            scales=wu_scales[:, s, P * r : P * r + P],
-                            in_=wu_grp[r, c][:, i, :],
+                            out=wu_codes[:, s, 256 * u : 256 * u + 256].bitcast(E4M3),
+                            scales=wu_scales[:, s, 256 * u : 256 * u + 256],
+                            in_=wu_grp[u, c][:, i].rearrange("p r c -> p (r c)"),
                         )
 
             wd_grp = {}
@@ -228,14 +231,7 @@ def tile_multilatentattention_pb_v_kernel(tc, x, wd, wu, rope_cos, rope_sin, g, 
                 if c == 0:
                     dz2_grp[k] = work.tile([P, J], BF16, name="dz2_grp", tag="dz2g", bufs=2, align_bytes=64)
                 bank = new_bank()
-                if k in SORTED:
-                    flat = sorted_words[k][:].rearrange("p u h m -> p u (h m)")
-                    for i in range(2):
-                        for w in range(2):
-                            q, s = 2 * i + w, 2 * c + i
-                            nc.tensor.transpose(bank[:, q * P : (q + 1) * P], flat[:, w, P * s : P * s + P], ident[:])
-                else:
-                    transpose_pairs(bank, [g_pass(k, 2 * c + i) for i in range(2)])
+                transpose_pairs(bank, [g_pass(k, 2 * c + i) for i in range(2)])
                 nc.scalar.copy(
                     out=dz2_grp[k][:, 1024 * c : 1024 * c + 1024].bitcast(F32).rearrange("p (i r w) -> p i r w", i=2, w=2),
                     in_=bank[:].rearrange("p (i w r) -> p i r w", i=2, w=2),
@@ -368,16 +364,13 @@ def tile_multilatentattention_pb_v_kernel(tc, x, wd, wu, rope_cos, rope_sin, g, 
 
             x_grp = {}
 
-            def x_interleave(n, b, parts=(0, 1)):
-                if 0 in parts:
-                    x_grp[n, b] = work.tile([P, 512, 4], BF16, name="x_grp", tag="xgrp", bufs=3, align_bytes=64)
-                grouped = x_grp[n, b]
-                lo = 512 * n
-                for i in parts:
-                    nc.vector.tensor_copy(
-                        out=grouped[:, 256 * i : 256 * i + 256, :].rearrange("p (g l) t -> p g t l", l=4),
-                        in_=x_raw[b][:, :, lo + i : lo + 512 : 2].rearrange("p t (g l) -> p g t l", l=4),
-                    )
+            def x_interleave(n, b):
+                grouped = work.tile([P, 512, 4], BF16, name="x_grp", tag="xgrp", bufs=3, align_bytes=64)
+                x_grp[n, b] = grouped
+                nc.vector.tensor_copy(
+                    out=grouped[:].rearrange("p (i g l) t -> p g t l i", i=2, l=4),
+                    in_=x_raw[b][:, :, 512 * n : 512 * n + 512].rearrange("p t (g l i) -> p g t l i", i=2, l=4),
+                )
 
             def x_quant(n, b):
                 nc.vector.quantize_mx(
@@ -424,149 +417,145 @@ def tile_multilatentattention_pb_v_kernel(tc, x, wd, wu, rope_cos, rope_sin, g, 
             issue_g(0, 0)
             issue_g(0, 1)
             load_wu(0, 2, 6)
+            load_tables(1, 4)
+            issue_g(1)
             load_wu(1)
             load_wu(2)
             load_wu(3)
-            load_tables(1, 4)
-            issue_g(1)
-            load_wd(0)
-            load_wd(1)
             issue_g(2)
+            load_wd(0)
+            issue_g(3)
+            load_wd(1)
             load_wd(2)
+            issue_g(4)
             load_wd(3)
-            for k in range(3, TILES):
+            for k in range(5, TILES):
                 issue_g(k)
-            load_x(0)
-            load_x(1)
 
+            tables_sin(0, 1)
             wu_bank(0, 0)
-            rope_mul(0, 0)
-            wu_quant(0, (0,))
-            rope_add(0, 0)
-            rope_mul(0, 1)
+            rope_cos(0, 0, 8, tables)
+            rope_sin(0, 0, 8, tables)
+            rope_cos(0, 8, H, tables)
+            rope_add(nc.vector, 0, 0, 8)
+            rope_sin(0, 8, H, tables)
+            tables_sin(1, 4)
             wu_bank(0, 1)
             wu_bank(0, 2)
+            tables_turn()
             dz2_bank(0, 0)
-            wu_quant(0, (1,))
-            rope_add(0, 1)
-            wu_quant(0, (2,))
-            dz2_quant(0, 0, 2)
-            for r in range(1, 4):
-                wu_row(r)
-                wu_quant(r)
+            rope_add(nc.vector, 0, 8, H)
             dz2_bank(0, 1)
+            tables_back()
             dz2_bank(0, 2)
-            sort_content(1, "s")
-            rope_cos(1, 0)
-            dz2_quant(0, 2, 4)
-            rope_sin(1, 0)
+            rope_cos(1, 0, H, tables)
+            rope_sin(1, 0, H, tables)
+            dz2_quant(0, 0, 4)
+            rope_add(nc.vector, 1, 0, H)
             dz2_quant(0, 4, 6)
-            rope_mul(1, 1)
-            rope_add(1, 0)
-            rope_add(1, 1)
+            wu_row(1)
+            wu_quant(0)
+            wu_row(2)
+            wu_row(3)
+            wu_quant(1)
+            load_x(0)
+            load_x(1)
+            for c in range(3):
+                dz2_bank(1, c)
+            rope_window(2)
+            dz2_quant(1, 0, 4)
+            rope_own(2)
+            dz2_quant(1, 4, 6)
             stage1(0, 0, 3)
             wd_bank(0)
             wd_bank(1)
             stage1(0, 3, 6)
-            sort_content(2, "s")
-            for c in range(3):
-                dz2_bank(1, c)
+            rope_window(3)
+            wd_quant(0)
+            rope_own(3)
             wd_bank(2)
             wd_bank(3)
             dz1_transpose(0)
-            rope_mul(2, 0)
-            wd_quant(0)
-            rope_cos(2, 1)
-            dz2_quant(1, 0, 4)
-            rope_sin(2, 1)
-            dz2_quant(1, 4, 6)
-            rope_add(2, 0)
-            rope_add(2, 1)
-            wd_quant(1)
-            dz1f_quant(0)
             stage1(1, 0, 3)
-            wd_bank(4)
-            wd_bank(5)
-            sort_content(3, "s")
-            stage1(1, 3, 6)
-            rope_mul(3, 0)
-            wd_quant(2)
-            rope_mul(3, 1)
             dz2_bank(2, 0)
             dz2_bank(2, 1)
-            out0_half(0, 0)
-            dz2_bank(2, 2)
-            wd_bank(6)
-            dz1_transpose(1)
-            rope_add(3, 0)
+            stage1(1, 3, 6)
+            wd_quant(1)
+            dz1f_quant(0)
+            rope_window(4)
             dz2_quant(2, 0, 4)
-            rope_add(3, 1)
-            rope_cos(4, 0)
+            rope_own(4)
+            dz2_bank(2, 2)
+            wd_bank(4)
+            dz1_transpose(1)
+            out0_half(0, 0)
+            wd_bank(5)
+            dz2_bank(3, 0)
+            stage1(2, 0, 3)
             dz2_quant(2, 4, 6)
             dz1f_quant(1)
-            stage1(2, 0, 3)
+            rope_window(5)
+            wd_quant(2)
+            wd_bank(6)
             wd_bank(7)
-            dz2_bank(3, 0)
             stage1(2, 3, 6)
-            rope_sin(4, 0)
-            rope_cos(4, 1)
-            wd_quant(3)
-            rope_sin(4, 1)
-            rope_add(4, 0)
-            rope_add(4, 1)
             dz2_bank(3, 1)
             dz2_bank(3, 2)
+            wd_quant(3)
+            rope_own(5)
             out0_half(0, 1)
-            rope_mul(5, 0)
             dz2_quant(3, 0, 4)
             dz2_quant(3, 4, 6)
-            rope_mul(5, 1)
-            rope_add(5, 0)
-            rope_add(5, 1)
+            x_units = [(n, b) for n in range(4) for b in range(B)]
             for k in range(3, TILES):
                 nxt = k + 1 < TILES
+                if k + 3 < TILES:
+                    rope_window(k + 3)
                 if nxt:
                     dz2_bank(k + 1, 0)
                     dz2_bank(k + 1, 1)
                 for n in range(4):
                     out0_pass(k - 2, n)
-                out0_copy(k - 2, 0)
-                out0_copy(k - 2, 1)
+                if k == 5:
+                    rope_window(TILES)
+                eng = "v" if k == 5 else "s"
+                out0_copy(k - 2, 0, eng)
+                out0_copy(k - 2, 1, eng)
                 dz1_transpose(k - 1)
-                out0_copy(k - 2, 2)
+                out0_copy(k - 2, 2, eng)
                 out0_copy(k - 2, 3)
                 if nxt:
                     dz2_bank(k + 1, 2)
                 stage1(k)
-                if k + 3 < TILES:
+                if nxt:
                     dz2_quant(k + 1, 0, 4)
+                if k + 3 < TILES:
+                    rope_own(k + 3)
+                if k == 3:
                     dz1f_quant(k - 1)
-                    rope_mul(k + 3, 0)
-                    rope_mul(k + 3, 1)
-                    dz2_quant(k + 1, 4, 6)
-                    rope_add(k + 3, 0)
-                    rope_add(k + 3, 1)
-                if k == 5:
-                    dz1_interleave(0)
-                    dz2_quant(6, 0, 4)
-                    dz1f_quant(4)
-                    dz1_quant(0)
                     x_interleave(0, 0)
-                    dz2_quant(6, 4, 6)
+                    dz2_quant(k + 1, 4, 6)
                     x_quant(0, 0)
+                if k == 4:
+                    dz1f_quant(k - 1)
+                    dz1_interleave(0)
+                    dz2_quant(k + 1, 4, 6)
+                    dz1_quant(0)
                     x_interleave(0, 1)
-                if k == 6:
-                    dz2_quant(7, 0, 4)
-                    dz1f_quant(5)
+                if k == 5:
+                    dz1f_quant(k - 1)
                     x_quant(0, 1)
+                    dz2_quant(k + 1, 4, 6)
                     x_interleave(1, 0)
-                    dz2_quant(7, 4, 6)
+                if k == 6:
                     x_quant(1, 0)
-                    x_interleave(1, 1, (0,))
-                if k == 7:
-                    dz1f_quant(6)
-                    x_interleave(1, 1, (1,))
+                    dz1f_quant(k - 1)
+                    x_interleave(1, 1)
+                    dz2_quant(k + 1, 4, 6)
                     x_quant(1, 1)
+                if k == 7:
+                    dz1f_quant(k - 1)
+                    x_interleave(2, 0)
             for n in range(4):
                 out0_pass(6, n)
             out0_copy(6, 0, "v")
@@ -580,11 +569,13 @@ def tile_multilatentattention_pb_v_kernel(tc, x, wd, wu, rope_cos, rope_sin, g, 
             for i in range(2):
                 out1_pass(0, 0, i, 0)
             out0(7)
-            for n in (2, 3):
-                x_interleave(n, 0)
-                x_interleave(n, 1)
-                x_quant(n, 0)
-                x_quant(n, 1)
+            x_quant(2, 0)
+            x_interleave(2, 1)
+            x_interleave(3, 0)
+            x_quant(2, 1)
+            x_interleave(3, 1)
+            x_quant(3, 0)
+            x_quant(3, 1)
             for n in range(4):
                 out1_pair(n, 0)
                 out1_pair(n, 1)

@@ -26,6 +26,9 @@ HF = DH + DR
 KIB = 1024
 FIRST_SHARED = 2
 OWN_HEADS = 4
+SORTED = (2,3,4,5,6,7)
+SORTED_WD = ()
+G_BUFS = 3
 
 
 def tile_multilatentattention_pb_v_kernel(tc, x, wd, wu, rope_cos, rope_sin, g, out_0, out_1):
@@ -54,7 +57,7 @@ def tile_multilatentattention_pb_v_kernel(tc, x, wd, wu, rope_cos, rope_sin, g, 
         warm2 = keep.tile([P, 16], F32, name="warm2", align_bytes=64)
 
         tables = keep.tile([P, 4, 2, DR], F32, name="tables", align_bytes=64)
-        sin_t = keep.tile([P, 4, DR], F32, name="sin_t", align_bytes=64)
+        tables_sorted = keep.tile([P, 4, 2, DR], F32, name="tables_sorted", align_bytes=64)
         tables_t = keep.tile([P, 4, P], F32, name="tables_t", align_bytes=64)
         tables_psum = psum_keep.tile([P, 4, 2, DR], F32, name="tables_psum")
         wu_codes = keep.tile([P, PASSES, DL], U32, name="wu_codes", align_bytes=64)
@@ -71,12 +74,12 @@ def tile_multilatentattention_pb_v_kernel(tc, x, wd, wu, rope_cos, rope_sin, g, 
 
             def load_tables(lo, hi):
                 nc.sync.dma_start(out=tables[:, lo:hi, 0, :], in_=cos_view[:, lo:hi, :])
-                nc.sync.dma_start(out=sin_t[:, lo:hi, :], in_=sin_view[:, lo:hi, :])
+                nc.sync.dma_start(out=tables[:, lo:hi, 1, :], in_=sin_view[:, lo:hi, :])
 
             def load_g(k, parts=1):
                 heads = H // parts
                 if parts == 1:
-                    g_raw[k] = [work.tile([P, H, HF], BF16, name=f"g{k}", tag="g", bufs=6, align_bytes=64)]
+                    g_raw[k] = [work.tile([P, H, HF], BF16, name=f"g{k}", tag="g", bufs=G_BUFS, align_bytes=64)]
                 else:
                     g_raw[k] = [keep.tile([P, heads, HF], BF16, name=f"g{k}_{i}", align_bytes=64) for i in range(parts)]
 
@@ -120,13 +123,19 @@ def tile_multilatentattention_pb_v_kernel(tc, x, wd, wu, rope_cos, rope_sin, g, 
                         nc.tensor.transpose(bank[:, q * P : (q + 1) * P], words[:, w:256:2], ident[:])
 
             def tables_sin(lo, hi):
-                nc.scalar.copy(out=tables[:, lo:hi, 1, 0:32], in_=sin_t[:, lo:hi, 32:64])
-                nc.scalar.mul(out=tables[:, lo:hi, 1, 32:64], in_=sin_t[:, lo:hi, 0:32], mul=-1.0)
+                nc.scalar.mul(out=tables[:, lo:hi, 1, 0:32], in_=tables[:, lo:hi, 1, 0:32], mul=-1.0)
+
+            def tables_sort():
+                nc.scalar.copy(
+                    out=tables_sorted[:].rearrange("p j a (u m e) -> p (j a) u m e", u=2, e=2),
+                    in_=tables[:].rearrange("p j a (m u e) -> p (j a) u m e", u=2, e=2),
+                )
 
             def tables_turn():
                 bank = new_bank()
                 for j in range(4):
-                    nc.tensor.transpose(bank[:, j * P : (j + 1) * P], tables[:, j].rearrange("p a r -> p (a r)"), ident[:])
+                    source = tables_sorted if any(k % 4 == j for k in SORTED) else tables
+                    nc.tensor.transpose(bank[:, j * P : (j + 1) * P], source[:, j].rearrange("p a r -> p (a r)"), ident[:])
                 nc.scalar.copy(out=tables_t[:].rearrange("p j c -> p (j c)"), in_=bank[:])
 
             def tables_back():
@@ -140,37 +149,70 @@ def tile_multilatentattention_pb_v_kernel(tc, x, wd, wu, rope_cos, rope_sin, g, 
 
             prods = {}
 
-            def rope_cos(k, lo, hi, table):
-                if lo == 0:
-                    pc = work.tile([P, H, DR], F32, name="pc", tag="pc", bufs=2, align_bytes=64)
-                    ps = work.tile([P, H, DR], F32, name="ps", tag="ps", bufs=2, align_bytes=64)
-                    prods[k] = (pc, ps)
-                row = table[:, k % 4, 0, :].unsqueeze(1).to_broadcast([P, hi - lo, DR])
-                nc.vector.tensor_tensor(out=prods[k][0][:, lo:hi, :], in0=rope_part(k, lo, hi), in1=row, op=MULT)
+            def rope_tiles(k):
+                pc = work.tile([P, H * DR], F32, name="pc", tag="pc", bufs=2, align_bytes=64)
+                ps = work.tile([P, H * DR], F32, name="ps", tag="ps", bufs=2, align_bytes=64)
+                prods[k] = (pc, ps)
 
-            def rope_sin(k, lo, hi, table):
-                row = table[:, k % 4, 1, :].rearrange("p (a j) -> p a j", a=2).unsqueeze(1).to_broadcast([P, hi - lo, 2, 32])
-                nc.vector.tensor_tensor(
-                    out=prods[k][1][:, lo:hi, :].rearrange("p h (a j) -> p h a j", a=2),
-                    in0=rope_part(k, lo, hi).rearrange("p h (a j) -> p h a j", a=2)[:, :, ::-1, :],
-                    in1=row,
-                    op=MULT,
-                )
+            def plain_product(k, which, lo, hi, table):
+                row = table[:, k % 4, which, :].rearrange("p (a j) -> p a j", a=2).unsqueeze(1).to_broadcast([P, hi - lo, 2, 32])
+                out = prods[k][which][:].rearrange("p (h a j) -> p h a j", h=H, a=2)[:, lo:hi]
+                if which == 1:
+                    out = out[:, :, ::-1]
+                rope = rope_part(k, lo, hi).rearrange("p h (a j) -> p h a j", a=2)
+                nc.vector.tensor_tensor(out=out, in0=rope, in1=row, op=MULT)
 
-            def rope_add(engine, k, lo, hi):
-                pc, ps = prods[k]
-                engine.tensor_tensor(out=rope_part(k, lo, hi), in0=pc[:, lo:hi, :], in1=ps[:, lo:hi, :], op=ADD)
+            def plain_add(engine, k, lo, hi):
+                pc, ps = [t[:].rearrange("p (h f) -> p h f", h=H)[:, lo:hi] for t in prods[k]]
+                engine.tensor_tensor(out=rope_part(k, lo, hi), in0=pc, in1=ps, op=ADD)
+
+            g_sorted = {}
+
+            def sort_g(k, engine="v"):
+                if k not in SORTED:
+                    return
+                t = work.tile([P, 2, H, HF // 4], F32, name="g_sorted", tag="gs", bufs=3, align_bytes=64)
+                g_sorted[k] = t
+                words = g_raw[k][0][:].bitcast(F32)[:, :, : DH // 2]
+                copy_out(engine, t[:, :, :, : DH // 4], words.rearrange("p h (m u) -> p u h m", u=2))
+
+            def product(k, which, u, lo, hi, table):
+                rope = rope_part(k, lo, hi).rearrange("p h (a m u e) -> p h a m u e", a=2, u=2, e=2)[:, :, :, :, u, :]
+                row = table[:, k % 4, which, 32 * u : 32 * u + 32].rearrange("p (a m e) -> p a m e", a=2, e=2)
+                out = prods[k][which][:].rearrange("p (u h a m e) -> p u h a m e", u=2, h=H, a=2, e=2)[:, u, lo:hi]
+                if which == 1:
+                    out = out[:, :, ::-1]
+                nc.vector.tensor_tensor(out=out, in0=rope, in1=row.unsqueeze(1).to_broadcast([P, hi - lo, 2, 8, 2]), op=MULT)
+
+            def rope_add(engine, k, u, lo, hi):
+                pc, ps = [t[:].rearrange("p (u h f) -> p u h f", u=2, h=H)[:, u, lo:hi] for t in prods[k]]
+                out = g_sorted[k][:].bitcast(BF16)[:, u, lo:hi, DH // 2 :]
+                engine.tensor_tensor(out=out, in0=pc, in1=ps, op=ADD)
 
             def rope_window(k):
-                if k - 1 >= FIRST_SHARED:
-                    rope_sin(k - 1, H - 1, H, tables_psum)
-                    rope_add(nc.gpsimd, k - 1, OWN_HEADS, H)
-                if k < TILES:
-                    rope_cos(k, 0, H, tables_psum)
-                    rope_sin(k, 0, H - 1, tables_psum)
+                if k - 1 in SORTED:
+                    product(k - 1, 1, 0, H - 2, H, tables_psum)
+                    rope_add(nc.gpsimd, k - 1, 0, 0, H)
+                    rope_add(nc.gpsimd, k - 1, 1, 2 * OWN_HEADS, H)
+                elif k - 1 >= FIRST_SHARED:
+                    plain_product(k - 1, 1, H - 1, H, tables_psum)
+                    plain_add(nc.gpsimd, k - 1, OWN_HEADS, H)
+                if k in SORTED:
+                    rope_tiles(k)
+                    product(k, 0, 0, 0, H, tables_psum)
+                    product(k, 0, 1, 0, H, tables_psum)
+                    product(k, 1, 1, 0, H, tables_psum)
+                    product(k, 1, 0, 0, H - 2, tables_psum)
+                elif k < TILES:
+                    rope_tiles(k)
+                    plain_product(k, 0, 0, H, tables_psum)
+                    plain_product(k, 1, 0, H - 1, tables_psum)
 
             def rope_own(k):
-                rope_add(nc.vector, k, 0, OWN_HEADS)
+                if k in SORTED:
+                    rope_add(nc.vector, k, 1, 0, 2 * OWN_HEADS)
+                else:
+                    plain_add(nc.vector, k, 0, OWN_HEADS)
 
             wu_grp = {}
 
@@ -200,13 +242,27 @@ def tile_multilatentattention_pb_v_kernel(tc, x, wd, wu, rope_cos, rope_sin, g, 
                         )
 
             wd_grp = {}
+            wd_sorted = {}
+
+            def sort_wd(c, engine="v"):
+                if c not in SORTED_WD:
+                    return
+                t = work.tile([P, 4, 2, P], F32, name="wd_sorted", tag="wds", bufs=2, align_bytes=64)
+                wd_sorted[c] = t
+                copy_out(engine, t[:], wd_raw[c][:].bitcast(F32).rearrange("p i (m u) -> p i u m", u=2))
 
             def wd_bank(n):
                 c, half = n // 2, n % 2
                 if half == 0:
                     wd_grp[c] = work.tile([P, 2048], BF16, name="wd_grp", tag="xgrp", bufs=3, align_bytes=64)
                 bank = new_bank()
-                transpose_pairs(bank, [wd_raw[c][:, 2 * half + i, :] for i in range(2)])
+                if c in wd_sorted:
+                    for i in range(2):
+                        for w in range(2):
+                            q = 2 * i + w
+                            nc.tensor.transpose(bank[:, q * P : (q + 1) * P], wd_sorted[c][:, 2 * half + i, w, :], ident[:])
+                else:
+                    transpose_pairs(bank, [wd_raw[c][:, 2 * half + i, :] for i in range(2)])
                 nc.scalar.copy(
                     out=wd_grp[c][:].bitcast(F32).rearrange("p (m i w) -> p m i w", i=4, w=2)[:, :, 2 * half : 2 * half + 2, :],
                     in_=bank[:].rearrange("p (i w m) -> p m i w", i=2, w=2),
@@ -231,7 +287,13 @@ def tile_multilatentattention_pb_v_kernel(tc, x, wd, wu, rope_cos, rope_sin, g, 
                 if c == 0:
                     dz2_grp[k] = work.tile([P, J], BF16, name="dz2_grp", tag="dz2g", bufs=2, align_bytes=64)
                 bank = new_bank()
-                transpose_pairs(bank, [g_pass(k, 2 * c + i) for i in range(2)])
+                if k in g_sorted:
+                    for i in range(2):
+                        for w in range(2):
+                            q, s = 2 * i + w, 2 * c + i
+                            nc.tensor.transpose(bank[:, q * P : (q + 1) * P], g_sorted[k][:].rearrange("p u h m -> p u (h m)")[:, w, P * s : P * s + P], ident[:])
+                else:
+                    transpose_pairs(bank, [g_pass(k, 2 * c + i) for i in range(2)])
                 nc.scalar.copy(
                     out=dz2_grp[k][:, 1024 * c : 1024 * c + 1024].bitcast(F32).rearrange("p (i r w) -> p i r w", i=2, w=2),
                     in_=bank[:].rearrange("p (i w r) -> p i r w", i=2, w=2),
@@ -396,7 +458,7 @@ def tile_multilatentattention_pb_v_kernel(tc, x, wd, wu, rope_cos, rope_sin, g, 
                     stop=(b == B - 1),
                 )
 
-            def out1_pair(n, h, engines="ss"):
+            def out1_pair(n, h, engines="ss", split=False):
                 res = new_result()
                 for i in range(2):
                     a = 4 * n + 2 * i + h
@@ -409,7 +471,10 @@ def tile_multilatentattention_pb_v_kernel(tc, x, wd, wu, rope_cos, rope_sin, g, 
                         res[:, i, :].rearrange("p (m u e) -> p m u e", u=2, e=2),
                         bank[:].rearrange("p (u m e) -> p m u e", u=2, e=2),
                     )
-                nc.sync.dma_start(out=out1_view[:, n, h], in_=res[:])
+                    if split:
+                        nc.sync.dma_start(out=out1_view[:, n, h, i], in_=res[:, i])
+                if not split:
+                    nc.sync.dma_start(out=out1_view[:, n, h], in_=res[:])
 
             load_g(0, 2)
             load_wu(0, 0, 2)
@@ -434,34 +499,41 @@ def tile_multilatentattention_pb_v_kernel(tc, x, wd, wu, rope_cos, rope_sin, g, 
 
             tables_sin(0, 1)
             wu_bank(0, 0)
-            rope_cos(0, 0, 8, tables)
-            rope_sin(0, 0, 8, tables)
-            rope_cos(0, 8, H, tables)
-            rope_add(nc.vector, 0, 0, 8)
-            rope_sin(0, 8, H, tables)
+            rope_tiles(0)
+            plain_product(0, 0, 0, 8, tables)
+            plain_product(0, 1, 0, 8, tables)
+            plain_product(0, 0, 8, H, tables)
+            plain_add(nc.vector, 0, 0, 8)
+            plain_product(0, 1, 8, H, tables)
             tables_sin(1, 4)
+            tables_sort()
             wu_bank(0, 1)
             wu_bank(0, 2)
-            tables_turn()
             dz2_bank(0, 0)
-            rope_add(nc.vector, 0, 8, H)
+            plain_add(nc.vector, 0, 8, H)
             dz2_bank(0, 1)
-            tables_back()
+            tables_turn()
             dz2_bank(0, 2)
-            rope_cos(1, 0, H, tables)
-            rope_sin(1, 0, H, tables)
+            rope_tiles(1)
+            plain_product(1, 0, 0, H, tables)
+            plain_product(1, 1, 0, H, tables)
             dz2_quant(0, 0, 4)
-            rope_add(nc.vector, 1, 0, H)
+            plain_add(nc.vector, 1, 0, H)
             dz2_quant(0, 4, 6)
-            wu_row(1)
+            wu_bank(1, 0)
+            wu_bank(1, 1)
+            tables_back()
+            wu_bank(1, 2)
             wu_quant(0)
             wu_row(2)
             wu_row(3)
+            sort_g(2)
             wu_quant(1)
             load_x(0)
             load_x(1)
             for c in range(3):
                 dz2_bank(1, c)
+            sort_g(3, "s")
             rope_window(2)
             dz2_quant(1, 0, 4)
             rope_own(2)
@@ -473,89 +545,99 @@ def tile_multilatentattention_pb_v_kernel(tc, x, wd, wu, rope_cos, rope_sin, g, 
             rope_window(3)
             wd_quant(0)
             rope_own(3)
+            sort_g(4)
             wd_bank(2)
             wd_bank(3)
             dz1_transpose(0)
             stage1(1, 0, 3)
+            wd_bank(4)
             dz2_bank(2, 0)
             dz2_bank(2, 1)
             stage1(1, 3, 6)
             wd_quant(1)
             dz1f_quant(0)
             rope_window(4)
-            dz2_quant(2, 0, 4)
-            rope_own(4)
             dz2_bank(2, 2)
-            wd_bank(4)
+            wd_bank(5)
             dz1_transpose(1)
             out0_half(0, 0)
-            wd_bank(5)
-            dz2_bank(3, 0)
-            stage1(2, 0, 3)
-            dz2_quant(2, 4, 6)
-            dz1f_quant(1)
-            rope_window(5)
-            wd_quant(2)
             wd_bank(6)
             wd_bank(7)
-            stage1(2, 3, 6)
-            dz2_bank(3, 1)
-            dz2_bank(3, 2)
+            dz2_quant(2, 0, 4)
+            dz2_quant(2, 4, 6)
+            rope_own(4)
+            sort_g(5)
+            wd_quant(2)
+            dz1f_quant(1)
+            stage1(2)
+            rope_window(5)
+            for c in range(3):
+                dz2_bank(3, c)
+            dz1_transpose(2)
+            out0_half(1, 0)
+            for k in range(2):
+                out0_pass(k, 2)
+                out0_copy(k, 2)
             wd_quant(3)
-            rope_own(5)
-            out0_half(0, 1)
             dz2_quant(3, 0, 4)
+            rope_own(5)
+            sort_g(6)
             dz2_quant(3, 4, 6)
-            x_units = [(n, b) for n in range(4) for b in range(B)]
-            for k in range(3, TILES):
+            rope_window(6)
+            for c in range(3):
+                dz2_bank(4, c)
+            stage1(3)
+            for k in range(2):
+                out0_pass(k, 3)
+                out0_copy(k, 3)
+            dz1f_quant(2)
+            dz2_quant(4, 0, 4)
+            rope_own(6)
+            dz2_quant(4, 4, 6)
+            sort_g(7)
+            for k in range(4, TILES):
                 nxt = k + 1 < TILES
                 if k + 3 < TILES:
                     rope_window(k + 3)
                 if nxt:
-                    dz2_bank(k + 1, 0)
-                    dz2_bank(k + 1, 1)
-                for n in range(4):
-                    out0_pass(k - 2, n)
-                if k == 5:
-                    rope_window(TILES)
-                eng = "v" if k == 5 else "s"
-                out0_copy(k - 2, 0, eng)
-                out0_copy(k - 2, 1, eng)
+                    for c in range(3):
+                        dz2_bank(k + 1, c)
                 dz1_transpose(k - 1)
-                out0_copy(k - 2, 2, eng)
-                out0_copy(k - 2, 3)
                 if nxt:
-                    dz2_bank(k + 1, 2)
-                stage1(k)
+                    stage1(k)
+                    out0(k - 2)
+                else:
+                    for n in range(4):
+                        out0_pass(k - 2, n)
+                    out0_copy(k - 2, 0)
+                    out0_copy(k - 2, 1)
+                    out0_copy(k - 2, 2)
+                    stage1(k)
                 if nxt:
                     dz2_quant(k + 1, 0, 4)
                 if k + 3 < TILES:
                     rope_own(k + 3)
-                if k == 3:
+                if nxt:
                     dz1f_quant(k - 1)
-                    x_interleave(0, 0)
                     dz2_quant(k + 1, 4, 6)
-                    x_quant(0, 0)
                 if k == 4:
-                    dz1f_quant(k - 1)
+                    product(7, 1, 0, H - 2, H, tables_psum)
+                    rope_add(nc.vector, 7, 1, 2 * OWN_HEADS, H)
+                    rope_add(nc.vector, 7, 0, 0, H)
                     dz1_interleave(0)
-                    dz2_quant(k + 1, 4, 6)
-                    dz1_quant(0)
-                    x_interleave(0, 1)
                 if k == 5:
-                    dz1f_quant(k - 1)
-                    x_quant(0, 1)
-                    dz2_quant(k + 1, 4, 6)
-                    x_interleave(1, 0)
+                    x_interleave(0, 0)
+                    dz1_quant(0)
+                    x_quant(0, 0)
+                    x_interleave(0, 1)
                 if k == 6:
+                    x_interleave(1, 0)
+                    x_quant(0, 1)
                     x_quant(1, 0)
-                    dz1f_quant(k - 1)
-                    x_interleave(1, 1)
-                    dz2_quant(k + 1, 4, 6)
-                    x_quant(1, 1)
                 if k == 7:
                     dz1f_quant(k - 1)
-                    x_interleave(2, 0)
+                    out0_copy(k - 2, 3)
+                    x_interleave(1, 1)
             for n in range(4):
                 out0_pass(6, n)
             out0_copy(6, 0, "v")
@@ -569,13 +651,12 @@ def tile_multilatentattention_pb_v_kernel(tc, x, wd, wu, rope_cos, rope_sin, g, 
             for i in range(2):
                 out1_pass(0, 0, i, 0)
             out0(7)
-            x_quant(2, 0)
-            x_interleave(2, 1)
-            x_interleave(3, 0)
-            x_quant(2, 1)
-            x_interleave(3, 1)
-            x_quant(3, 0)
-            x_quant(3, 1)
+            x_quant(1, 1)
+            for n in (2, 3):
+                x_interleave(n, 0)
+                x_interleave(n, 1)
+                x_quant(n, 0)
+                x_quant(n, 1)
             for n in range(4):
                 out1_pair(n, 0)
-                out1_pair(n, 1)
+                out1_pair(n, 1, "sv" if n == 3 else "ss", n == 3)

@@ -25,7 +25,7 @@ GTILES = S // P
 HF = DH + DR
 KIB = 1024
 FIRST_SHARED = 2
-OWN_HEADS = 4
+OWN_HEADS = 6
 SORTED = (2,3,4,5,6,7)
 SORTED_WD = ()
 G_BUFS = 3
@@ -174,7 +174,11 @@ def tile_multilatentattention_pb_v_kernel(tc, x, wd, wu, rope_cos, rope_sin, g, 
                 t = work.tile([P, 2, H, HF // 4], F32, name="g_sorted", tag="gs", bufs=3, align_bytes=64)
                 g_sorted[k] = t
                 words = g_raw[k][0][:].bitcast(F32)[:, :, : DH // 2]
-                copy_out(engine, t[:, :, :, : DH // 4], words.rearrange("p h (m u) -> p u h m", u=2))
+                copy_out(
+                    engine,
+                    t[:, :, :, : DH // 4].rearrange("p u h (g l) -> p h g u l", l=2),
+                    words.rearrange("p h (g l u) -> p h g u l", l=2, u=2),
+                )
 
             def product(k, which, u, lo, hi, table):
                 rope = rope_part(k, lo, hi).rearrange("p h (a m u e) -> p h a m u e", a=2, u=2, e=2)[:, :, :, :, u, :]
@@ -184,16 +188,15 @@ def tile_multilatentattention_pb_v_kernel(tc, x, wd, wu, rope_cos, rope_sin, g, 
                     out = out[:, :, ::-1]
                 nc.vector.tensor_tensor(out=out, in0=rope, in1=row.unsqueeze(1).to_broadcast([P, hi - lo, 2, 8, 2]), op=MULT)
 
-            def rope_add(engine, k, u, lo, hi):
-                pc, ps = [t[:].rearrange("p (u h f) -> p u h f", u=2, h=H)[:, u, lo:hi] for t in prods[k]]
-                out = g_sorted[k][:].bitcast(BF16)[:, u, lo:hi, DH // 2 :]
+            def rope_add(engine, k, lo, hi):
+                pc, ps = [t[:].rearrange("p (u h f) -> p u h f", u=2, h=H)[:, :, lo:hi] for t in prods[k]]
+                out = g_sorted[k][:].bitcast(BF16)[:, :, lo:hi, DH // 2 :]
                 engine.tensor_tensor(out=out, in0=pc, in1=ps, op=ADD)
 
             def rope_window(k):
                 if k - 1 in SORTED:
                     product(k - 1, 1, 0, H - 2, H, tables_psum)
-                    rope_add(nc.gpsimd, k - 1, 0, 0, H)
-                    rope_add(nc.gpsimd, k - 1, 1, 2 * OWN_HEADS, H)
+                    rope_add(nc.gpsimd, k - 1, OWN_HEADS, H)
                 elif k - 1 >= FIRST_SHARED:
                     plain_product(k - 1, 1, H - 1, H, tables_psum)
                     plain_add(nc.gpsimd, k - 1, OWN_HEADS, H)
@@ -208,9 +211,17 @@ def tile_multilatentattention_pb_v_kernel(tc, x, wd, wu, rope_cos, rope_sin, g, 
                     plain_product(k, 0, 0, H, tables_psum)
                     plain_product(k, 1, 0, H - 1, tables_psum)
 
+            def rope_last(k):
+                if k in SORTED:
+                    product(k, 1, 0, H - 2, H, tables_psum)
+                    rope_add(nc.vector, k, OWN_HEADS, H)
+                else:
+                    plain_product(k, 1, H - 1, H, tables_psum)
+                    plain_add(nc.vector, k, OWN_HEADS, H)
+
             def rope_own(k):
                 if k in SORTED:
-                    rope_add(nc.vector, k, 1, 0, 2 * OWN_HEADS)
+                    rope_add(nc.vector, k, 0, OWN_HEADS)
                 else:
                     plain_add(nc.vector, k, 0, OWN_HEADS)
 
@@ -621,9 +632,7 @@ def tile_multilatentattention_pb_v_kernel(tc, x, wd, wu, rope_cos, rope_sin, g, 
                     dz1f_quant(k - 1)
                     dz2_quant(k + 1, 4, 6)
                 if k == 4:
-                    product(7, 1, 0, H - 2, H, tables_psum)
-                    rope_add(nc.vector, 7, 1, 2 * OWN_HEADS, H)
-                    rope_add(nc.vector, 7, 0, 0, H)
+                    rope_last(7)
                     dz1_interleave(0)
                 if k == 5:
                     x_interleave(0, 0)

@@ -16,7 +16,6 @@ E4M3 = mybir.dt.float8_e4m3fn_x4
 E5M2 = mybir.dt.float8_e5m2_x4
 MULT = mybir.AluOpType.mult
 ADD = mybir.AluOpType.add
-SUB = mybir.AluOpType.subtract
 
 P = 128
 PASSES = J // 512
@@ -24,11 +23,10 @@ TILES = T // P
 GTILES = S // P
 HF = DH + DR
 KIB = 1024
-FIRST_SHARED = 2
+COS, SIN = 0, 1
 OWN_HEADS = 6
-SORTED = (2,3,4,5,6,7)
-SORTED_WD = ()
-G_BUFS = 3
+GRAD_SLOTS = 4
+RESULT_SLOTS = 10
 
 
 def tile_multilatentattention_pb_v_kernel(tc, x, wd, wu, rope_cos, rope_sin, g, out_0, out_1):
@@ -51,14 +49,12 @@ def tile_multilatentattention_pb_v_kernel(tc, x, wd, wu, rope_cos, rope_sin, g, 
         psum_keep = ctx.enter_context(tc.psum_pool(name="psum_keep", bufs=1))
 
         ident = keep.tile([P, P], F32, name="ident", align_bytes=64)
-        make_identity(nc, ident[:])
-        warm = keep.tile([P, 16], F32, name="warm", align_bytes=64)
-        nc.vector.memset(warm[:], 0.0)
-        warm2 = keep.tile([P, 16], F32, name="warm2", align_bytes=64)
+        ident_first = keep.tile([P, P], F32, name="ident_first", align_bytes=64)
+        make_identity(nc, ident_first[:])
 
         tables = keep.tile([P, 4, 2, DR], F32, name="tables", align_bytes=64)
-        tables_sorted = keep.tile([P, 4, 2, DR], F32, name="tables_sorted", align_bytes=64)
-        tables_t = keep.tile([P, 4, P], F32, name="tables_t", align_bytes=64)
+        tables_sorted = arena.tile([P, 4, 2, DR], F32, name="tables_sorted", offset=64 * KIB, align_bytes=64)
+        tables_t = arena.tile([P, 4, P], F32, name="tables_t", offset=66 * KIB, align_bytes=64)
         tables_psum = psum_keep.tile([P, 4, 2, DR], F32, name="tables_psum")
         wu_codes = keep.tile([P, PASSES, DL], U32, name="wu_codes", align_bytes=64)
         wu_scales = keep.tile([P, PASSES, DL], U8, name="wu_scales", align_bytes=64)
@@ -68,27 +64,23 @@ def tile_multilatentattention_pb_v_kernel(tc, x, wd, wu, rope_cos, rope_sin, g, 
         x_scales = keep.tile([P, B, D], U8, name="x_scales", align_bytes=64)
 
         with tc.manual_schedule():
-            nc.scalar.copy(out=warm2[:], in_=warm[:])
+            nc.scalar.copy(out=ident[:], in_=ident_first[:])
 
             wu_raw, g_raw, wd_raw, x_raw = {}, {}, {}, {}
 
             def load_tables(lo, hi):
-                nc.sync.dma_start(out=tables[:, lo:hi, 0, :], in_=cos_view[:, lo:hi, :])
-                nc.sync.dma_start(out=tables[:, lo:hi, 1, :], in_=sin_view[:, lo:hi, :])
+                nc.sync.dma_start(out=tables[:, lo:hi, COS, :], in_=cos_view[:, lo:hi, :])
+                nc.sync.dma_start(out=tables[:, lo:hi, SIN, :], in_=sin_view[:, lo:hi, :])
 
-            def load_g(k, parts=1):
-                heads = H // parts
-                if parts == 1:
-                    g_raw[k] = [work.tile([P, H, HF], BF16, name=f"g{k}", tag="g", bufs=G_BUFS, align_bytes=64)]
-                else:
-                    g_raw[k] = [keep.tile([P, heads, HF], BF16, name=f"g{k}_{i}", align_bytes=64) for i in range(parts)]
+            def load_g(k):
+                t = work.tile([P, H, HF], BF16, name=f"g{k}", tag="g", bufs=GRAD_SLOTS, align_bytes=64)
+                nc.sync.dma_start(out=t[:], in_=g_view[k // GTILES][:, k % GTILES])
+                g_raw[k] = [t]
 
-            def issue_g(k, i=0):
-                if k not in g_raw:
-                    load_g(k)
-                t = g_raw[k][i]
-                heads = t.shape[1]
-                nc.sync.dma_start(out=t[:], in_=g_view[k // GTILES][:, k % GTILES, i * heads : (i + 1) * heads])
+            def load_first_g(half):
+                t = keep.tile([P, H // 2, HF], BF16, name=f"g0_{half}", align_bytes=64)
+                nc.sync.dma_start(out=t[:], in_=g_view[0][:, 0, half * H // 2 : (half + 1) * H // 2])
+                g_raw.setdefault(0, []).append(t)
 
             def load_wu(r, lo=0, hi=PASSES):
                 t = arena.tile([P, 512 * (hi - lo)], BF16, name=f"wu{r}_{lo}", offset=KIB * (PASSES * r + lo), align_bytes=64)
@@ -97,7 +89,7 @@ def tile_multilatentattention_pb_v_kernel(tc, x, wd, wu, rope_cos, rope_sin, g, 
                     wu_raw[r, s] = t[:, 512 * (s - lo) : 512 * (s - lo + 1)]
 
             def load_wd(c):
-                t = arena.tile([P, 4, DL], BF16, name=f"wd{c}", offset=4 * KIB * (PASSES + c), align_bytes=64)
+                t = arena.tile([P, 4, DL], BF16, name=f"wd{c}", offset=KIB * (24 + 4 * c), align_bytes=64)
                 nc.sync.dma_start(out=t[:], in_=wd_view[:, c])
                 wd_raw[c] = t
 
@@ -106,8 +98,8 @@ def tile_multilatentattention_pb_v_kernel(tc, x, wd, wu, rope_cos, rope_sin, g, 
                 nc.sync.dma_start(out=t[:], in_=x_view[b])
                 x_raw[b] = t
 
-            def copy_out(engine, out, in_):
-                if engine == "v":
+            def copy(engine, out, in_):
+                if engine == "vector":
                     nc.vector.tensor_copy(out=out, in_=in_)
                 else:
                     nc.scalar.copy(out=out, in_=in_)
@@ -118,12 +110,12 @@ def tile_multilatentattention_pb_v_kernel(tc, x, wd, wu, rope_cos, rope_sin, g, 
             def transpose_pairs(bank, rows):
                 for i in range(2):
                     words = rows[i].bitcast(F32)
-                    for w in range(2):
-                        q = 2 * i + w
-                        nc.tensor.transpose(bank[:, q * P : (q + 1) * P], words[:, w:256:2], ident[:])
+                    for u in range(2):
+                        q = 2 * i + u
+                        nc.tensor.transpose(bank[:, q * P : (q + 1) * P], words[:, u:256:2], ident[:])
 
-            def tables_sin(lo, hi):
-                nc.scalar.mul(out=tables[:, lo:hi, 1, 0:32], in_=tables[:, lo:hi, 1, 0:32], mul=-1.0)
+            def tables_negate(lo, hi):
+                nc.scalar.mul(out=tables[:, lo:hi, SIN, 0:32], in_=tables[:, lo:hi, SIN, 0:32], mul=-1.0)
 
             def tables_sort():
                 nc.scalar.copy(
@@ -134,11 +126,10 @@ def tile_multilatentattention_pb_v_kernel(tc, x, wd, wu, rope_cos, rope_sin, g, 
             def tables_turn():
                 bank = new_bank()
                 for j in range(4):
-                    source = tables_sorted if any(k % 4 == j for k in SORTED) else tables
-                    nc.tensor.transpose(bank[:, j * P : (j + 1) * P], source[:, j].rearrange("p a r -> p (a r)"), ident[:])
+                    nc.tensor.transpose(bank[:, j * P : (j + 1) * P], tables_sorted[:, j].rearrange("p a r -> p (a r)"), ident[:])
                 nc.scalar.copy(out=tables_t[:].rearrange("p j c -> p (j c)"), in_=bank[:])
 
-            def tables_back():
+            def tables_turn_back():
                 for j in range(4):
                     nc.tensor.transpose(tables_psum[:, j].rearrange("p a r -> p (a r)"), tables_t[:, j, :], ident[:])
 
@@ -147,136 +138,102 @@ def tile_multilatentattention_pb_v_kernel(tc, x, wd, wu, rope_cos, rope_sin, g, 
                 per = H // len(parts)
                 return parts[lo // per][:, lo % per : lo % per + hi - lo, DH:HF]
 
-            prods = {}
+            products = {}
 
-            def rope_tiles(k):
-                pc = work.tile([P, H * DR], F32, name="pc", tag="pc", bufs=2, align_bytes=64)
-                ps = work.tile([P, H * DR], F32, name="ps", tag="ps", bufs=2, align_bytes=64)
-                prods[k] = (pc, ps)
+            def new_products(k):
+                products[k] = [work.tile([P, H * DR], F32, name=n, tag=n, bufs=2, align_bytes=64) for n in ("pc", "ps")]
 
-            def plain_product(k, which, lo, hi, table):
-                row = table[:, k % 4, which, :].rearrange("p (a j) -> p a j", a=2).unsqueeze(1).to_broadcast([P, hi - lo, 2, 32])
-                out = prods[k][which][:].rearrange("p (h a j) -> p h a j", h=H, a=2)[:, lo:hi]
-                if which == 1:
+            def plain_product(k, which, lo, hi):
+                row = tables[:, k, which, :].rearrange("p (a j) -> p a j", a=2).unsqueeze(1).to_broadcast([P, hi - lo, 2, 32])
+                out = products[k][which][:].rearrange("p (h a j) -> p h a j", h=H, a=2)[:, lo:hi]
+                if which == SIN:
                     out = out[:, :, ::-1]
                 rope = rope_part(k, lo, hi).rearrange("p h (a j) -> p h a j", a=2)
                 nc.vector.tensor_tensor(out=out, in0=rope, in1=row, op=MULT)
 
-            def plain_add(engine, k, lo, hi):
-                pc, ps = [t[:].rearrange("p (h f) -> p h f", h=H)[:, lo:hi] for t in prods[k]]
-                engine.tensor_tensor(out=rope_part(k, lo, hi), in0=pc, in1=ps, op=ADD)
+            def plain_sum(k, lo, hi):
+                pc, ps = [t[:].rearrange("p (h f) -> p h f", h=H)[:, lo:hi] for t in products[k]]
+                nc.vector.tensor_tensor(out=rope_part(k, lo, hi), in0=pc, in1=ps, op=ADD)
 
             g_sorted = {}
 
-            def sort_g(k, engine="v"):
-                if k not in SORTED:
-                    return
+            def sort_content(k, engine="vector"):
                 t = work.tile([P, 2, H, HF // 4], F32, name="g_sorted", tag="gs", bufs=3, align_bytes=64)
                 g_sorted[k] = t
                 words = g_raw[k][0][:].bitcast(F32)[:, :, : DH // 2]
-                copy_out(
+                copy(
                     engine,
                     t[:, :, :, : DH // 4].rearrange("p u h (g l) -> p h g u l", l=2),
                     words.rearrange("p h (g l u) -> p h g u l", l=2, u=2),
                 )
 
-            def product(k, which, u, lo, hi, table):
+            def sorted_product(k, which, u, lo, hi):
                 rope = rope_part(k, lo, hi).rearrange("p h (a m u e) -> p h a m u e", a=2, u=2, e=2)[:, :, :, :, u, :]
-                row = table[:, k % 4, which, 32 * u : 32 * u + 32].rearrange("p (a m e) -> p a m e", a=2, e=2)
-                out = prods[k][which][:].rearrange("p (u h a m e) -> p u h a m e", u=2, h=H, a=2, e=2)[:, u, lo:hi]
-                if which == 1:
+                row = tables_psum[:, k % 4, which, 32 * u : 32 * u + 32].rearrange("p (a m e) -> p a m e", a=2, e=2)
+                out = products[k][which][:].rearrange("p (u h a m e) -> p u h a m e", u=2, h=H, a=2, e=2)[:, u, lo:hi]
+                if which == SIN:
                     out = out[:, :, ::-1]
                 nc.vector.tensor_tensor(out=out, in0=rope, in1=row.unsqueeze(1).to_broadcast([P, hi - lo, 2, 8, 2]), op=MULT)
 
-            def rope_add(engine, k, lo, hi):
-                pc, ps = [t[:].rearrange("p (u h f) -> p u h f", u=2, h=H)[:, :, lo:hi] for t in prods[k]]
+            def sorted_sum(engine, k, lo, hi):
+                pc, ps = [t[:].rearrange("p (u h f) -> p u h f", u=2, h=H)[:, :, lo:hi] for t in products[k]]
                 out = g_sorted[k][:].bitcast(BF16)[:, :, lo:hi, DH // 2 :]
                 engine.tensor_tensor(out=out, in0=pc, in1=ps, op=ADD)
 
-            def rope_window(k):
-                if k - 1 in SORTED:
-                    product(k - 1, 1, 0, H - 2, H, tables_psum)
-                    rope_add(nc.gpsimd, k - 1, OWN_HEADS, H)
-                elif k - 1 >= FIRST_SHARED:
-                    plain_product(k - 1, 1, H - 1, H, tables_psum)
-                    plain_add(nc.gpsimd, k - 1, OWN_HEADS, H)
-                if k in SORTED:
-                    rope_tiles(k)
-                    product(k, 0, 0, 0, H, tables_psum)
-                    product(k, 0, 1, 0, H, tables_psum)
-                    product(k, 1, 1, 0, H, tables_psum)
-                    product(k, 1, 0, 0, H - 2, tables_psum)
-                elif k < TILES:
-                    rope_tiles(k)
-                    plain_product(k, 0, 0, H, tables_psum)
-                    plain_product(k, 1, 0, H - 1, tables_psum)
+            def rope_products(k):
+                new_products(k)
+                sorted_product(k, COS, 0, 0, H)
+                sorted_product(k, COS, 1, 0, H)
+                sorted_product(k, SIN, 1, 0, H)
+                sorted_product(k, SIN, 0, 0, H - 2)
 
-            def rope_last(k):
-                if k in SORTED:
-                    product(k, 1, 0, H - 2, H, tables_psum)
-                    rope_add(nc.vector, k, OWN_HEADS, H)
-                else:
-                    plain_product(k, 1, H - 1, H, tables_psum)
-                    plain_add(nc.vector, k, OWN_HEADS, H)
+            def rope_finish(k, engine):
+                sorted_product(k, SIN, 0, H - 2, H)
+                sorted_sum(engine, k, OWN_HEADS, H)
+
+            def rope_window(k):
+                rope_finish(k - 1, nc.gpsimd)
+                rope_products(k)
 
             def rope_own(k):
-                if k in SORTED:
-                    rope_add(nc.vector, k, 0, OWN_HEADS)
-                else:
-                    plain_add(nc.vector, k, 0, OWN_HEADS)
+                sorted_sum(nc.vector, k, 0, OWN_HEADS)
 
             wu_grp = {}
 
             def wu_bank(r, c):
                 if r % 2 == 0:
-                    wu_grp[r // 2, c] = arena.tile([P, 2, 2, 512], BF16, name=f"wu_grp{r}_{c}", offset=KIB * (40 + 4 * (3 * (r // 2) + c)), align_bytes=64)
-                grouped = wu_grp[r // 2, c]
+                    offset = KIB * (40 + 4 * (3 * (r // 2) + c))
+                    wu_grp[r // 2, c] = arena.tile([P, 2, 2, 512], BF16, name=f"wu_grp{r}_{c}", offset=offset, align_bytes=64)
                 bank = new_bank()
                 transpose_pairs(bank, [wu_raw[r, 2 * c + i] for i in range(2)])
                 nc.scalar.copy(
-                    out=grouped[:, :, r % 2, :].bitcast(F32).rearrange("p i (m w) -> p i m w", w=2),
-                    in_=bank[:].rearrange("p (i w m) -> p i m w", i=2, w=2),
+                    out=wu_grp[r // 2, c][:, :, r % 2, :].bitcast(F32).rearrange("p i (m u) -> p i m u", u=2),
+                    in_=bank[:].rearrange("p (i u m) -> p i m u", i=2, u=2),
                 )
 
             def wu_row(r):
                 for c in range(3):
                     wu_bank(r, c)
 
-            def wu_quant(u, cs=(0, 1, 2)):
-                for c in cs:
-                    for i in range(2):
-                        s = 2 * c + i
-                        nc.vector.quantize_mx(
-                            out=wu_codes[:, s, 256 * u : 256 * u + 256].bitcast(E4M3),
-                            scales=wu_scales[:, s, 256 * u : 256 * u + 256],
-                            in_=wu_grp[u, c][:, i].rearrange("p r c -> p (r c)"),
-                        )
+            def wu_quant(pair):
+                for s in range(PASSES):
+                    nc.vector.quantize_mx(
+                        out=wu_codes[:, s, 256 * pair : 256 * pair + 256].bitcast(E4M3),
+                        scales=wu_scales[:, s, 256 * pair : 256 * pair + 256],
+                        in_=wu_grp[pair, s // 2][:, s % 2].rearrange("p r c -> p (r c)"),
+                    )
 
             wd_grp = {}
-            wd_sorted = {}
-
-            def sort_wd(c, engine="v"):
-                if c not in SORTED_WD:
-                    return
-                t = work.tile([P, 4, 2, P], F32, name="wd_sorted", tag="wds", bufs=2, align_bytes=64)
-                wd_sorted[c] = t
-                copy_out(engine, t[:], wd_raw[c][:].bitcast(F32).rearrange("p i (m u) -> p i u m", u=2))
 
             def wd_bank(n):
                 c, half = n // 2, n % 2
                 if half == 0:
                     wd_grp[c] = work.tile([P, 2048], BF16, name="wd_grp", tag="xgrp", bufs=3, align_bytes=64)
                 bank = new_bank()
-                if c in wd_sorted:
-                    for i in range(2):
-                        for w in range(2):
-                            q = 2 * i + w
-                            nc.tensor.transpose(bank[:, q * P : (q + 1) * P], wd_sorted[c][:, 2 * half + i, w, :], ident[:])
-                else:
-                    transpose_pairs(bank, [wd_raw[c][:, 2 * half + i, :] for i in range(2)])
+                transpose_pairs(bank, [wd_raw[c][:, 2 * half + i, :] for i in range(2)])
                 nc.scalar.copy(
-                    out=wd_grp[c][:].bitcast(F32).rearrange("p (m i w) -> p m i w", i=4, w=2)[:, :, 2 * half : 2 * half + 2, :],
-                    in_=bank[:].rearrange("p (i w m) -> p m i w", i=2, w=2),
+                    out=wd_grp[c][:].bitcast(F32).rearrange("p (m i u) -> p m i u", i=4, u=2)[:, :, 2 * half : 2 * half + 2, :],
+                    in_=bank[:].rearrange("p (i u m) -> p m i u", i=2, u=2),
                 )
 
             def wd_quant(c):
@@ -299,41 +256,42 @@ def tile_multilatentattention_pb_v_kernel(tc, x, wd, wu, rope_cos, rope_sin, g, 
                     dz2_grp[k] = work.tile([P, J], BF16, name="dz2_grp", tag="dz2g", bufs=2, align_bytes=64)
                 bank = new_bank()
                 if k in g_sorted:
+                    words = g_sorted[k][:].rearrange("p u h m -> p u (h m)")
                     for i in range(2):
-                        for w in range(2):
-                            q, s = 2 * i + w, 2 * c + i
-                            nc.tensor.transpose(bank[:, q * P : (q + 1) * P], g_sorted[k][:].rearrange("p u h m -> p u (h m)")[:, w, P * s : P * s + P], ident[:])
+                        for u in range(2):
+                            q, s = 2 * i + u, 2 * c + i
+                            nc.tensor.transpose(bank[:, q * P : (q + 1) * P], words[:, u, P * s : P * s + P], ident[:])
                 else:
                     transpose_pairs(bank, [g_pass(k, 2 * c + i) for i in range(2)])
                 nc.scalar.copy(
-                    out=dz2_grp[k][:, 1024 * c : 1024 * c + 1024].bitcast(F32).rearrange("p (i r w) -> p i r w", i=2, w=2),
-                    in_=bank[:].rearrange("p (i w r) -> p i r w", i=2, w=2),
+                    out=dz2_grp[k][:, 1024 * c : 1024 * c + 1024].bitcast(F32).rearrange("p (i r u) -> p i r u", i=2, u=2),
+                    in_=bank[:].rearrange("p (i u r) -> p i r u", i=2, u=2),
                 )
 
             dz2 = {}
 
-            def dz2_quant(k, a, b):
-                if a == 0:
+            def dz2_quant(k, lo, hi):
+                if lo == 0:
                     codes = work.tile([P, PASSES, P], U32, name="dz2_codes", tag="dz2c", bufs=3, align_bytes=64)
                     scales = work.tile([P, PASSES, P], U8, name="dz2_scales", tag="dz2s", bufs=3, align_bytes=64)
                     dz2[k] = (codes, scales)
                 codes, scales = dz2[k]
                 nc.vector.quantize_mx(
-                    out=codes[:, a:b, :].rearrange("p s r -> p (s r)").bitcast(E5M2),
-                    scales=scales[:, a:b, :].rearrange("p s r -> p (s r)"),
-                    in_=dz2_grp[k][:, 512 * a : 512 * b],
+                    out=codes[:, lo:hi, :].rearrange("p s r -> p (s r)").bitcast(E5M2),
+                    scales=scales[:, lo:hi, :].rearrange("p s r -> p (s r)"),
+                    in_=dz2_grp[k][:, 512 * lo : 512 * hi],
                 )
 
             dz1_tok = {}
-            acc = {}
+            dz1_acc = {}
 
-            def stage1(k, lo=0, hi=PASSES):
+            def dz1_passes(k, lo=0, hi=PASSES):
                 codes, scales = dz2[k]
                 if lo == 0:
-                    acc[k] = new_bank()
+                    dz1_acc[k] = new_bank()
                 for s in range(lo, hi):
                     nc.tensor.matmul_mx(
-                        out=acc[k][:],
+                        out=dz1_acc[k][:],
                         lhsT=codes[:, s, :].bitcast(E5M2),
                         lhsT_scale=scales[:, s, :],
                         rhs=wu_codes[:, s, :].bitcast(E4M3),
@@ -346,7 +304,7 @@ def tile_multilatentattention_pb_v_kernel(tc, x, wd, wu, rope_cos, rope_sin, g, 
                         dz1_tok[k // GTILES] = work.tile([P, GTILES, DL], BF16, name="dz1_tok", tag="dz1t", bufs=2, align_bytes=64)
                     nc.scalar.copy(
                         out=dz1_tok[k // GTILES][:, k % GTILES, :].rearrange("p (u m e) -> p u m e", u=2, e=2),
-                        in_=acc[k][:].rearrange("p (u e m) -> p u m e", u=2, e=2),
+                        in_=dz1_acc[k][:].rearrange("p (u e m) -> p u m e", u=2, e=2),
                     )
 
             dz1f_grp = {}
@@ -356,12 +314,11 @@ def tile_multilatentattention_pb_v_kernel(tc, x, wd, wu, rope_cos, rope_sin, g, 
                 bank = new_bank()
                 for u in range(2):
                     nc.tensor.transpose(bank[:, u * P : (u + 1) * P], words[:, u * P : (u + 1) * P], ident[:])
-                grouped = work.tile([P, DL], BF16, name="dz1f_grp", tag="dz1fg", bufs=2, align_bytes=64)
+                dz1f_grp[k] = work.tile([P, DL], BF16, name="dz1f_grp", tag="dz1fg", bufs=2, align_bytes=64)
                 nc.scalar.copy(
-                    out=grouped[:].bitcast(F32).rearrange("p (r u) -> p r u", u=2),
+                    out=dz1f_grp[k][:].bitcast(F32).rearrange("p (r u) -> p r u", u=2),
                     in_=bank[:, : 2 * P].rearrange("p (u r) -> p r u", u=2),
                 )
-                dz1f_grp[k] = grouped
 
             dz1f = {}
 
@@ -374,18 +331,18 @@ def tile_multilatentattention_pb_v_kernel(tc, x, wd, wu, rope_cos, rope_sin, g, 
             results = []
 
             def new_result():
-                slot = len(results) % 10
+                slot = len(results) % RESULT_SLOTS
                 t = arena.tile([P, 2, 512], F32, name=f"res{len(results)}", offset=4 * KIB * slot, align_bytes=64)
                 results.append(t)
                 return t
 
-            acc0 = {}
+            out0_acc = {}
 
             def out0_pass(k, n):
                 codes, scales = dz1f[k]
-                acc0[k, n] = new_bank()
+                out0_acc[k, n] = new_bank()
                 nc.tensor.matmul_mx(
-                    out=acc0[k, n][:],
+                    out=out0_acc[k, n][:],
                     lhsT=codes[:].bitcast(E5M2),
                     lhsT_scale=scales[:],
                     rhs=wd_codes[:, 512 * n : 512 * n + 512].bitcast(E4M3),
@@ -394,28 +351,24 @@ def tile_multilatentattention_pb_v_kernel(tc, x, wd, wu, rope_cos, rope_sin, g, 
                     stop=True,
                 )
 
-            res0 = {}
+            out0_res = {}
 
-            def out0_copy(k, n, engine="s"):
+            def out0_copy(k, n, engine="scalar"):
                 half, i = n // 2, n % 2
                 if i == 0:
-                    res0[k, half] = new_result()
-                res = res0[k, half]
-                copy_out(engine, res[:, i, :], acc0[k, n][:])
+                    out0_res[k, half] = new_result()
+                res = out0_res[k, half]
+                copy(engine, res[:, i, :], out0_acc[k, n][:])
                 if i == 1:
                     nc.sync.dma_start(
                         out=out0_view[k // GTILES][:, k % GTILES, 1024 * half : 1024 * half + 1024],
                         in_=res[:].rearrange("p i c -> p (i c)"),
                     )
 
-            def out0_half(k, half, engines="ss"):
-                for i in range(2):
-                    out0_pass(k, 2 * half + i)
-                    out0_copy(k, 2 * half + i, engines[i])
-
-            def out0(k):
-                out0_half(k, 0)
-                out0_half(k, 1)
+            def out0(k, blocks=range(4)):
+                for n in blocks:
+                    out0_pass(k, n)
+                    out0_copy(k, n)
 
             dz1 = {}
             dz1_grp = {}
@@ -438,10 +391,9 @@ def tile_multilatentattention_pb_v_kernel(tc, x, wd, wu, rope_cos, rope_sin, g, 
             x_grp = {}
 
             def x_interleave(n, b):
-                grouped = work.tile([P, 512, 4], BF16, name="x_grp", tag="xgrp", bufs=3, align_bytes=64)
-                x_grp[n, b] = grouped
+                x_grp[n, b] = work.tile([P, 512, 4], BF16, name="x_grp", tag="xgrp", bufs=3, align_bytes=64)
                 nc.vector.tensor_copy(
-                    out=grouped[:].rearrange("p (i g l) t -> p g t l i", i=2, l=4),
+                    out=x_grp[n, b][:].rearrange("p (i g l) t -> p g t l i", i=2, l=4),
                     in_=x_raw[b][:, :, 512 * n : 512 * n + 512].rearrange("p t (g l i) -> p g t l i", i=2, l=4),
                 )
 
@@ -452,15 +404,15 @@ def tile_multilatentattention_pb_v_kernel(tc, x, wd, wu, rope_cos, rope_sin, g, 
                     in_=x_grp[n, b][:].rearrange("p c t -> p (c t)"),
                 )
 
-            acc1 = {}
+            out1_acc = {}
 
             def out1_pass(n, h, i, b):
                 a = 4 * n + 2 * i + h
                 if b == 0:
-                    acc1[a] = new_bank()
+                    out1_acc[a] = new_bank()
                 codes, scales = dz1[b]
                 nc.tensor.matmul_mx(
-                    out=acc1[a][:],
+                    out=out1_acc[a][:],
                     lhsT=x_codes[:, b, P * a : P * a + P].bitcast(E4M3),
                     lhsT_scale=x_scales[:, b, P * a : P * a + P],
                     rhs=codes[:].bitcast(E5M2),
@@ -469,170 +421,157 @@ def tile_multilatentattention_pb_v_kernel(tc, x, wd, wu, rope_cos, rope_sin, g, 
                     stop=(b == B - 1),
                 )
 
-            def out1_pair(n, h, engines="ss", split=False):
+            def out1_pair(n, h):
+                last = (n, h) == (3, 1)
                 res = new_result()
                 for i in range(2):
                     a = 4 * n + 2 * i + h
-                    if a not in acc1:
+                    if a not in out1_acc:
                         out1_pass(n, h, i, 0)
                     out1_pass(n, h, i, 1)
-                    bank = acc1[a]
-                    copy_out(
-                        engines[i],
+                    copy(
+                        "vector" if last and i == 1 else "scalar",
                         res[:, i, :].rearrange("p (m u e) -> p m u e", u=2, e=2),
-                        bank[:].rearrange("p (u m e) -> p m u e", u=2, e=2),
+                        out1_acc[a][:].rearrange("p (u m e) -> p m u e", u=2, e=2),
                     )
-                    if split:
+                    if last:
                         nc.sync.dma_start(out=out1_view[:, n, h, i], in_=res[:, i])
-                if not split:
+                if not last:
                     nc.sync.dma_start(out=out1_view[:, n, h], in_=res[:])
 
-            load_g(0, 2)
             load_wu(0, 0, 2)
             load_tables(0, 1)
-            issue_g(0, 0)
-            issue_g(0, 1)
-            load_wu(0, 2, 6)
+            load_first_g(0)
+            load_first_g(1)
+            load_wu(0, 2, PASSES)
             load_tables(1, 4)
-            issue_g(1)
-            load_wu(1)
-            load_wu(2)
-            load_wu(3)
-            issue_g(2)
+            load_g(1)
+            for r in range(1, 4):
+                load_wu(r)
+            load_g(2)
             load_wd(0)
-            issue_g(3)
+            load_g(3)
             load_wd(1)
             load_wd(2)
-            issue_g(4)
+            load_g(4)
             load_wd(3)
             for k in range(5, TILES):
-                issue_g(k)
+                load_g(k)
 
-            tables_sin(0, 1)
+            tables_negate(0, 1)
             wu_bank(0, 0)
-            rope_tiles(0)
-            plain_product(0, 0, 0, 8, tables)
-            plain_product(0, 1, 0, 8, tables)
-            plain_product(0, 0, 8, H, tables)
-            plain_add(nc.vector, 0, 0, 8)
-            plain_product(0, 1, 8, H, tables)
-            tables_sin(1, 4)
+            new_products(0)
+            plain_product(0, COS, 0, 8)
+            plain_product(0, SIN, 0, 8)
+            plain_product(0, COS, 8, H)
+            plain_sum(0, 0, 8)
+            plain_product(0, SIN, 8, H)
+            tables_negate(1, 4)
             tables_sort()
             wu_bank(0, 1)
             wu_bank(0, 2)
             dz2_bank(0, 0)
-            plain_add(nc.vector, 0, 8, H)
+            plain_sum(0, 8, H)
             dz2_bank(0, 1)
             tables_turn()
             dz2_bank(0, 2)
-            rope_tiles(1)
-            plain_product(1, 0, 0, H, tables)
-            plain_product(1, 1, 0, H, tables)
+            new_products(1)
+            plain_product(1, COS, 0, H)
+            plain_product(1, SIN, 0, H)
             dz2_quant(0, 0, 4)
-            plain_add(nc.vector, 1, 0, H)
+            plain_sum(1, 0, H)
             dz2_quant(0, 4, 6)
             wu_bank(1, 0)
             wu_bank(1, 1)
-            tables_back()
+            tables_turn_back()
             wu_bank(1, 2)
             wu_quant(0)
             wu_row(2)
             wu_row(3)
-            sort_g(2)
+            sort_content(2)
             wu_quant(1)
-            load_x(0)
-            load_x(1)
+            for b in range(B):
+                load_x(b)
             for c in range(3):
                 dz2_bank(1, c)
-            sort_g(3, "s")
-            rope_window(2)
+            sort_content(3, "scalar")
+            rope_products(2)
             dz2_quant(1, 0, 4)
             rope_own(2)
             dz2_quant(1, 4, 6)
-            stage1(0, 0, 3)
+
+            dz1_passes(0, 0, 3)
             wd_bank(0)
             wd_bank(1)
-            stage1(0, 3, 6)
+            dz1_passes(0, 3, 6)
             rope_window(3)
             wd_quant(0)
             rope_own(3)
-            sort_g(4)
+            sort_content(4)
             wd_bank(2)
             wd_bank(3)
             dz1_transpose(0)
-            stage1(1, 0, 3)
+            dz1_passes(1, 0, 3)
             wd_bank(4)
             dz2_bank(2, 0)
             dz2_bank(2, 1)
-            stage1(1, 3, 6)
+            dz1_passes(1, 3, 6)
             wd_quant(1)
             dz1f_quant(0)
             rope_window(4)
             dz2_bank(2, 2)
             wd_bank(5)
             dz1_transpose(1)
-            out0_half(0, 0)
+            out0(0, (0, 1))
             wd_bank(6)
             wd_bank(7)
             dz2_quant(2, 0, 4)
             dz2_quant(2, 4, 6)
             rope_own(4)
-            sort_g(5)
+            sort_content(5)
             wd_quant(2)
             dz1f_quant(1)
-            stage1(2)
+            dz1_passes(2)
             rope_window(5)
-            for c in range(3):
-                dz2_bank(3, c)
+            dz2_bank(3, 0)
+            dz2_bank(3, 1)
+            out0(1, (0, 1))
+            dz2_bank(3, 2)
             dz1_transpose(2)
-            out0_half(1, 0)
             for k in range(2):
-                out0_pass(k, 2)
-                out0_copy(k, 2)
+                out0(k, (2,))
             wd_quant(3)
             dz2_quant(3, 0, 4)
             rope_own(5)
-            sort_g(6)
+            sort_content(6)
             dz2_quant(3, 4, 6)
             rope_window(6)
             for c in range(3):
                 dz2_bank(4, c)
-            stage1(3)
+            dz1_passes(3)
             for k in range(2):
-                out0_pass(k, 3)
-                out0_copy(k, 3)
+                out0(k, (3,))
             dz1f_quant(2)
             dz2_quant(4, 0, 4)
             rope_own(6)
             dz2_quant(4, 4, 6)
-            sort_g(7)
-            for k in range(4, TILES):
-                nxt = k + 1 < TILES
-                if k + 3 < TILES:
-                    rope_window(k + 3)
-                if nxt:
-                    for c in range(3):
-                        dz2_bank(k + 1, c)
+            sort_content(7)
+            rope_window(7)
+
+            for k in range(4, TILES - 1):
+                dz2_bank(k + 1, 0)
+                dz2_bank(k + 1, 1)
+                dz1_passes(k)
+                dz2_bank(k + 1, 2)
                 dz1_transpose(k - 1)
-                if nxt:
-                    stage1(k)
-                    out0(k - 2)
-                else:
-                    for n in range(4):
-                        out0_pass(k - 2, n)
-                    out0_copy(k - 2, 0)
-                    out0_copy(k - 2, 1)
-                    out0_copy(k - 2, 2)
-                    stage1(k)
-                if nxt:
-                    dz2_quant(k + 1, 0, 4)
-                if k + 3 < TILES:
-                    rope_own(k + 3)
-                if nxt:
-                    dz1f_quant(k - 1)
-                    dz2_quant(k + 1, 4, 6)
+                out0(k - 2)
+                dz2_quant(k + 1, 0, 4)
                 if k == 4:
-                    rope_last(7)
+                    rope_own(7)
+                dz1f_quant(k - 1)
+                dz2_quant(k + 1, 4, 6)
+                if k == 4:
+                    rope_finish(7, nc.vector)
                     dz1_interleave(0)
                 if k == 5:
                     x_interleave(0, 0)
@@ -643,13 +582,19 @@ def tile_multilatentattention_pb_v_kernel(tc, x, wd, wu, rope_cos, rope_sin, g, 
                     x_interleave(1, 0)
                     x_quant(0, 1)
                     x_quant(1, 0)
-                if k == 7:
-                    dz1f_quant(k - 1)
-                    out0_copy(k - 2, 3)
-                    x_interleave(1, 1)
+
+            dz1_transpose(6)
+            for n in range(4):
+                out0_pass(5, n)
+            for n in range(3):
+                out0_copy(5, n)
+            dz1_passes(7)
+            dz1f_quant(6)
+            out0_copy(5, 3)
+            x_interleave(1, 1)
             for n in range(4):
                 out0_pass(6, n)
-            out0_copy(6, 0, "v")
+            out0_copy(6, 0, "vector")
             out0_copy(6, 1)
             dz1_interleave(1)
             dz1_transpose(7)
@@ -662,10 +607,10 @@ def tile_multilatentattention_pb_v_kernel(tc, x, wd, wu, rope_cos, rope_sin, g, 
             out0(7)
             x_quant(1, 1)
             for n in (2, 3):
-                x_interleave(n, 0)
-                x_interleave(n, 1)
-                x_quant(n, 0)
-                x_quant(n, 1)
+                for b in range(B):
+                    x_interleave(n, b)
+                for b in range(B):
+                    x_quant(n, b)
             for n in range(4):
-                out1_pair(n, 0)
-                out1_pair(n, 1, "sv" if n == 3 else "ss", n == 3)
+                for h in range(2):
+                    out1_pair(n, h)

@@ -24,7 +24,7 @@ GTILES = S // P
 HF = DH + DR
 KIB = 1024
 COS, SIN = 0, 1
-OWN_HEADS = 6
+OWN_HEADS = 4
 GRAD_SLOTS = 4
 RESULT_SLOTS = 10
 
@@ -507,10 +507,10 @@ def tile_multilatentattention_pb_v_kernel(tc, x, wd, wu, rope_cos, rope_sin, g, 
             rope_window(3)
             wd_quant(0)
             rope_own(3)
-            sort_content(4)
             wd_bank(2)
             wd_bank(3)
             dz1_transpose(0)
+            sort_content(4, "scalar")
             dz1_passes(1, 0, 3)
             wd_bank(4)
             dz2_bank(2, 0)
@@ -533,11 +533,10 @@ def tile_multilatentattention_pb_v_kernel(tc, x, wd, wu, rope_cos, rope_sin, g, 
             dz1f_quant(1)
             dz1_passes(2)
             rope_window(5)
-            dz2_bank(3, 0)
-            dz2_bank(3, 1)
-            out0(1, (0, 1))
-            dz2_bank(3, 2)
+            for c in range(3):
+                dz2_bank(3, c)
             dz1_transpose(2)
+            out0(1, (0, 1))
             for k in range(2):
                 out0(k, (2,))
             wd_quant(3)
@@ -559,17 +558,20 @@ def tile_multilatentattention_pb_v_kernel(tc, x, wd, wu, rope_cos, rope_sin, g, 
             rope_window(7)
 
             for k in range(4, TILES - 1):
-                dz2_bank(k + 1, 0)
-                dz2_bank(k + 1, 1)
-                dz1_passes(k)
-                dz2_bank(k + 1, 2)
+                for c in range(3):
+                    dz2_bank(k + 1, c)
                 dz1_transpose(k - 1)
-                out0(k - 2)
+                dz1_passes(k)
+                for n in range(4):
+                    out0_pass(k - 2, n)
+                for n in range(3):
+                    out0_copy(k - 2, n)
                 dz2_quant(k + 1, 0, 4)
                 if k == 4:
                     rope_own(7)
                 dz1f_quant(k - 1)
                 dz2_quant(k + 1, 4, 6)
+                out0_copy(k - 2, 3, "vector" if k == 5 else "scalar")
                 if k == 4:
                     rope_finish(7, nc.vector)
                     dz1_interleave(0)

@@ -39,23 +39,22 @@ def tile_multilatentattention_pb_v_kernel(tc, x, wd, wu, rope_cos, rope_sin, g, 
     cos_view = rope_cos.rearrange("(p j) r -> p j r", j=4)
     sin_view = rope_sin.rearrange("(p j) r -> p j r", j=4)
     out0_view = out_0.rearrange("b (p j) d -> b p j d", j=4)
-    out1_view = out_1.rearrange("(n h p i) l -> p n h i l", h=2, p=P, i=2)
+    out1_view = out_1.rearrange("(n p i) l -> p n i l", p=P, i=2)
 
     with ExitStack() as ctx:
         keep = ctx.enter_context(tc.tile_pool(name="keep", bufs=1))
         arena = ctx.enter_context(tc.tile_pool(name="arena", bufs=1))
         work = ctx.enter_context(tc.tile_pool(name="work", bufs=2))
-        psum = ctx.enter_context(tc.psum_pool(name="psum", bufs=7))
-        psum_keep = ctx.enter_context(tc.psum_pool(name="psum_keep", bufs=1))
+        psum = ctx.enter_context(tc.psum_pool(name="psum", bufs=1))
 
         ident = keep.tile([P, P], F32, name="ident", align_bytes=64)
         ident_first = keep.tile([P, P], F32, name="ident_first", align_bytes=64)
         make_identity(nc, ident_first[:])
 
-        tables = keep.tile([P, 4, 2, DR], F32, name="tables", align_bytes=64)
-        tables_sorted = arena.tile([P, 4, 2, DR], F32, name="tables_sorted", offset=64 * KIB, align_bytes=64)
+        tables = keep.tile([P, 2, 4, DR], F32, name="tables", align_bytes=64)
+        tables_sorted = arena.tile([P, 2, 4, DR], F32, name="tables_sorted", offset=64 * KIB, align_bytes=64)
         tables_t = arena.tile([P, 4, P], F32, name="tables_t", offset=66 * KIB, align_bytes=64)
-        tables_psum = psum_keep.tile([P, 4, 2, DR], F32, name="tables_psum")
+        tables_psum = psum.tile([P, 2, 4, DR], F32, name="tables_psum", tag="bank7")
         wu_codes = keep.tile([P, PASSES, DL], U32, name="wu_codes", align_bytes=64)
         wu_scales = keep.tile([P, PASSES, DL], U8, name="wu_scales", align_bytes=64)
         wd_codes = keep.tile([P, D], U32, name="wd_codes", align_bytes=64)
@@ -68,9 +67,9 @@ def tile_multilatentattention_pb_v_kernel(tc, x, wd, wu, rope_cos, rope_sin, g, 
 
             wu_raw, g_raw, wd_raw, x_raw = {}, {}, {}, {}
 
-            def load_tables(lo, hi):
-                nc.sync.dma_start(out=tables[:, lo:hi, COS, :], in_=cos_view[:, lo:hi, :])
-                nc.sync.dma_start(out=tables[:, lo:hi, SIN, :], in_=sin_view[:, lo:hi, :])
+            def load_tables():
+                nc.sync.dma_start(out=tables[:, SIN], in_=sin_view)
+                nc.sync.dma_start(out=tables[:, COS], in_=cos_view)
 
             def load_g(k):
                 t = work.tile([P, H, HF], BF16, name=f"g{k}", tag="g", bufs=GRAD_SLOTS, align_bytes=64)
@@ -104,8 +103,18 @@ def tile_multilatentattention_pb_v_kernel(tc, x, wd, wu, rope_cos, rope_sin, g, 
                 else:
                     nc.scalar.copy(out=out, in_=in_)
 
-            def new_bank():
-                return psum.tile([P, 512], F32, name="bank", tag="bank")
+            free_banks = list(range(7))
+            bank_of = {}
+
+            def new_bank(key):
+                n = free_banks.pop(0)
+                bank_of[key] = (n, psum.tile([P, 512], F32, name=f"bank{n}", tag=f"bank{n}"))
+                return bank_of[key][1]
+
+            def empty_bank(key, engine, out, view):
+                n, bank = bank_of.pop(key)
+                copy(engine, out, view(bank))
+                free_banks.append(n)
 
             def transpose_pairs(bank, rows):
                 for i in range(2):
@@ -114,24 +123,26 @@ def tile_multilatentattention_pb_v_kernel(tc, x, wd, wu, rope_cos, rope_sin, g, 
                         q = 2 * i + u
                         nc.tensor.transpose(bank[:, q * P : (q + 1) * P], words[:, u:256:2], ident[:])
 
-            def tables_negate(lo, hi):
-                nc.scalar.mul(out=tables[:, lo:hi, SIN, 0:32], in_=tables[:, lo:hi, SIN, 0:32], mul=-1.0)
+            def tables_negate():
+                nc.scalar.mul(out=tables[:, SIN, :, 0:32], in_=tables[:, SIN, :, 0:32], mul=-1.0)
 
             def tables_sort():
                 nc.scalar.copy(
-                    out=tables_sorted[:].rearrange("p j a (u m e) -> p (j a) u m e", u=2, e=2),
-                    in_=tables[:].rearrange("p j a (m u e) -> p (j a) u m e", u=2, e=2),
+                    out=tables_sorted[:].rearrange("p a j (u m e) -> p (a j) u m e", u=2, e=2),
+                    in_=tables[:].rearrange("p a j (m u e) -> p (a j) u m e", u=2, e=2),
                 )
 
             def tables_turn():
-                bank = new_bank()
-                for j in range(4):
-                    nc.tensor.transpose(bank[:, j * P : (j + 1) * P], tables_sorted[:, j].rearrange("p a r -> p (a r)"), ident[:])
-                nc.scalar.copy(out=tables_t[:].rearrange("p j c -> p (j c)"), in_=bank[:])
+                bank = new_bank("tables")
+                flat = tables_sorted[:].rearrange("p a j r -> p (a j r)")
+                for q in range(4):
+                    nc.tensor.transpose(bank[:, q * P : (q + 1) * P], flat[:, q * P : (q + 1) * P], ident[:])
+                empty_bank("tables", "scalar", tables_t[:].rearrange("p j c -> p (j c)"), lambda bank: bank[:])
 
             def tables_turn_back():
-                for j in range(4):
-                    nc.tensor.transpose(tables_psum[:, j].rearrange("p a r -> p (a r)"), tables_t[:, j, :], ident[:])
+                flat = tables_psum[:].rearrange("p a j r -> p (a j r)")
+                for q in range(4):
+                    nc.tensor.transpose(flat[:, q * P : (q + 1) * P], tables_t[:, q, :], ident[:])
 
             def rope_part(k, lo, hi):
                 parts = g_raw[k]
@@ -144,7 +155,7 @@ def tile_multilatentattention_pb_v_kernel(tc, x, wd, wu, rope_cos, rope_sin, g, 
                 products[k] = [work.tile([P, H * DR], F32, name=n, tag=n, bufs=2, align_bytes=64) for n in ("pc", "ps")]
 
             def plain_product(k, which, lo, hi):
-                row = tables[:, k, which, :].rearrange("p (a j) -> p a j", a=2).unsqueeze(1).to_broadcast([P, hi - lo, 2, 32])
+                row = tables[:, which, k, :].rearrange("p (a j) -> p a j", a=2).unsqueeze(1).to_broadcast([P, hi - lo, 2, 32])
                 out = products[k][which][:].rearrange("p (h a j) -> p h a j", h=H, a=2)[:, lo:hi]
                 if which == SIN:
                     out = out[:, :, ::-1]
@@ -169,7 +180,7 @@ def tile_multilatentattention_pb_v_kernel(tc, x, wd, wu, rope_cos, rope_sin, g, 
 
             def sorted_product(k, which, u, lo, hi):
                 rope = rope_part(k, lo, hi).rearrange("p h (a m u e) -> p h a m u e", a=2, u=2, e=2)[:, :, :, :, u, :]
-                row = tables_psum[:, k % 4, which, 32 * u : 32 * u + 32].rearrange("p (a m e) -> p a m e", a=2, e=2)
+                row = tables_psum[:, which, k % 4, 32 * u : 32 * u + 32].rearrange("p (a m e) -> p a m e", a=2, e=2)
                 out = products[k][which][:].rearrange("p (u h a m e) -> p u h a m e", u=2, h=H, a=2, e=2)[:, u, lo:hi]
                 if which == SIN:
                     out = out[:, :, ::-1]
@@ -187,36 +198,43 @@ def tile_multilatentattention_pb_v_kernel(tc, x, wd, wu, rope_cos, rope_sin, g, 
                 sorted_product(k, SIN, 1, 0, H)
                 sorted_product(k, SIN, 0, 0, H - 2)
 
-            def rope_finish(k, engine):
+            def rope_finish(k, engine, own=OWN_HEADS):
                 sorted_product(k, SIN, 0, H - 2, H)
-                sorted_sum(engine, k, OWN_HEADS, H)
+                sorted_sum(engine, k, own, H)
 
-            def rope_window(k):
-                rope_finish(k - 1, nc.gpsimd)
+            def rope_window(k, own=OWN_HEADS):
+                rope_finish(k - 1, nc.gpsimd, own)
                 rope_products(k)
 
-            def rope_own(k):
-                sorted_sum(nc.vector, k, 0, OWN_HEADS)
+            def rope_own(k, own=OWN_HEADS):
+                sorted_sum(nc.vector, k, 0, own)
 
             wu_grp = {}
 
-            def wu_bank(r, c):
-                if r % 2 == 0:
+            def wu_turn(r, c):
+                transpose_pairs(new_bank(("wu", r, c)), [wu_raw[r, 2 * c + i] for i in range(2)])
+
+            def wu_copy(r, c, engine="scalar"):
+                if (r // 2, c) not in wu_grp:
                     offset = KIB * (40 + 4 * (3 * (r // 2) + c))
                     wu_grp[r // 2, c] = arena.tile([P, 2, 2, 512], BF16, name=f"wu_grp{r}_{c}", offset=offset, align_bytes=64)
-                bank = new_bank()
-                transpose_pairs(bank, [wu_raw[r, 2 * c + i] for i in range(2)])
-                nc.scalar.copy(
-                    out=wu_grp[r // 2, c][:, :, r % 2, :].bitcast(F32).rearrange("p i (m u) -> p i m u", u=2),
-                    in_=bank[:].rearrange("p (i u m) -> p i m u", i=2, u=2),
+                empty_bank(
+                    ("wu", r, c),
+                    engine,
+                    wu_grp[r // 2, c][:, :, r % 2, :].bitcast(F32).rearrange("p i (m u) -> p i m u", u=2),
+                    lambda bank: bank[:].rearrange("p (i u m) -> p i m u", i=2, u=2),
                 )
+
+            def wu_bank(r, c):
+                wu_turn(r, c)
+                wu_copy(r, c)
 
             def wu_row(r):
                 for c in range(3):
                     wu_bank(r, c)
 
-            def wu_quant(pair):
-                for s in range(PASSES):
+            def wu_quant(pair, lo=0, hi=PASSES):
+                for s in range(lo, hi):
                     nc.vector.quantize_mx(
                         out=wu_codes[:, s, 256 * pair : 256 * pair + 256].bitcast(E4M3),
                         scales=wu_scales[:, s, 256 * pair : 256 * pair + 256],
@@ -225,16 +243,24 @@ def tile_multilatentattention_pb_v_kernel(tc, x, wd, wu, rope_cos, rope_sin, g, 
 
             wd_grp = {}
 
-            def wd_bank(n):
+            def wd_turn(n):
                 c, half = n // 2, n % 2
-                if half == 0:
+                transpose_pairs(new_bank(("wd", n)), [wd_raw[c][:, 2 * half + i, :] for i in range(2)])
+
+            def wd_copy(n, engine="scalar"):
+                c, half = n // 2, n % 2
+                if c not in wd_grp:
                     wd_grp[c] = work.tile([P, 2048], BF16, name="wd_grp", tag="xgrp", bufs=3, align_bytes=64)
-                bank = new_bank()
-                transpose_pairs(bank, [wd_raw[c][:, 2 * half + i, :] for i in range(2)])
-                nc.scalar.copy(
-                    out=wd_grp[c][:].bitcast(F32).rearrange("p (m i u) -> p m i u", i=4, u=2)[:, :, 2 * half : 2 * half + 2, :],
-                    in_=bank[:].rearrange("p (i u m) -> p m i u", i=2, u=2),
+                empty_bank(
+                    ("wd", n),
+                    engine,
+                    wd_grp[c][:].bitcast(F32).rearrange("p (m i u) -> p m i u", i=4, u=2)[:, :, 2 * half : 2 * half + 2, :],
+                    lambda bank: bank[:].rearrange("p (i u m) -> p m i u", i=2, u=2),
                 )
+
+            def wd_bank(n):
+                wd_turn(n)
+                wd_copy(n)
 
             def wd_quant(c):
                 nc.vector.quantize_mx(
@@ -251,10 +277,8 @@ def tile_multilatentattention_pb_v_kernel(tc, x, wd, wu, rope_cos, rope_sin, g, 
 
             dz2_grp = {}
 
-            def dz2_bank(k, c):
-                if c == 0:
-                    dz2_grp[k] = work.tile([P, J], BF16, name="dz2_grp", tag="dz2g", bufs=2, align_bytes=64)
-                bank = new_bank()
+            def dz2_turn(k, c):
+                bank = new_bank(("dz2", k, c))
                 if k in g_sorted:
                     words = g_sorted[k][:].rearrange("p u h m -> p u (h m)")
                     for i in range(2):
@@ -263,15 +287,25 @@ def tile_multilatentattention_pb_v_kernel(tc, x, wd, wu, rope_cos, rope_sin, g, 
                             nc.tensor.transpose(bank[:, q * P : (q + 1) * P], words[:, u, P * s : P * s + P], ident[:])
                 else:
                     transpose_pairs(bank, [g_pass(k, 2 * c + i) for i in range(2)])
-                nc.scalar.copy(
-                    out=dz2_grp[k][:, 1024 * c : 1024 * c + 1024].bitcast(F32).rearrange("p (i r u) -> p i r u", i=2, u=2),
-                    in_=bank[:].rearrange("p (i u r) -> p i r u", i=2, u=2),
+
+            def dz2_copy(k, c, engine="scalar"):
+                if k not in dz2_grp:
+                    dz2_grp[k] = work.tile([P, J], BF16, name="dz2_grp", tag="dz2g", bufs=2, align_bytes=64)
+                empty_bank(
+                    ("dz2", k, c),
+                    engine,
+                    dz2_grp[k][:, 1024 * c : 1024 * c + 1024].bitcast(F32).rearrange("p (i r u) -> p i r u", i=2, u=2),
+                    lambda bank: bank[:].rearrange("p (i u r) -> p i r u", i=2, u=2),
                 )
+
+            def dz2_bank(k, c, engine="scalar"):
+                dz2_turn(k, c)
+                dz2_copy(k, c, engine)
 
             dz2 = {}
 
             def dz2_quant(k, lo, hi):
-                if lo == 0:
+                if k not in dz2:
                     codes = work.tile([P, PASSES, P], U32, name="dz2_codes", tag="dz2c", bufs=3, align_bytes=64)
                     scales = work.tile([P, PASSES, P], U8, name="dz2_scales", tag="dz2s", bufs=3, align_bytes=64)
                     dz2[k] = (codes, scales)
@@ -285,46 +319,57 @@ def tile_multilatentattention_pb_v_kernel(tc, x, wd, wu, rope_cos, rope_sin, g, 
             dz1_tok = {}
             dz1_acc = {}
 
-            def dz1_passes(k, lo=0, hi=PASSES):
+            def dz1_passes(k, lo=0, hi=PASSES, cols=slice(0, DL)):
                 codes, scales = dz2[k]
-                if lo == 0:
-                    dz1_acc[k] = new_bank()
+                if k not in dz1_acc:
+                    dz1_acc[k] = new_bank(("dz1", k))
                 for s in range(lo, hi):
                     nc.tensor.matmul_mx(
-                        out=dz1_acc[k][:],
+                        out=dz1_acc[k][:, cols],
                         lhsT=codes[:, s, :].bitcast(E5M2),
                         lhsT_scale=scales[:, s, :],
-                        rhs=wu_codes[:, s, :].bitcast(E4M3),
-                        rhs_scale=wu_scales[:, s, :],
+                        rhs=wu_codes[:, s, cols].bitcast(E4M3),
+                        rhs_scale=wu_scales[:, s, cols],
                         start=(s == 0),
                         stop=(s == PASSES - 1),
                     )
-                if hi == PASSES:
-                    if k % GTILES == 0:
-                        dz1_tok[k // GTILES] = work.tile([P, GTILES, DL], BF16, name="dz1_tok", tag="dz1t", bufs=2, align_bytes=64)
-                    nc.scalar.copy(
-                        out=dz1_tok[k // GTILES][:, k % GTILES, :].rearrange("p (u m e) -> p u m e", u=2, e=2),
-                        in_=dz1_acc[k][:].rearrange("p (u e m) -> p u m e", u=2, e=2),
-                    )
+
+            def dz1_copy(k, engine="scalar"):
+                if k % GTILES == 0:
+                    dz1_tok[k // GTILES] = work.tile([P, GTILES, DL], BF16, name="dz1_tok", tag="dz1t", bufs=2, align_bytes=64)
+                empty_bank(
+                    ("dz1", k),
+                    engine,
+                    dz1_tok[k // GTILES][:, k % GTILES, :].rearrange("p (u m e) -> p u m e", u=2, e=2),
+                    lambda bank: bank[:].rearrange("p (u e m) -> p u m e", u=2, e=2),
+                )
 
             dz1f_grp = {}
 
-            def dz1_transpose(k):
+            def dz1_turn(k):
                 words = dz1_tok[k // GTILES][:, k % GTILES, :].bitcast(F32)
-                bank = new_bank()
+                bank = new_bank(("dz1f", k))
                 for u in range(2):
                     nc.tensor.transpose(bank[:, u * P : (u + 1) * P], words[:, u * P : (u + 1) * P], ident[:])
+
+            def dz1f_copy(k, engine="scalar"):
                 dz1f_grp[k] = work.tile([P, DL], BF16, name="dz1f_grp", tag="dz1fg", bufs=2, align_bytes=64)
-                nc.scalar.copy(
-                    out=dz1f_grp[k][:].bitcast(F32).rearrange("p (r u) -> p r u", u=2),
-                    in_=bank[:, : 2 * P].rearrange("p (u r) -> p r u", u=2),
+                empty_bank(
+                    ("dz1f", k),
+                    engine,
+                    dz1f_grp[k][:].bitcast(F32).rearrange("p (r u) -> p r u", u=2),
+                    lambda bank: bank[:, : 2 * P].rearrange("p (u r) -> p r u", u=2),
                 )
+
+            def dz1_transpose(k):
+                dz1_turn(k)
+                dz1f_copy(k)
 
             dz1f = {}
 
             def dz1f_quant(k):
-                codes = work.tile([P, P], U32, name="dz1f_codes", tag="dz1fc", bufs=3, align_bytes=64)
-                scales = work.tile([P, P], U8, name="dz1f_scales", tag="dz1fs", bufs=3, align_bytes=64)
+                codes = work.tile([P, P], U32, name="dz1f_codes", tag="dz1fc", bufs=5, align_bytes=64)
+                scales = work.tile([P, P], U8, name="dz1f_scales", tag="dz1fs", bufs=5, align_bytes=64)
                 nc.vector.quantize_mx(out=codes[:].bitcast(E5M2), scales=scales[:], in_=dz1f_grp[k][:])
                 dz1f[k] = (codes, scales)
 
@@ -336,13 +381,10 @@ def tile_multilatentattention_pb_v_kernel(tc, x, wd, wu, rope_cos, rope_sin, g, 
                 results.append(t)
                 return t
 
-            out0_acc = {}
-
             def out0_pass(k, n):
                 codes, scales = dz1f[k]
-                out0_acc[k, n] = new_bank()
                 nc.tensor.matmul_mx(
-                    out=out0_acc[k, n][:],
+                    out=new_bank(("out0", k, n))[:],
                     lhsT=codes[:].bitcast(E5M2),
                     lhsT_scale=scales[:],
                     rhs=wd_codes[:, 512 * n : 512 * n + 512].bitcast(E4M3),
@@ -358,7 +400,7 @@ def tile_multilatentattention_pb_v_kernel(tc, x, wd, wu, rope_cos, rope_sin, g, 
                 if i == 0:
                     out0_res[k, half] = new_result()
                 res = out0_res[k, half]
-                copy(engine, res[:, i, :], out0_acc[k, n][:])
+                empty_bank(("out0", k, n), engine, res[:, i, :], lambda bank: bank[:])
                 if i == 1:
                     nc.sync.dma_start(
                         out=out0_view[k // GTILES][:, k % GTILES, 1024 * half : 1024 * half + 1024],
@@ -389,230 +431,262 @@ def tile_multilatentattention_pb_v_kernel(tc, x, wd, wu, rope_cos, rope_sin, g, 
                 dz1[b] = (codes, scales)
 
             x_grp = {}
+            x_first = {}
 
-            def x_interleave(n, b):
-                x_grp[n, b] = work.tile([P, 512, 4], BF16, name="x_grp", tag="xgrp", bufs=3, align_bytes=64)
-                nc.vector.tensor_copy(
-                    out=x_grp[n, b][:].rearrange("p (i g l) t -> p g t l i", i=2, l=4),
-                    in_=x_raw[b][:, :, 512 * n : 512 * n + 512].rearrange("p t (g l i) -> p g t l i", i=2, l=4),
+            def x_interleave(lo, hi, b, engine="vector"):
+                x_grp[lo, b] = work.tile([P, 256 * (hi - lo), 4], BF16, name="x_grp", tag="xgrp", bufs=3, align_bytes=64)
+                copy(
+                    engine,
+                    x_grp[lo, b][:].rearrange("p (i g l) t -> p g t l i", i=2, l=4),
+                    x_raw[b][:, :, 256 * lo : 256 * hi].rearrange("p t (g l i) -> p g t l i", i=2, l=4),
                 )
+                for n in range(lo, hi):
+                    for i in range(2):
+                        x_first[n, i] = 256 * lo + P * ((hi - lo) * i + n - lo)
 
-            def x_quant(n, b):
+            def x_quant(lo, hi, b):
                 nc.vector.quantize_mx(
-                    out=x_codes[:, b, 512 * n : 512 * n + 512].bitcast(E4M3),
-                    scales=x_scales[:, b, 512 * n : 512 * n + 512],
-                    in_=x_grp[n, b][:].rearrange("p c t -> p (c t)"),
+                    out=x_codes[:, b, 256 * lo : 256 * hi].bitcast(E4M3),
+                    scales=x_scales[:, b, 256 * lo : 256 * hi],
+                    in_=x_grp[lo, b][:].rearrange("p c t -> p (c t)"),
                 )
 
             out1_acc = {}
 
-            def out1_pass(n, h, i, b):
-                a = 4 * n + 2 * i + h
+            def out1_pass(n, i, b):
+                a = 2 * n + i
                 if b == 0:
-                    out1_acc[a] = new_bank()
+                    out1_acc[a] = new_bank(("out1", a))
                 codes, scales = dz1[b]
+                cols = slice(x_first[n, i], x_first[n, i] + P)
                 nc.tensor.matmul_mx(
                     out=out1_acc[a][:],
-                    lhsT=x_codes[:, b, P * a : P * a + P].bitcast(E4M3),
-                    lhsT_scale=x_scales[:, b, P * a : P * a + P],
+                    lhsT=x_codes[:, b, cols].bitcast(E4M3),
+                    lhsT_scale=x_scales[:, b, cols],
                     rhs=codes[:].bitcast(E5M2),
                     rhs_scale=scales[:],
                     start=(b == 0),
                     stop=(b == B - 1),
                 )
 
-            def out1_pair(n, h):
-                last = (n, h) == (3, 1)
-                res = new_result()
-                for i in range(2):
-                    a = 4 * n + 2 * i + h
-                    if a not in out1_acc:
-                        out1_pass(n, h, i, 0)
-                    out1_pass(n, h, i, 1)
-                    copy(
-                        "vector" if last and i == 1 else "scalar",
-                        res[:, i, :].rearrange("p (m u e) -> p m u e", u=2, e=2),
-                        out1_acc[a][:].rearrange("p (u m e) -> p m u e", u=2, e=2),
-                    )
-                    if last:
-                        nc.sync.dma_start(out=out1_view[:, n, h, i], in_=res[:, i])
-                if not last:
-                    nc.sync.dma_start(out=out1_view[:, n, h], in_=res[:])
+            out1_res = {}
 
-            load_wu(0, 0, 2)
-            load_tables(0, 1)
+            def out1_copy(n, i, engine="scalar", alone=False):
+                if n not in out1_res:
+                    out1_res[n] = new_result()
+                res = out1_res[n]
+                empty_bank(
+                    ("out1", 2 * n + i),
+                    engine,
+                    res[:, i, :].rearrange("p (m u e) -> p m u e", u=2, e=2),
+                    lambda bank: bank[:].rearrange("p (u m e) -> p m u e", u=2, e=2),
+                )
+                if alone:
+                    nc.sync.dma_start(out=out1_view[:, n, i], in_=res[:, i])
+                elif i == 1:
+                    nc.sync.dma_start(out=out1_view[:, n], in_=res[:])
+
+            def out1_bank(n, i, engine="scalar", alone=False):
+                if 2 * n + i not in out1_acc:
+                    out1_pass(n, i, 0)
+                out1_pass(n, i, 1)
+                out1_copy(n, i, engine, alone)
+
+            load_tables()
             load_first_g(0)
+            load_wu(0, 0, 2)
             load_first_g(1)
             load_wu(0, 2, PASSES)
-            load_tables(1, 4)
             load_g(1)
-            for r in range(1, 4):
-                load_wu(r)
+            load_wu(1)
+            load_wu(2)
             load_g(2)
+            load_wu(3)
             load_wd(0)
             load_g(3)
             load_wd(1)
-            load_wd(2)
             load_g(4)
+            load_wd(2)
+            load_g(5)
             load_wd(3)
-            for k in range(5, TILES):
-                load_g(k)
-
-            tables_negate(0, 1)
-            wu_bank(0, 0)
-            new_products(0)
-            plain_product(0, COS, 0, 8)
-            plain_product(0, SIN, 0, 8)
-            plain_product(0, COS, 8, H)
-            plain_sum(0, 0, 8)
-            plain_product(0, SIN, 8, H)
-            tables_negate(1, 4)
+            load_g(6)
+            load_g(7)
+            tables_negate()
             tables_sort()
+            new_products(0)
+            plain_product(0, SIN, 0, 8)
+            plain_product(0, COS, 0, 8)
+            plain_sum(0, 0, 8)
+            plain_product(0, COS, 8, H)
+            plain_product(0, SIN, 8, H)
+            tables_turn()
+            wu_bank(0, 0)
+            plain_sum(0, 8, H)
+            tables_turn_back()
+            dz2_bank(0, 0)
             wu_bank(0, 1)
             wu_bank(0, 2)
-            dz2_bank(0, 0)
-            plain_sum(0, 8, H)
+            rope_products(1)
             dz2_bank(0, 1)
-            tables_turn()
             dz2_bank(0, 2)
-            new_products(1)
-            plain_product(1, COS, 0, H)
-            plain_product(1, SIN, 0, H)
+            sort_content(1, "scalar")
+            wu_row(1)
             dz2_quant(0, 0, 4)
-            plain_sum(1, 0, H)
+            rope_own(1)
             dz2_quant(0, 4, 6)
-            wu_bank(1, 0)
-            wu_bank(1, 1)
-            tables_turn_back()
-            wu_bank(1, 2)
-            wu_quant(0)
-            wu_row(2)
+            wu_quant(0, 0, 4)
+            wu_bank(2, 0)
+            wu_bank(2, 1)
+            rope_window(2)
+            sort_content(2, "scalar")
+            wu_bank(2, 2)
+            wu_quant(0, 4, 6)
+            rope_own(2)
             wu_row(3)
-            sort_content(2)
+            dz1_passes(0, cols=slice(0, 256))
+            sort_content(3, "scalar")
             wu_quant(1)
             for b in range(B):
                 load_x(b)
             for c in range(3):
                 dz2_bank(1, c)
-            sort_content(3, "scalar")
-            rope_products(2)
-            dz2_quant(1, 0, 4)
-            rope_own(2)
-            dz2_quant(1, 4, 6)
-
-            dz1_passes(0, 0, 3)
             wd_bank(0)
-            wd_bank(1)
-            dz1_passes(0, 3, 6)
             rope_window(3)
-            wd_quant(0)
+            dz1_passes(0, cols=slice(256, 512))
+            dz2_quant(1, 0, 4)
+            dz2_quant(1, 4, 6)
+            rope_window(4)
+            wd_bank(1)
+            dz1_copy(0)
+            for c in range(3):
+                dz2_bank(2, c)
             rope_own(3)
-            wd_bank(2)
-            wd_bank(3)
+            wd_quant(0)
             dz1_transpose(0)
             sort_content(4, "scalar")
-            dz1_passes(1, 0, 3)
-            wd_bank(4)
-            dz2_bank(2, 0)
-            dz2_bank(2, 1)
-            dz1_passes(1, 3, 6)
-            wd_quant(1)
-            dz1f_quant(0)
-            rope_window(4)
-            dz2_bank(2, 2)
-            wd_bank(5)
-            dz1_transpose(1)
-            out0(0, (0, 1))
-            wd_bank(6)
-            wd_bank(7)
+            dz1_passes(1)
+            dz1_copy(1)
+            sort_content(5)
             dz2_quant(2, 0, 4)
             dz2_quant(2, 4, 6)
-            rope_own(4)
-            sort_content(5)
-            wd_quant(2)
-            dz1f_quant(1)
+            dz1f_quant(0)
+            wd_bank(2)
+            wd_bank(3)
+            for c in range(3):
+                dz2_turn(3, c)
+            dz2_copy(3, 0)
+            dz2_copy(3, 1)
+            rope_window(5, 0)
+            dz2_copy(3, 2, "vector")
+            dz1_transpose(1)
+            out0(0, (0,))
             dz1_passes(2)
-            rope_window(5)
-            for c in range(3):
-                dz2_bank(3, c)
-            dz1_transpose(2)
-            out0(1, (0, 1))
-            for k in range(2):
-                out0(k, (2,))
-            wd_quant(3)
+            dz1_copy(2)
+            wd_quant(1)
             dz2_quant(3, 0, 4)
-            rope_own(5)
-            sort_content(6)
             dz2_quant(3, 4, 6)
-            rope_window(6)
+            dz1f_quant(1)
+            wd_bank(4)
+            wd_bank(5)
             for c in range(3):
-                dz2_bank(4, c)
+                dz2_turn(4, c)
+            dz2_copy(4, 0)
+            dz2_copy(4, 1)
+            rope_window(6, 0)
+            dz2_copy(4, 2, "vector")
+            dz1_transpose(2)
+            out0(0, (1,))
+            out0(1, (0, 1))
             dz1_passes(3)
-            for k in range(2):
-                out0(k, (3,))
+            dz1_copy(3)
+            wd_quant(2)
             dz1f_quant(2)
+            sort_content(6)
             dz2_quant(4, 0, 4)
-            rope_own(6)
             dz2_quant(4, 4, 6)
+            wd_bank(6)
+            wd_bank(7)
+            for c in range(3):
+                dz2_turn(5, c)
+            dz2_copy(5, 0)
+            dz2_copy(5, 1)
+            rope_window(7, 0)
+            dz2_copy(5, 2, "vector")
+            dz1_transpose(3)
+            out0(2, (0, 1))
+            out0(0, (2,))
+            out0(1, (2,))
+            dz1_passes(4)
+            dz1_copy(4)
+            wd_quant(3)
+            dz1f_quant(3)
             sort_content(7)
-            rope_window(7)
-
-            for k in range(4, TILES - 1):
-                for c in range(3):
-                    dz2_bank(k + 1, c)
-                dz1_transpose(k - 1)
-                dz1_passes(k)
-                for n in range(4):
-                    out0_pass(k - 2, n)
-                for n in range(3):
-                    out0_copy(k - 2, n)
-                dz2_quant(k + 1, 0, 4)
-                if k == 4:
-                    rope_own(7)
-                dz1f_quant(k - 1)
-                dz2_quant(k + 1, 4, 6)
-                out0_copy(k - 2, 3, "vector" if k == 5 else "scalar")
-                if k == 4:
-                    rope_finish(7, nc.vector)
-                    dz1_interleave(0)
-                if k == 5:
-                    x_interleave(0, 0)
-                    dz1_quant(0)
-                    x_quant(0, 0)
-                    x_interleave(0, 1)
-                if k == 6:
-                    x_interleave(1, 0)
-                    x_quant(0, 1)
-                    x_quant(1, 0)
-
-            dz1_transpose(6)
+            dz2_quant(5, 0, 4)
+            dz2_quant(5, 4, 6)
+            rope_finish(7, nc.vector, 0)
+            free_banks.append(7)
+            for c in range(3):
+                dz2_bank(6, c)
+            dz1_transpose(4)
+            out0(0, (3,))
+            out0(1, (3,))
+            out0(2, (2, 3))
+            dz1_passes(5)
+            dz1_copy(5)
+            dz1_interleave(0)
+            dz1f_quant(4)
+            dz2_quant(6, 0, 4)
+            dz2_quant(6, 4, 6)
+            x_interleave(0, 2, 0)
+            for c in range(3):
+                dz2_bank(7, c)
+            dz1_turn(5)
+            dz1f_copy(5, "vector")
+            dz1_quant(0)
             for n in range(4):
-                out0_pass(5, n)
-            for n in range(3):
-                out0_copy(5, n)
-            dz1_passes(7)
+                out0_pass(3, n)
+                out0_copy(3, n, "vector" if n == 3 else "scalar")
+            dz1_passes(6)
+            dz1_copy(6)
+            dz1f_quant(5)
+            dz2_quant(7, 0, 4)
+            x_quant(0, 2, 0)
+            dz2_quant(7, 4, 6)
+            x_interleave(0, 2, 1)
+            out0(4)
+            dz1_turn(6)
+            dz1f_copy(6, "vector")
+            x_quant(0, 2, 1)
             dz1f_quant(6)
-            out0_copy(5, 3)
-            x_interleave(1, 1)
-            for n in range(4):
+            out0(5, (0, 1))
+            dz1_passes(7)
+            dz1_copy(7)
+            x_interleave(2, 4, 0)
+            out0(5, (2, 3))
+            for n in range(2):
                 out0_pass(6, n)
-            out0_copy(6, 0, "vector")
-            out0_copy(6, 1)
             dz1_interleave(1)
             dz1_transpose(7)
-            out0_copy(6, 2)
-            out0_copy(6, 3)
+            for n in range(2):
+                out0_copy(6, n)
+            out0(6, (2, 3))
             dz1f_quant(7)
+            x_quant(2, 4, 0)
             dz1_quant(1)
             for i in range(2):
-                out1_pass(0, 0, i, 0)
+                out1_pass(0, i, 0)
             out0(7)
-            x_quant(1, 1)
-            for n in (2, 3):
+            x_interleave(2, 4, 1)
+            x_interleave(4, 6, 0)
+            x_quant(2, 4, 1)
+            x_interleave(4, 6, 1)
+            x_quant(4, 6, 0)
+            x_quant(4, 6, 1)
+            for n in (6, 7):
                 for b in range(B):
-                    x_interleave(n, b)
+                    x_interleave(n, n + 1, b)
                 for b in range(B):
-                    x_quant(n, b)
-            for n in range(4):
-                for h in range(2):
-                    out1_pair(n, h)
+                    x_quant(n, n + 1, b)
+            for n in range(8):
+                for i in range(2):
+                    out1_bank(n, i, "vector" if n == 7 and i == 1 else "scalar", n == 7)

@@ -26,6 +26,8 @@ KIB = 1024
 COS, SIN = 0, 1
 OWN_HEADS = 4
 GRAD_SLOTS = 4
+WHOLE_FROM = 8
+X_PIECES = ((0, 4), (512, 4), (1024, 4), (1536, 2), (1792, 1), (1920, 1))
 RESULT_SLOTS = 10
 
 
@@ -39,7 +41,6 @@ def tile_multilatentattention_pb_v_kernel(tc, x, wd, wu, rope_cos, rope_sin, g, 
     cos_view = rope_cos.rearrange("(p j) r -> p j r", j=4)
     sin_view = rope_sin.rearrange("(p j) r -> p j r", j=4)
     out0_view = out_0.rearrange("b (p j) d -> b p j d", j=4)
-    out1_view = out_1.rearrange("(n p i) l -> p n i l", p=P, i=2)
 
     with ExitStack() as ctx:
         keep = ctx.enter_context(tc.tile_pool(name="keep", bufs=1))
@@ -375,10 +376,12 @@ def tile_multilatentattention_pb_v_kernel(tc, x, wd, wu, rope_cos, rope_sin, g, 
 
             results = []
 
-            def new_result():
+            def new_result(banks):
+                if banks == 4 and len(results) % 2 == 1:
+                    results.append(None)
                 slot = len(results) % RESULT_SLOTS
-                t = arena.tile([P, 2, 512], F32, name=f"res{len(results)}", offset=4 * KIB * slot, align_bytes=64)
-                results.append(t)
+                t = arena.tile([P, banks, 512], F32, name=f"res{len(results)}", offset=4 * KIB * slot, align_bytes=64)
+                results.extend([t] * ((banks + 1) // 2))
                 return t
 
             def out0_pass(k, n):
@@ -396,14 +399,15 @@ def tile_multilatentattention_pb_v_kernel(tc, x, wd, wu, rope_cos, rope_sin, g, 
             out0_res = {}
 
             def out0_copy(k, n, engine="scalar"):
-                half, i = n // 2, n % 2
-                if i == 0:
-                    out0_res[k, half] = new_result()
-                res = out0_res[k, half]
+                banks = 4 if k >= WHOLE_FROM else 2
+                part, i = divmod(n, banks)
+                if (k, part) not in out0_res:
+                    out0_res[k, part] = new_result(banks)
+                res = out0_res[k, part]
                 empty_bank(("out0", k, n), engine, res[:, i, :], lambda bank: bank[:])
-                if i == 1:
+                if i == banks - 1:
                     nc.sync.dma_start(
-                        out=out0_view[k // GTILES][:, k % GTILES, 1024 * half : 1024 * half + 1024],
+                        out=out0_view[k // GTILES][:, k % GTILES, 512 * banks * part : 512 * banks * (part + 1)],
                         in_=res[:].rearrange("p i c -> p (i c)"),
                     )
 
@@ -431,38 +435,35 @@ def tile_multilatentattention_pb_v_kernel(tc, x, wd, wu, rope_cos, rope_sin, g, 
                 dz1[b] = (codes, scales)
 
             x_grp = {}
-            x_first = {}
 
-            def x_interleave(lo, hi, b, engine="vector"):
-                x_grp[lo, b] = work.tile([P, 256 * (hi - lo), 4], BF16, name="x_grp", tag="xgrp", bufs=3, align_bytes=64)
+            def x_interleave(piece, b, engine="vector"):
+                first, rows = X_PIECES[piece]
+                x_grp[piece, b] = work.tile([P, P * rows, 4], BF16, name="x_grp", tag="xgrp", bufs=3, align_bytes=64)
                 copy(
                     engine,
-                    x_grp[lo, b][:].rearrange("p (i g l) t -> p g t l i", i=2, l=4),
-                    x_raw[b][:, :, 256 * lo : 256 * hi].rearrange("p t (g l i) -> p g t l i", i=2, l=4),
+                    x_grp[piece, b][:].rearrange("p (i g l) t -> p g t l i", i=rows, l=8 // rows),
+                    x_raw[b][:, :, first : first + P * rows].rearrange("p t (g l i) -> p g t l i", i=rows, l=8 // rows),
                 )
-                for n in range(lo, hi):
-                    for i in range(2):
-                        x_first[n, i] = 256 * lo + P * ((hi - lo) * i + n - lo)
 
-            def x_quant(lo, hi, b):
+            def x_quant(piece, b):
+                first, rows = X_PIECES[piece]
                 nc.vector.quantize_mx(
-                    out=x_codes[:, b, 256 * lo : 256 * hi].bitcast(E4M3),
-                    scales=x_scales[:, b, 256 * lo : 256 * hi],
-                    in_=x_grp[lo, b][:].rearrange("p c t -> p (c t)"),
+                    out=x_codes[:, b, first : first + P * rows].bitcast(E4M3),
+                    scales=x_scales[:, b, first : first + P * rows],
+                    in_=x_grp[piece, b][:].rearrange("p c t -> p (c t)"),
                 )
 
             out1_acc = {}
 
-            def out1_pass(n, i, b):
-                a = 2 * n + i
+            def out1_pass(piece, i, b):
                 if b == 0:
-                    out1_acc[a] = new_bank(("out1", a))
+                    out1_acc[piece, i] = new_bank(("out1", piece, i))
                 codes, scales = dz1[b]
-                cols = slice(x_first[n, i], x_first[n, i] + P)
+                first = X_PIECES[piece][0] + P * i
                 nc.tensor.matmul_mx(
-                    out=out1_acc[a][:],
-                    lhsT=x_codes[:, b, cols].bitcast(E4M3),
-                    lhsT_scale=x_scales[:, b, cols],
+                    out=out1_acc[piece, i][:],
+                    lhsT=x_codes[:, b, first : first + P].bitcast(E4M3),
+                    lhsT_scale=x_scales[:, b, first : first + P],
                     rhs=codes[:].bitcast(E5M2),
                     rhs_scale=scales[:],
                     start=(b == 0),
@@ -471,26 +472,27 @@ def tile_multilatentattention_pb_v_kernel(tc, x, wd, wu, rope_cos, rope_sin, g, 
 
             out1_res = {}
 
-            def out1_copy(n, i, engine="scalar", alone=False):
-                if n not in out1_res:
-                    out1_res[n] = new_result()
-                res = out1_res[n]
+            def out1_copy(piece, i, engine="scalar", store=None):
+                first, rows = X_PIECES[piece]
+                store = store or rows
+                if piece not in out1_res:
+                    out1_res[piece] = new_result(rows)
+                res = out1_res[piece]
                 empty_bank(
-                    ("out1", 2 * n + i),
+                    ("out1", piece, i),
                     engine,
                     res[:, i, :].rearrange("p (m u e) -> p m u e", u=2, e=2),
                     lambda bank: bank[:].rearrange("p (u m e) -> p m u e", u=2, e=2),
                 )
-                if alone:
-                    nc.sync.dma_start(out=out1_view[:, n, i], in_=res[:, i])
-                elif i == 1:
-                    nc.sync.dma_start(out=out1_view[:, n], in_=res[:])
+                if (i + 1) % store == 0:
+                    view = out_1[first : first + P * rows].rearrange("(p i) l -> p i l", i=rows)
+                    nc.sync.dma_start(out=view[:, i + 1 - store : i + 1], in_=res[:, i + 1 - store : i + 1])
 
-            def out1_bank(n, i, engine="scalar", alone=False):
-                if 2 * n + i not in out1_acc:
-                    out1_pass(n, i, 0)
-                out1_pass(n, i, 1)
-                out1_copy(n, i, engine, alone)
+            def out1_bank(piece, i, engine="scalar", store=None):
+                if (piece, i) not in out1_acc:
+                    out1_pass(piece, i, 0)
+                out1_pass(piece, i, 1)
+                out1_copy(piece, i, engine, store)
 
             load_tables()
             load_first_g(0)
@@ -534,60 +536,60 @@ def tile_multilatentattention_pb_v_kernel(tc, x, wd, wu, rope_cos, rope_sin, g, 
             dz2_quant(0, 0, 4)
             rope_own(1)
             dz2_quant(0, 4, 6)
-            wu_quant(0, 0, 4)
-            wu_bank(2, 0)
-            wu_bank(2, 1)
+            wu_quant(0)
+            wu_row(2)
             rope_window(2)
             sort_content(2, "scalar")
-            wu_bank(2, 2)
-            wu_quant(0, 4, 6)
             rope_own(2)
-            wu_row(3)
             dz1_passes(0, cols=slice(0, 256))
-            sort_content(3, "scalar")
+            wu_row(3)
             wu_quant(1)
             for b in range(B):
                 load_x(b)
             for c in range(3):
                 dz2_bank(1, c)
             wd_bank(0)
-            rope_window(3)
             dz1_passes(0, cols=slice(256, 512))
+            sort_content(3, "scalar")
             dz2_quant(1, 0, 4)
             dz2_quant(1, 4, 6)
-            rope_window(4)
+            rope_window(3)
             wd_bank(1)
             dz1_copy(0)
+            dz1_passes(1, 0, 3)
+            wd_bank(2)
+            wd_bank(3)
+            rope_window(4)
             for c in range(3):
                 dz2_bank(2, c)
+            dz1_passes(1, 3, 6)
+            dz1_transpose(0)
+            dz1_copy(1)
             rope_own(3)
             wd_quant(0)
-            dz1_transpose(0)
-            sort_content(4, "scalar")
-            dz1_passes(1)
-            dz1_copy(1)
-            sort_content(5)
             dz2_quant(2, 0, 4)
             dz2_quant(2, 4, 6)
             dz1f_quant(0)
-            wd_bank(2)
-            wd_bank(3)
+            wd_turn(4)
+            sort_content(4, "scalar")
+            wd_copy(4)
             for c in range(3):
                 dz2_turn(3, c)
             dz2_copy(3, 0)
             dz2_copy(3, 1)
+            wd_quant(1)
             rope_window(5, 0)
             dz2_copy(3, 2, "vector")
-            dz1_transpose(1)
-            out0(0, (0,))
             dz1_passes(2)
             dz1_copy(2)
-            wd_quant(1)
+            dz1_transpose(1)
+            sort_content(5)
+            dz1f_quant(1)
             dz2_quant(3, 0, 4)
             dz2_quant(3, 4, 6)
-            dz1f_quant(1)
-            wd_bank(4)
             wd_bank(5)
+            wd_bank(6)
+            out0(0, (0, 1))
             for c in range(3):
                 dz2_turn(4, c)
             dz2_copy(4, 0)
@@ -595,17 +597,15 @@ def tile_multilatentattention_pb_v_kernel(tc, x, wd, wu, rope_cos, rope_sin, g, 
             rope_window(6, 0)
             dz2_copy(4, 2, "vector")
             dz1_transpose(2)
-            out0(0, (1,))
-            out0(1, (0, 1))
             dz1_passes(3)
+            sort_content(6, "scalar")
             dz1_copy(3)
             wd_quant(2)
             dz1f_quant(2)
-            sort_content(6)
             dz2_quant(4, 0, 4)
             dz2_quant(4, 4, 6)
-            wd_bank(6)
             wd_bank(7)
+            out0(1, (0, 1))
             for c in range(3):
                 dz2_turn(5, c)
             dz2_copy(5, 0)
@@ -618,17 +618,21 @@ def tile_multilatentattention_pb_v_kernel(tc, x, wd, wu, rope_cos, rope_sin, g, 
             out0(1, (2,))
             dz1_passes(4)
             dz1_copy(4)
+            sort_content(7, "scalar")
             wd_quant(3)
             dz1f_quant(3)
-            sort_content(7)
             dz2_quant(5, 0, 4)
             dz2_quant(5, 4, 6)
-            rope_finish(7, nc.vector, 0)
+            for c in range(3):
+                dz2_turn(6, c)
+            rope_finish(7, nc.gpsimd, 0)
             free_banks.append(7)
             for c in range(3):
-                dz2_bank(6, c)
-            dz1_transpose(4)
-            out0(0, (3,))
+                dz2_copy(6, c, "vector")
+            dz1_turn(4)
+            dz1f_copy(4, "vector")
+            out0_pass(0, 3)
+            out0_copy(0, 3, "vector")
             out0(1, (3,))
             out0(2, (2, 3))
             dz1_passes(5)
@@ -637,31 +641,33 @@ def tile_multilatentattention_pb_v_kernel(tc, x, wd, wu, rope_cos, rope_sin, g, 
             dz1f_quant(4)
             dz2_quant(6, 0, 4)
             dz2_quant(6, 4, 6)
-            x_interleave(0, 2, 0)
+            x_interleave(0, 0)
             for c in range(3):
                 dz2_bank(7, c)
             dz1_turn(5)
-            dz1f_copy(5, "vector")
+            dz1f_copy(5)
             dz1_quant(0)
             for n in range(4):
                 out0_pass(3, n)
-                out0_copy(3, n, "vector" if n == 3 else "scalar")
+                out0_copy(3, n)
             dz1_passes(6)
             dz1_copy(6)
             dz1f_quant(5)
             dz2_quant(7, 0, 4)
-            x_quant(0, 2, 0)
+            x_quant(0, 0)
             dz2_quant(7, 4, 6)
-            x_interleave(0, 2, 1)
-            out0(4)
+            x_interleave(0, 1)
+            for n in range(4):
+                out0_pass(4, n)
+                out0_copy(4, n, "vector" if n == 3 else "scalar")
+            out0(5, (0, 1))
             dz1_turn(6)
             dz1f_copy(6, "vector")
-            x_quant(0, 2, 1)
+            x_quant(0, 1)
             dz1f_quant(6)
-            out0(5, (0, 1))
             dz1_passes(7)
             dz1_copy(7)
-            x_interleave(2, 4, 0)
+            x_interleave(1, 0)
             out0(5, (2, 3))
             for n in range(2):
                 out0_pass(6, n)
@@ -671,22 +677,29 @@ def tile_multilatentattention_pb_v_kernel(tc, x, wd, wu, rope_cos, rope_sin, g, 
                 out0_copy(6, n)
             out0(6, (2, 3))
             dz1f_quant(7)
-            x_quant(2, 4, 0)
+            x_interleave(1, 1)
             dz1_quant(1)
             for i in range(2):
                 out1_pass(0, i, 0)
             out0(7)
-            x_interleave(2, 4, 1)
-            x_interleave(4, 6, 0)
-            x_quant(2, 4, 1)
-            x_interleave(4, 6, 1)
-            x_quant(4, 6, 0)
-            x_quant(4, 6, 1)
-            for n in (6, 7):
-                for b in range(B):
-                    x_interleave(n, n + 1, b)
-                for b in range(B):
-                    x_quant(n, n + 1, b)
-            for n in range(8):
-                for i in range(2):
-                    out1_bank(n, i, "vector" if n == 7 and i == 1 else "scalar", n == 7)
+            x_quant(1, 0)
+            x_quant(1, 1)
+            x_interleave(2, 0)
+            x_interleave(2, 1)
+            x_quant(2, 0)
+            x_quant(2, 1)
+            x_interleave(3, 0)
+            x_interleave(3, 1)
+            x_quant(3, 0)
+            x_interleave(4, 0)
+            x_quant(3, 1)
+            x_interleave(4, 1)
+            x_quant(4, 0)
+            x_interleave(5, 0)
+            x_quant(4, 1)
+            x_interleave(5, 1)
+            x_quant(5, 0)
+            x_quant(5, 1)
+            for n, (first, rows) in enumerate(X_PIECES):
+                for i in range(rows):
+                    out1_bank(n, i, "vector" if n >= 4 else "scalar", min(rows, 2))

@@ -541,8 +541,11 @@ def tile_multilatentattention_pb_v_kernel(tc, x, wd, wu, rope_cos, rope_sin, g, 
             rope_window(2)
             sort_content(2, "scalar")
             rope_own(2)
-            dz1_passes(0, cols=slice(0, 256))
-            wu_row(3)
+            dz1_passes(0, 0, 4, cols=slice(0, 256))
+            wu_bank(3, 0)
+            wu_bank(3, 1)
+            dz1_passes(0, 4, 6, cols=slice(0, 256))
+            wu_bank(3, 2)
             wu_quant(1)
             for b in range(B):
                 load_x(b)
@@ -556,8 +559,8 @@ def tile_multilatentattention_pb_v_kernel(tc, x, wd, wu, rope_cos, rope_sin, g, 
             rope_window(3)
             wd_bank(1)
             dz1_copy(0)
-            dz1_passes(1, 0, 3)
             wd_bank(2)
+            dz1_passes(1, 0, 3)
             wd_bank(3)
             rope_window(4)
             for c in range(3):

@@ -319,59 +319,40 @@ def tile_multilatentattention_pb_v_kernel(tc, x, wd, wu, rope_cos, rope_sin, g, 
 
             dz1_tok = {}
             dz1_acc = {}
+            dz1_feat = {}
 
-            def dz1_passes(k, lo=0, hi=PASSES, cols=slice(0, DL)):
+            def dz1_passes(k, lo=0, hi=4):
                 codes, scales = dz2[k]
                 if k not in dz1_acc:
                     dz1_acc[k] = new_bank(("dz1", k))
-                for s in range(lo, hi):
-                    nc.tensor.matmul_mx(
-                        out=dz1_acc[k][:, cols],
-                        lhsT=codes[:, s, :].bitcast(E5M2),
-                        lhsT_scale=scales[:, s, :],
-                        rhs=wu_codes[:, s, cols].bitcast(E4M3),
-                        rhs_scale=wu_scales[:, s, cols],
-                        start=(s == 0),
-                        stop=(s == PASSES - 1),
-                    )
+                for t in range(lo, hi):
+                    for s in range(PASSES):
+                        nc.tensor.matmul_mx(
+                            out=dz1_acc[k][:, P * t : P * t + P],
+                            lhsT=wu_codes[:, s, P * t : P * t + P].bitcast(E4M3),
+                            lhsT_scale=wu_scales[:, s, P * t : P * t + P],
+                            rhs=codes[:, s, :].bitcast(E5M2),
+                            rhs_scale=scales[:, s, :],
+                            start=(s == 0),
+                            stop=(s == PASSES - 1),
+                        )
 
             def dz1_copy(k, engine="scalar"):
                 if k % GTILES == 0:
-                    dz1_tok[k // GTILES] = work.tile([P, GTILES, DL], BF16, name="dz1_tok", tag="dz1t", bufs=2, align_bytes=64)
+                    dz1_feat[k // GTILES] = work.tile([P, GTILES, DL], BF16, name="dz1_feat", tag="dz1t", bufs=2, align_bytes=64)
                 empty_bank(
                     ("dz1", k),
                     engine,
-                    dz1_tok[k // GTILES][:, k % GTILES, :].rearrange("p (u m e) -> p u m e", u=2, e=2),
-                    lambda bank: bank[:].rearrange("p (u e m) -> p u m e", u=2, e=2),
+                    dz1_feat[k // GTILES][:, k % GTILES, :].rearrange("p (n t) -> p n t", t=4),
+                    lambda bank: bank[:].rearrange("p (t n) -> p n t", t=4),
                 )
-
-            dz1f_grp = {}
-
-            def dz1_turn(k):
-                words = dz1_tok[k // GTILES][:, k % GTILES, :].bitcast(F32)
-                bank = new_bank(("dz1f", k))
-                for u in range(2):
-                    nc.tensor.transpose(bank[:, u * P : (u + 1) * P], words[:, u * P : (u + 1) * P], ident[:])
-
-            def dz1f_copy(k, engine="scalar"):
-                dz1f_grp[k] = work.tile([P, DL], BF16, name="dz1f_grp", tag="dz1fg", bufs=2, align_bytes=64)
-                empty_bank(
-                    ("dz1f", k),
-                    engine,
-                    dz1f_grp[k][:].bitcast(F32).rearrange("p (r u) -> p r u", u=2),
-                    lambda bank: bank[:, : 2 * P].rearrange("p (u r) -> p r u", u=2),
-                )
-
-            def dz1_transpose(k):
-                dz1_turn(k)
-                dz1f_copy(k)
 
             dz1f = {}
 
             def dz1f_quant(k):
                 codes = work.tile([P, P], U32, name="dz1f_codes", tag="dz1fc", bufs=5, align_bytes=64)
                 scales = work.tile([P, P], U8, name="dz1f_scales", tag="dz1fs", bufs=5, align_bytes=64)
-                nc.vector.quantize_mx(out=codes[:].bitcast(E5M2), scales=scales[:], in_=dz1f_grp[k][:])
+                nc.vector.quantize_mx(out=codes[:].bitcast(E5M2), scales=scales[:], in_=dz1_feat[k // GTILES][:, k % GTILES, :])
                 dz1f[k] = (codes, scales)
 
             results = []
@@ -419,11 +400,20 @@ def tile_multilatentattention_pb_v_kernel(tc, x, wd, wu, rope_cos, rope_sin, g, 
             dz1 = {}
             dz1_grp = {}
 
-            def dz1_interleave(b):
-                dz1_grp[b] = work.tile([P, DL, 4], BF16, name="dz1_grp", tag="xgrp", bufs=3, align_bytes=64)
-                nc.vector.tensor_copy(
-                    out=dz1_grp[b][:].rearrange("p (g l) t -> p g t l", l=4),
-                    in_=dz1_tok[b][:].rearrange("p t (g l) -> p g t l", l=4),
+            def dz1_turn(b, u, lo=0, hi=GTILES):
+                bank = new_bank(("dz1t", b, u)) if lo == 0 else bank_of["dz1t", b, u][1]
+                for j in range(lo, hi):
+                    words = dz1_feat[b][:, j, :].bitcast(F32).rearrange("p (n u) -> p u n", u=2)
+                    nc.tensor.transpose(bank[:, j * P : (j + 1) * P], words[:, u, :], ident[:])
+
+            def dz1t_copy(b, u, engine="scalar"):
+                if b not in dz1_grp:
+                    dz1_grp[b] = work.tile([P, DL, 4], BF16, name="dz1_grp", tag="xgrp", bufs=3, align_bytes=64)
+                empty_bank(
+                    ("dz1t", b, u),
+                    engine,
+                    dz1_grp[b][:, 256 * u : 256 * u + 256, :],
+                    lambda bank: bank[:].bitcast(BF16).rearrange("p (j c) -> p c j", j=4),
                 )
 
             def dz1_quant(b):
@@ -541,10 +531,10 @@ def tile_multilatentattention_pb_v_kernel(tc, x, wd, wu, rope_cos, rope_sin, g, 
             rope_window(2)
             sort_content(2, "scalar")
             rope_own(2)
-            dz1_passes(0, 0, 4, cols=slice(0, 256))
+            dz1_passes(0, 0, 1)
             wu_bank(3, 0)
             wu_bank(3, 1)
-            dz1_passes(0, 4, 6, cols=slice(0, 256))
+            dz1_passes(0, 1, 2)
             wu_bank(3, 2)
             wu_quant(1)
             for b in range(B):
@@ -552,7 +542,7 @@ def tile_multilatentattention_pb_v_kernel(tc, x, wd, wu, rope_cos, rope_sin, g, 
             for c in range(3):
                 dz2_bank(1, c)
             wd_bank(0)
-            dz1_passes(0, cols=slice(256, 512))
+            dz1_passes(0, 2, 4)
             sort_content(3, "scalar")
             dz2_quant(1, 0, 4)
             dz2_quant(1, 4, 6)
@@ -560,13 +550,12 @@ def tile_multilatentattention_pb_v_kernel(tc, x, wd, wu, rope_cos, rope_sin, g, 
             wd_bank(1)
             dz1_copy(0)
             wd_bank(2)
-            dz1_passes(1, 0, 3)
+            dz1_passes(1, 0, 2)
             wd_bank(3)
             rope_window(4)
             for c in range(3):
                 dz2_bank(2, c)
-            dz1_passes(1, 3, 6)
-            dz1_transpose(0)
+            dz1_passes(1, 2, 4)
             dz1_copy(1)
             rope_own(3)
             wd_quant(0)
@@ -585,7 +574,6 @@ def tile_multilatentattention_pb_v_kernel(tc, x, wd, wu, rope_cos, rope_sin, g, 
             dz2_copy(3, 2, "vector")
             dz1_passes(2)
             dz1_copy(2)
-            dz1_transpose(1)
             sort_content(5)
             dz1f_quant(1)
             dz2_quant(3, 0, 4)
@@ -599,7 +587,6 @@ def tile_multilatentattention_pb_v_kernel(tc, x, wd, wu, rope_cos, rope_sin, g, 
             dz2_copy(4, 1)
             rope_window(6, 0)
             dz2_copy(4, 2, "vector")
-            dz1_transpose(2)
             dz1_passes(3)
             sort_content(6, "scalar")
             dz1_copy(3)
@@ -615,7 +602,6 @@ def tile_multilatentattention_pb_v_kernel(tc, x, wd, wu, rope_cos, rope_sin, g, 
             dz2_copy(5, 1)
             rope_window(7, 0)
             dz2_copy(5, 2, "vector")
-            dz1_transpose(3)
             out0(2, (0, 1))
             out0(0, (2,))
             out0(1, (2,))
@@ -632,59 +618,57 @@ def tile_multilatentattention_pb_v_kernel(tc, x, wd, wu, rope_cos, rope_sin, g, 
             free_banks.append(7)
             for c in range(3):
                 dz2_copy(6, c, "vector")
-            dz1_turn(4)
-            dz1f_copy(4, "vector")
             out0_pass(0, 3)
             out0_copy(0, 3, "vector")
-            out0(1, (3,))
+            out0_pass(1, 3)
+            out0_copy(1, 3, "vector")
             out0(2, (2, 3))
+            out0(3, (0, 1))
             dz1_passes(5)
             dz1_copy(5)
-            dz1_interleave(0)
             dz1f_quant(4)
             dz2_quant(6, 0, 4)
             dz2_quant(6, 4, 6)
             x_interleave(0, 0)
             for c in range(3):
                 dz2_bank(7, c)
-            dz1_turn(5)
-            dz1f_copy(5)
-            dz1_quant(0)
-            for n in range(4):
-                out0_pass(3, n)
-                out0_copy(3, n)
-            dz1_passes(6)
-            dz1_copy(6)
-            dz1f_quant(5)
-            dz2_quant(7, 0, 4)
+            dz1_turn(0, 0)
             x_quant(0, 0)
+            dz1t_copy(0, 0, "vector")
+            dz1f_quant(5)
+            out0(3, (2, 3))
+            out0(4, (0, 1))
+            dz1_passes(6)
+            dz2_quant(7, 0, 4)
             dz2_quant(7, 4, 6)
             x_interleave(0, 1)
-            for n in range(4):
-                out0_pass(4, n)
-                out0_copy(4, n, "vector" if n == 3 else "scalar")
-            out0(5, (0, 1))
-            dz1_turn(6)
-            dz1f_copy(6, "vector")
-            x_quant(0, 1)
-            dz1f_quant(6)
+            dz1_copy(6)
+            out0(4, (2, 3))
+            dz1_turn(0, 1)
+            dz1t_copy(0, 1, "vector")
+            out0(5, range(4))
             dz1_passes(7)
             dz1_copy(7)
+            dz1f_quant(6)
+            x_quant(0, 1)
+            dz1_quant(0)
             x_interleave(1, 0)
-            out0(5, (2, 3))
+            dz1f_quant(7)
+            out0(5, ())
             for n in range(2):
                 out0_pass(6, n)
-            dz1_interleave(1)
-            dz1_transpose(7)
+            for u in range(2):
+                dz1_turn(1, u)
             for n in range(2):
                 out0_copy(6, n)
+            dz1t_copy(1, 0, "vector")
+            dz1t_copy(1, 1)
             out0(6, (2, 3))
-            dz1f_quant(7)
             x_interleave(1, 1)
             dz1_quant(1)
+            out0(7)
             for i in range(2):
                 out1_pass(0, i, 0)
-            out0(7)
             x_quant(1, 0)
             x_quant(1, 1)
             x_interleave(2, 0)

@@ -319,9 +319,58 @@ def tile_multilatentattention_pb_v_kernel(tc, x, wd, wu, rope_cos, rope_sin, g, 
 
             dz1_tok = {}
             dz1_acc = {}
+
+            def dz1_passes(k, lo=0, hi=PASSES, cols=slice(0, DL)):
+                codes, scales = dz2[k]
+                if k not in dz1_acc:
+                    dz1_acc[k] = new_bank(("dz1", k))
+                for s in range(lo, hi):
+                    nc.tensor.matmul_mx(
+                        out=dz1_acc[k][:, cols],
+                        lhsT=codes[:, s, :].bitcast(E5M2),
+                        lhsT_scale=scales[:, s, :],
+                        rhs=wu_codes[:, s, cols].bitcast(E4M3),
+                        rhs_scale=wu_scales[:, s, cols],
+                        start=(s == 0),
+                        stop=(s == PASSES - 1),
+                    )
+
+            def dz1_copy(k, engine="scalar"):
+                if k % GTILES == 0:
+                    dz1_tok[k // GTILES] = work.tile([P, GTILES, DL], BF16, name="dz1_tok", tag="dz1t", bufs=2, align_bytes=64)
+                empty_bank(
+                    ("dz1", k),
+                    engine,
+                    dz1_tok[k // GTILES][:, k % GTILES, :].rearrange("p (u m e) -> p u m e", u=2, e=2),
+                    lambda bank: bank[:].rearrange("p (u e m) -> p u m e", u=2, e=2),
+                )
+
+            dz1f_grp = {}
+
+            def dz1_turn(k):
+                words = dz1_tok[k // GTILES][:, k % GTILES, :].bitcast(F32)
+                bank = new_bank(("dz1f", k))
+                for u in range(2):
+                    nc.tensor.transpose(bank[:, u * P : (u + 1) * P], words[:, u * P : (u + 1) * P], ident[:])
+
+            def dz1f_copy(k, engine="scalar"):
+                dz1f_grp[k] = work.tile([P, DL], BF16, name="dz1f_grp", tag="dz1fg", bufs=2, align_bytes=64)
+                empty_bank(
+                    ("dz1f", k),
+                    engine,
+                    dz1f_grp[k][:].bitcast(F32).rearrange("p (r u) -> p r u", u=2),
+                    lambda bank: bank[:, : 2 * P].rearrange("p (u r) -> p r u", u=2),
+                )
+
+            def dz1_transpose(k):
+                dz1_turn(k)
+                dz1f_copy(k)
+
+            dz1f = {}
+
             dz1_feat = {}
 
-            def dz1_passes(k, lo=0, hi=4):
+            def feat_passes(k, lo=0, hi=4):
                 codes, scales = dz2[k]
                 if k not in dz1_acc:
                     dz1_acc[k] = new_bank(("dz1", k))
@@ -337,7 +386,7 @@ def tile_multilatentattention_pb_v_kernel(tc, x, wd, wu, rope_cos, rope_sin, g, 
                             stop=(s == PASSES - 1),
                         )
 
-            def dz1_copy(k, engine="scalar"):
+            def feat_copy(k, engine="scalar"):
                 if k % GTILES == 0:
                     dz1_feat[k // GTILES] = work.tile([P, GTILES, DL], BF16, name="dz1_feat", tag="dz1t", bufs=2, align_bytes=64)
                 empty_bank(
@@ -347,12 +396,10 @@ def tile_multilatentattention_pb_v_kernel(tc, x, wd, wu, rope_cos, rope_sin, g, 
                     lambda bank: bank[:].rearrange("p (t n) -> p n t", t=4),
                 )
 
-            dz1f = {}
-
             def dz1f_quant(k):
                 codes = work.tile([P, P], U32, name="dz1f_codes", tag="dz1fc", bufs=5, align_bytes=64)
                 scales = work.tile([P, P], U8, name="dz1f_scales", tag="dz1fs", bufs=5, align_bytes=64)
-                nc.vector.quantize_mx(out=codes[:].bitcast(E5M2), scales=scales[:], in_=dz1_feat[k // GTILES][:, k % GTILES, :])
+                nc.vector.quantize_mx(out=codes[:].bitcast(E5M2), scales=scales[:], in_=dz1f_grp[k][:] if k < GTILES else dz1_feat[1][:, k - GTILES, :])
                 dz1f[k] = (codes, scales)
 
             results = []
@@ -400,7 +447,14 @@ def tile_multilatentattention_pb_v_kernel(tc, x, wd, wu, rope_cos, rope_sin, g, 
             dz1 = {}
             dz1_grp = {}
 
-            def dz1_turn(b, u, lo=0, hi=GTILES):
+            def dz1_interleave(b):
+                dz1_grp[b] = work.tile([P, DL, 4], BF16, name="dz1_grp", tag="xgrp", bufs=3, align_bytes=64)
+                nc.vector.tensor_copy(
+                    out=dz1_grp[b][:].rearrange("p (g l) t -> p g t l", l=4),
+                    in_=dz1_tok[b][:].rearrange("p t (g l) -> p g t l", l=4),
+                )
+
+            def feat_turn(b, u, lo=0, hi=GTILES):
                 bank = new_bank(("dz1t", b, u)) if lo == 0 else bank_of["dz1t", b, u][1]
                 for j in range(lo, hi):
                     words = dz1_feat[b][:, j, :].bitcast(F32).rearrange("p (n u) -> p u n", u=2)
@@ -524,17 +578,17 @@ def tile_multilatentattention_pb_v_kernel(tc, x, wd, wu, rope_cos, rope_sin, g, 
             sort_content(1, "scalar")
             wu_row(1)
             dz2_quant(0, 0, 4)
-            rope_own(1)
+            rope_own(1, 5)
             dz2_quant(0, 4, 6)
             wu_quant(0)
             wu_row(2)
-            rope_window(2)
+            rope_window(2, 5)
             sort_content(2, "scalar")
-            rope_own(2)
-            dz1_passes(0, 0, 1)
+            rope_own(2, 5)
+            dz1_passes(0, 0, 4, cols=slice(0, 256))
             wu_bank(3, 0)
             wu_bank(3, 1)
-            dz1_passes(0, 1, 2)
+            dz1_passes(0, 4, 6, cols=slice(0, 256))
             wu_bank(3, 2)
             wu_quant(1)
             for b in range(B):
@@ -542,22 +596,23 @@ def tile_multilatentattention_pb_v_kernel(tc, x, wd, wu, rope_cos, rope_sin, g, 
             for c in range(3):
                 dz2_bank(1, c)
             wd_bank(0)
-            dz1_passes(0, 2, 4)
+            dz1_passes(0, cols=slice(256, 512))
             sort_content(3, "scalar")
             dz2_quant(1, 0, 4)
             dz2_quant(1, 4, 6)
-            rope_window(3)
+            rope_window(3, 5)
             wd_bank(1)
             dz1_copy(0)
             wd_bank(2)
-            dz1_passes(1, 0, 2)
+            dz1_passes(1, 0, 3)
             wd_bank(3)
-            rope_window(4)
+            rope_window(4, 5)
             for c in range(3):
                 dz2_bank(2, c)
-            dz1_passes(1, 2, 4)
+            dz1_passes(1, 3, 6)
+            dz1_transpose(0)
             dz1_copy(1)
-            rope_own(3)
+            rope_own(3, 5)
             wd_quant(0)
             dz2_quant(2, 0, 4)
             dz2_quant(2, 4, 6)
@@ -574,6 +629,7 @@ def tile_multilatentattention_pb_v_kernel(tc, x, wd, wu, rope_cos, rope_sin, g, 
             dz2_copy(3, 2, "vector")
             dz1_passes(2)
             dz1_copy(2)
+            dz1_transpose(1)
             sort_content(5)
             dz1f_quant(1)
             dz2_quant(3, 0, 4)
@@ -587,6 +643,7 @@ def tile_multilatentattention_pb_v_kernel(tc, x, wd, wu, rope_cos, rope_sin, g, 
             dz2_copy(4, 1)
             rope_window(6, 0)
             dz2_copy(4, 2, "vector")
+            dz1_transpose(2)
             dz1_passes(3)
             sort_content(6, "scalar")
             dz1_copy(3)
@@ -602,11 +659,12 @@ def tile_multilatentattention_pb_v_kernel(tc, x, wd, wu, rope_cos, rope_sin, g, 
             dz2_copy(5, 1)
             rope_window(7, 0)
             dz2_copy(5, 2, "vector")
+            dz1_transpose(3)
             out0(2, (0, 1))
             out0(0, (2,))
             out0(1, (2,))
-            dz1_passes(4)
-            dz1_copy(4)
+            feat_passes(4)
+            feat_copy(4)
             sort_content(7, "scalar")
             wd_quant(3)
             dz1f_quant(3)
@@ -614,64 +672,62 @@ def tile_multilatentattention_pb_v_kernel(tc, x, wd, wu, rope_cos, rope_sin, g, 
             dz2_quant(5, 4, 6)
             for c in range(3):
                 dz2_turn(6, c)
-            rope_finish(7, nc.gpsimd, 0)
+            rope_own(7, 7)
+            rope_finish(7, nc.gpsimd, 7)
             free_banks.append(7)
             for c in range(3):
                 dz2_copy(6, c, "vector")
-            out0_pass(0, 3)
-            out0_copy(0, 3, "vector")
-            out0_pass(1, 3)
-            out0_copy(1, 3, "vector")
+            out0(0, (3,))
+            out0(1, (3,))
             out0(2, (2, 3))
             out0(3, (0, 1))
-            dz1_passes(5)
-            dz1_copy(5)
+            feat_passes(5)
+            feat_copy(5)
             dz1f_quant(4)
             dz2_quant(6, 0, 4)
             dz2_quant(6, 4, 6)
             x_interleave(0, 0)
             for c in range(3):
                 dz2_bank(7, c)
-            dz1_turn(0, 0)
+            dz1_interleave(0)
             x_quant(0, 0)
-            dz1t_copy(0, 0, "vector")
             dz1f_quant(5)
             out0(3, (2, 3))
             out0(4, (0, 1))
-            dz1_passes(6)
+            feat_passes(6)
             dz2_quant(7, 0, 4)
             dz2_quant(7, 4, 6)
+            dz1_quant(0)
             x_interleave(0, 1)
-            dz1_copy(6)
+            feat_copy(6)
             out0(4, (2, 3))
-            dz1_turn(0, 1)
-            dz1t_copy(0, 1, "vector")
-            out0(5, range(4))
-            dz1_passes(7)
-            dz1_copy(7)
+            out0(5, (0, 1))
+            feat_passes(7)
+            feat_copy(7)
             dz1f_quant(6)
             x_quant(0, 1)
-            dz1_quant(0)
             x_interleave(1, 0)
+            x_interleave(1, 1)
             dz1f_quant(7)
-            out0(5, ())
+            out0(5, (2, 3))
             for n in range(2):
                 out0_pass(6, n)
             for u in range(2):
-                dz1_turn(1, u)
+                feat_turn(1, u)
             for n in range(2):
                 out0_copy(6, n)
             dz1t_copy(1, 0, "vector")
-            dz1t_copy(1, 1)
-            out0(6, (2, 3))
-            x_interleave(1, 1)
+            dz1t_copy(1, 1, "vector")
+            for n in (2, 3):
+                out0_pass(6, n)
+                out0_copy(6, n, "scalar")
+            x_quant(1, 0)
             dz1_quant(1)
             out0(7)
             for i in range(2):
                 out1_pass(0, i, 0)
-            x_quant(1, 0)
-            x_quant(1, 1)
             x_interleave(2, 0)
+            x_quant(1, 1)
             x_interleave(2, 1)
             x_quant(2, 0)
             x_quant(2, 1)

@@ -175,8 +175,8 @@ def tile_multilatentattention_pb_v_kernel(tc, x, wd, wu, rope_cos, rope_sin, g, 
                 words = g_raw[k][0][:].bitcast(F32)[:, :, : DH // 2]
                 copy(
                     engine,
-                    t[:, :, :, : DH // 4].rearrange("p u h (g l) -> p h g u l", l=2),
-                    words.rearrange("p h (g l u) -> p h g u l", l=2, u=2),
+                    t[:, :, :, : DH // 4].rearrange("p u h (g l) -> p h g u l", l=4),
+                    words.rearrange("p h (g l u) -> p h g u l", l=4, u=2),
                 )
 
             def sorted_product(k, which, u, lo, hi):
@@ -480,34 +480,35 @@ def tile_multilatentattention_pb_v_kernel(tc, x, wd, wu, rope_cos, rope_sin, g, 
 
             x_grp = {}
 
-            def x_interleave(piece, b, engine="vector"):
-                first, rows = X_PIECES[piece]
-                x_grp[piece, b] = work.tile([P, P * rows, 4], BF16, name="x_grp", tag="xgrp", bufs=3, align_bytes=64)
-                copy(
-                    engine,
-                    x_grp[piece, b][:].rearrange("p (i g l) t -> p g t l i", i=rows, l=8 // rows),
-                    x_raw[b][:, :, first : first + P * rows].rearrange("p t (g l i) -> p g t l i", i=rows, l=8 // rows),
+            def x_interleave(piece, b):
+                first, banks = X_PIECES[piece]
+                rows = min(banks, 2)
+                x_grp[piece, b] = work.tile([P, P * banks, 4], BF16, name="x_grp", tag="xgrp", bufs=3, align_bytes=64)
+                nc.vector.tensor_copy(
+                    out=x_grp[piece, b][:].rearrange("p (i g l) t -> p g t l i", i=rows, l=4 // rows),
+                    in_=x_raw[b][:, :, first : first + P * banks].rearrange("p t (g l i) -> p g t l i", i=rows, l=4 // rows),
                 )
 
             def x_quant(piece, b):
-                first, rows = X_PIECES[piece]
+                first, banks = X_PIECES[piece]
                 nc.vector.quantize_mx(
-                    out=x_codes[:, b, first : first + P * rows].bitcast(E4M3),
-                    scales=x_scales[:, b, first : first + P * rows],
+                    out=x_codes[:, b, first : first + P * banks].bitcast(E4M3),
+                    scales=x_scales[:, b, first : first + P * banks],
                     in_=x_grp[piece, b][:].rearrange("p c t -> p (c t)"),
                 )
 
             out1_acc = {}
 
-            def out1_pass(piece, i, b):
+            def out1_pass(piece, n, b):
                 if b == 0:
-                    out1_acc[piece, i] = new_bank(("out1", piece, i))
+                    out1_acc[piece, n] = new_bank(("out1", piece, n))
                 codes, scales = dz1[b]
-                first = X_PIECES[piece][0] + P * i
+                first, banks = X_PIECES[piece]
+                col = first + P * (n // 2 + banks // 2 * (n % 2))
                 nc.tensor.matmul_mx(
-                    out=out1_acc[piece, i][:],
-                    lhsT=x_codes[:, b, first : first + P].bitcast(E4M3),
-                    lhsT_scale=x_scales[:, b, first : first + P],
+                    out=out1_acc[piece, n][:],
+                    lhsT=x_codes[:, b, col : col + P].bitcast(E4M3),
+                    lhsT_scale=x_scales[:, b, col : col + P],
                     rhs=codes[:].bitcast(E5M2),
                     rhs_scale=scales[:],
                     start=(b == 0),
@@ -516,27 +517,25 @@ def tile_multilatentattention_pb_v_kernel(tc, x, wd, wu, rope_cos, rope_sin, g, 
 
             out1_res = {}
 
-            def out1_copy(piece, i, engine="scalar", store=None):
-                first, rows = X_PIECES[piece]
-                store = store or rows
-                if piece not in out1_res:
-                    out1_res[piece] = new_result(rows)
-                res = out1_res[piece]
+            def out1_copy(piece, n, engine="scalar", rows=2):
+                first = X_PIECES[piece][0] + 256 * (n // 2)
+                if (piece, n // 2) not in out1_res:
+                    out1_res[piece, n // 2] = new_result(rows)
+                res = out1_res[piece, n // 2]
                 empty_bank(
-                    ("out1", piece, i),
+                    ("out1", piece, n),
                     engine,
-                    res[:, i, :].rearrange("p (m u e) -> p m u e", u=2, e=2),
+                    res[:, n % 2, :].rearrange("p (m u e) -> p m u e", u=2, e=2),
                     lambda bank: bank[:].rearrange("p (u m e) -> p m u e", u=2, e=2),
                 )
-                if (i + 1) % store == 0:
-                    view = out_1[first : first + P * rows].rearrange("(p i) l -> p i l", i=rows)
-                    nc.sync.dma_start(out=view[:, i + 1 - store : i + 1], in_=res[:, i + 1 - store : i + 1])
+                if n % 2 == rows - 1:
+                    nc.sync.dma_start(out=out_1[first : first + P * rows].rearrange("(p i) l -> p i l", i=rows), in_=res[:])
 
-            def out1_bank(piece, i, engine="scalar", store=None):
-                if (piece, i) not in out1_acc:
-                    out1_pass(piece, i, 0)
-                out1_pass(piece, i, 1)
-                out1_copy(piece, i, engine, store)
+            def out1_bank(piece, n, engine="scalar", rows=2):
+                if (piece, n) not in out1_acc:
+                    out1_pass(piece, n, 0)
+                out1_pass(piece, n, 1)
+                out1_copy(piece, n, engine, rows)
 
             load_tables()
             load_first_g(0)

@@ -25,9 +25,10 @@ HF = DH + DR
 KIB = 1024
 COS, SIN = 0, 1
 OWN_HEADS = 4
+SORTED_SLOTS = 3
 GRAD_SLOTS = 4
 WHOLE_FROM = 8
-X_PIECES = ((0, 4), (512, 4), (1024, 4), (1536, 2), (1792, 1), (1920, 1))
+X_PIECES = ((0, 4), (512, 4), (1024, 2), (1280, 2), (1536, 2), (1792, 1), (1920, 1))
 RESULT_SLOTS = 10
 
 
@@ -53,11 +54,10 @@ def tile_multilatentattention_pb_v_kernel(tc, x, wd, wu, rope_cos, rope_sin, g, 
         make_identity(nc, ident_first[:])
 
         tables = keep.tile([P, 2, 4, DR], F32, name="tables", align_bytes=64)
-        tables_sorted = arena.tile([P, 2, 4, DR], F32, name="tables_sorted", offset=64 * KIB, align_bytes=64)
         tables_t = arena.tile([P, 4, P], F32, name="tables_t", offset=66 * KIB, align_bytes=64)
         tables_psum = psum.tile([P, 2, 4, DR], F32, name="tables_psum", tag="bank7")
-        wu_codes = keep.tile([P, PASSES, DL], U32, name="wu_codes", align_bytes=64)
-        wu_scales = keep.tile([P, PASSES, DL], U8, name="wu_scales", align_bytes=64)
+        wu_codes = keep.tile([P, 2, PASSES, DL // 2], U32, name="wu_codes", align_bytes=64)
+        wu_scales = keep.tile([P, 2, PASSES, DL // 2], U8, name="wu_scales", align_bytes=64)
         wd_codes = keep.tile([P, D], U32, name="wd_codes", align_bytes=64)
         wd_scales = keep.tile([P, D], U8, name="wd_scales", align_bytes=64)
         x_codes = keep.tile([P, B, D], U32, name="x_codes", align_bytes=64)
@@ -78,7 +78,7 @@ def tile_multilatentattention_pb_v_kernel(tc, x, wd, wu, rope_cos, rope_sin, g, 
                 g_raw[k] = [t]
 
             def load_first_g(half):
-                t = keep.tile([P, H // 2, HF], BF16, name=f"g0_{half}", align_bytes=64)
+                t = arena.tile([P, H // 2, HF], BF16, name=f"g0_{half}", offset=KIB * (24 + 3 * half), align_bytes=64)
                 nc.sync.dma_start(out=t[:], in_=g_view[0][:, 0, half * H // 2 : (half + 1) * H // 2])
                 g_raw.setdefault(0, []).append(t)
 
@@ -93,10 +93,10 @@ def tile_multilatentattention_pb_v_kernel(tc, x, wd, wu, rope_cos, rope_sin, g, 
                 nc.sync.dma_start(out=t[:], in_=wd_view[:, c])
                 wd_raw[c] = t
 
-            def load_x(b):
-                t = arena.tile([P, 4, D], BF16, name=f"x{b}", offset=KIB * (40 + 16 * b), align_bytes=64)
-                nc.sync.dma_start(out=t[:], in_=x_view[b])
-                x_raw[b] = t
+            def load_x(b, lo=0, hi=4):
+                if b not in x_raw:
+                    x_raw[b] = arena.tile([P, 4, D], BF16, name=f"x{b}", offset=KIB * (40 + 16 * b), align_bytes=64)
+                nc.sync.dma_start(out=x_raw[b][:, lo:hi], in_=x_view[b][:, lo:hi])
 
             def copy(engine, out, in_):
                 if engine == "vector":
@@ -127,16 +127,10 @@ def tile_multilatentattention_pb_v_kernel(tc, x, wd, wu, rope_cos, rope_sin, g, 
             def tables_negate():
                 nc.scalar.mul(out=tables[:, SIN, :, 0:32], in_=tables[:, SIN, :, 0:32], mul=-1.0)
 
-            def tables_sort():
-                nc.scalar.copy(
-                    out=tables_sorted[:].rearrange("p a j (u m e) -> p (a j) u m e", u=2, e=2),
-                    in_=tables[:].rearrange("p a j (m u e) -> p (a j) u m e", u=2, e=2),
-                )
-
             def tables_turn():
                 bank = new_bank("tables")
-                flat = tables_sorted[:].rearrange("p a j r -> p (a j r)")
-                for q in range(4):
+                flat = tables[:].rearrange("p a j r -> p (a j r)")
+                for q in (2, 3, 0, 1):
                     nc.tensor.transpose(bank[:, q * P : (q + 1) * P], flat[:, q * P : (q + 1) * P], ident[:])
                 empty_bank("tables", "scalar", tables_t[:].rearrange("p j c -> p (j c)"), lambda bank: bank[:])
 
@@ -169,9 +163,13 @@ def tile_multilatentattention_pb_v_kernel(tc, x, wd, wu, rope_cos, rope_sin, g, 
 
             g_sorted = {}
 
+            def new_sorted(k):
+                if k not in g_sorted:
+                    g_sorted[k] = work.tile([P, 2, H, HF // 4], F32, name="g_sorted", tag="gs", bufs=SORTED_SLOTS, align_bytes=64)
+                return g_sorted[k]
+
             def sort_content(k, engine="vector"):
-                t = work.tile([P, 2, H, HF // 4], F32, name="g_sorted", tag="gs", bufs=3, align_bytes=64)
-                g_sorted[k] = t
+                t = new_sorted(k)
                 words = g_raw[k][0][:].bitcast(F32)[:, :, : DH // 2]
                 copy(
                     engine,
@@ -181,7 +179,7 @@ def tile_multilatentattention_pb_v_kernel(tc, x, wd, wu, rope_cos, rope_sin, g, 
 
             def sorted_product(k, which, u, lo, hi):
                 rope = rope_part(k, lo, hi).rearrange("p h (a m u e) -> p h a m u e", a=2, u=2, e=2)[:, :, :, :, u, :]
-                row = tables_psum[:, which, k % 4, 32 * u : 32 * u + 32].rearrange("p (a m e) -> p a m e", a=2, e=2)
+                row = tables_psum[:, which, k % 4, :].rearrange("p (a m u e) -> p a m u e", a=2, u=2, e=2)[:, :, :, u, :]
                 out = products[k][which][:].rearrange("p (u h a m e) -> p u h a m e", u=2, h=H, a=2, e=2)[:, u, lo:hi]
                 if which == SIN:
                     out = out[:, :, ::-1]
@@ -189,7 +187,7 @@ def tile_multilatentattention_pb_v_kernel(tc, x, wd, wu, rope_cos, rope_sin, g, 
 
             def sorted_sum(engine, k, lo, hi):
                 pc, ps = [t[:].rearrange("p (u h f) -> p u h f", u=2, h=H)[:, :, lo:hi] for t in products[k]]
-                out = g_sorted[k][:].bitcast(BF16)[:, :, lo:hi, DH // 2 :]
+                out = new_sorted(k)[:].bitcast(BF16)[:, :, lo:hi, DH // 2 :]
                 engine.tensor_tensor(out=out, in0=pc, in1=ps, op=ADD)
 
             def rope_products(k):
@@ -234,12 +232,12 @@ def tile_multilatentattention_pb_v_kernel(tc, x, wd, wu, rope_cos, rope_sin, g, 
                 for c in range(3):
                     wu_bank(r, c)
 
-            def wu_quant(pair, lo=0, hi=PASSES):
-                for s in range(lo, hi):
+            def wu_quant(pair, lo=0, hi=3):
+                for c in range(lo, hi):
                     nc.vector.quantize_mx(
-                        out=wu_codes[:, s, 256 * pair : 256 * pair + 256].bitcast(E4M3),
-                        scales=wu_scales[:, s, 256 * pair : 256 * pair + 256],
-                        in_=wu_grp[pair, s // 2][:, s % 2].rearrange("p r c -> p (r c)"),
+                        out=wu_codes[:, pair, 2 * c : 2 * c + 2].rearrange("p s l -> p (s l)").bitcast(E4M3),
+                        scales=wu_scales[:, pair, 2 * c : 2 * c + 2].rearrange("p s l -> p (s l)"),
+                        in_=wu_grp[pair, c][:].rearrange("p s r c -> p (s r c)"),
                     )
 
             wd_grp = {}
@@ -320,17 +318,17 @@ def tile_multilatentattention_pb_v_kernel(tc, x, wd, wu, rope_cos, rope_sin, g, 
             dz1_tok = {}
             dz1_acc = {}
 
-            def dz1_passes(k, lo=0, hi=PASSES, cols=slice(0, DL)):
+            def dz1_passes(k, half, lo=0, hi=PASSES):
                 codes, scales = dz2[k]
                 if k not in dz1_acc:
                     dz1_acc[k] = new_bank(("dz1", k))
                 for s in range(lo, hi):
                     nc.tensor.matmul_mx(
-                        out=dz1_acc[k][:, cols],
+                        out=dz1_acc[k][:, 256 * half : 256 * half + 256],
                         lhsT=codes[:, s, :].bitcast(E5M2),
                         lhsT_scale=scales[:, s, :],
-                        rhs=wu_codes[:, s, cols].bitcast(E4M3),
-                        rhs_scale=wu_scales[:, s, cols],
+                        rhs=wu_codes[:, half, s].bitcast(E4M3),
+                        rhs_scale=wu_scales[:, half, s],
                         start=(s == 0),
                         stop=(s == PASSES - 1),
                     )
@@ -347,24 +345,21 @@ def tile_multilatentattention_pb_v_kernel(tc, x, wd, wu, rope_cos, rope_sin, g, 
 
             dz1f_grp = {}
 
-            def dz1_turn(k):
-                words = dz1_tok[k // GTILES][:, k % GTILES, :].bitcast(F32)
-                bank = new_bank(("dz1f", k))
-                for u in range(2):
-                    nc.tensor.transpose(bank[:, u * P : (u + 1) * P], words[:, u * P : (u + 1) * P], ident[:])
+            def dz1_turn(q):
+                bank = new_bank(("dz1f", q))
+                for j in range(2):
+                    words = dz1_tok[0][:, 2 * q + j, :].bitcast(F32)
+                    for u in range(2):
+                        nc.tensor.transpose(bank[:, (2 * j + u) * P : (2 * j + u + 1) * P], words[:, u * P : (u + 1) * P], ident[:])
 
-            def dz1f_copy(k, engine="scalar"):
-                dz1f_grp[k] = work.tile([P, DL], BF16, name="dz1f_grp", tag="dz1fg", bufs=2, align_bytes=64)
+            def dz1f_copy(q, engine="scalar"):
+                dz1f_grp[q] = work.tile([P, 2 * DL], BF16, name="dz1f_grp", tag="dz1fg", bufs=1, align_bytes=64)
                 empty_bank(
-                    ("dz1f", k),
+                    ("dz1f", q),
                     engine,
-                    dz1f_grp[k][:].bitcast(F32).rearrange("p (r u) -> p r u", u=2),
-                    lambda bank: bank[:, : 2 * P].rearrange("p (u r) -> p r u", u=2),
+                    dz1f_grp[q][:].bitcast(F32).rearrange("p (j r u) -> p j r u", j=2, u=2),
+                    lambda bank: bank[:].rearrange("p (j u r) -> p j r u", j=2, u=2),
                 )
-
-            def dz1_transpose(k):
-                dz1_turn(k)
-                dz1f_copy(k)
 
             dz1f = {}
 
@@ -378,8 +373,8 @@ def tile_multilatentattention_pb_v_kernel(tc, x, wd, wu, rope_cos, rope_sin, g, 
                     for s in range(PASSES):
                         nc.tensor.matmul_mx(
                             out=dz1_acc[k][:, P * t : P * t + P],
-                            lhsT=wu_codes[:, s, P * t : P * t + P].bitcast(E4M3),
-                            lhsT_scale=wu_scales[:, s, P * t : P * t + P],
+                            lhsT=wu_codes[:, t // 2, s, P * (t % 2) : P * (t % 2) + P].bitcast(E4M3),
+                            lhsT_scale=wu_scales[:, t // 2, s, P * (t % 2) : P * (t % 2) + P],
                             rhs=codes[:, s, :].bitcast(E5M2),
                             rhs_scale=scales[:, s, :],
                             start=(s == 0),
@@ -396,11 +391,16 @@ def tile_multilatentattention_pb_v_kernel(tc, x, wd, wu, rope_cos, rope_sin, g, 
                     lambda bank: bank[:].rearrange("p (t n) -> p n t", t=4),
                 )
 
-            def dz1f_quant(k):
-                codes = work.tile([P, P], U32, name="dz1f_codes", tag="dz1fc", bufs=5, align_bytes=64)
-                scales = work.tile([P, P], U8, name="dz1f_scales", tag="dz1fs", bufs=5, align_bytes=64)
-                nc.vector.quantize_mx(out=codes[:].bitcast(E5M2), scales=scales[:], in_=dz1f_grp[k][:] if k < GTILES else dz1_feat[1][:, k - GTILES, :])
-                dz1f[k] = (codes, scales)
+            def dz1f_quant(k, n=1):
+                codes = work.tile([P, n * P], U32, name="dz1f_codes", tag="dz1fc", bufs=3, align_bytes=64)
+                scales = work.tile([P, n * P], U8, name="dz1f_scales", tag="dz1fs", bufs=3, align_bytes=64)
+                if k < GTILES:
+                    src = dz1f_grp[k // 2][:]
+                else:
+                    src = dz1_feat[1][:, k - GTILES : k - GTILES + n, :].rearrange("p j c -> p (j c)")
+                nc.vector.quantize_mx(out=codes[:].bitcast(E5M2), scales=scales[:], in_=src)
+                for j in range(n):
+                    dz1f[k + j] = (codes[:, P * j : P * j + P], scales[:, P * j : P * j + P])
 
             results = []
 
@@ -416,8 +416,8 @@ def tile_multilatentattention_pb_v_kernel(tc, x, wd, wu, rope_cos, rope_sin, g, 
                 codes, scales = dz1f[k]
                 nc.tensor.matmul_mx(
                     out=new_bank(("out0", k, n))[:],
-                    lhsT=codes[:].bitcast(E5M2),
-                    lhsT_scale=scales[:],
+                    lhsT=codes.bitcast(E5M2),
+                    lhsT_scale=scales,
                     rhs=wd_codes[:, 512 * n : 512 * n + 512].bitcast(E4M3),
                     rhs_scale=wd_scales[:, 512 * n : 512 * n + 512],
                     start=True,
@@ -425,6 +425,7 @@ def tile_multilatentattention_pb_v_kernel(tc, x, wd, wu, rope_cos, rope_sin, g, 
                 )
 
             out0_res = {}
+            out0_done = set()
 
             def out0_copy(k, n, engine="scalar"):
                 banks = 4 if k >= WHOLE_FROM else 2
@@ -433,16 +434,28 @@ def tile_multilatentattention_pb_v_kernel(tc, x, wd, wu, rope_cos, rope_sin, g, 
                     out0_res[k, part] = new_result(banks)
                 res = out0_res[k, part]
                 empty_bank(("out0", k, n), engine, res[:, i, :], lambda bank: bank[:])
-                if i == banks - 1:
+                out0_done.add((k, n))
+                if all((k, banks * part + j) in out0_done for j in range(banks)):
                     nc.sync.dma_start(
                         out=out0_view[k // GTILES][:, k % GTILES, 512 * banks * part : 512 * banks * (part + 1)],
                         in_=res[:].rearrange("p i c -> p (i c)"),
                     )
 
-            def out0(k, blocks=range(4)):
+            def out0_passes(k, blocks=range(4)):
                 for n in blocks:
                     out0_pass(k, n)
-                    out0_copy(k, n)
+
+            def out0_copies(k, blocks=range(4), engine="scalar"):
+                for n in blocks:
+                    out0_copy(k, n, engine)
+
+            def dz2_turns(k):
+                for c in range(3):
+                    dz2_turn(k, c)
+
+            def dz2_copies(k, order=(1, 0, 2), engine="scalar"):
+                for c in order:
+                    dz2_copy(k, c, engine)
 
             dz1 = {}
             dz1_grp = {}
@@ -480,13 +493,29 @@ def tile_multilatentattention_pb_v_kernel(tc, x, wd, wu, rope_cos, rope_sin, g, 
 
             x_grp = {}
 
+            def new_x_grp(piece, b):
+                tag, bufs = ("xside", 1) if (piece, b) in ((1, 0), (2, 0)) else ("xgrp", 3)
+                x_grp[piece, b] = work.tile([P, P * X_PIECES[piece][1], 4], BF16, name="x_grp", tag=tag, bufs=bufs, align_bytes=64)
+
             def x_interleave(piece, b):
                 first, banks = X_PIECES[piece]
                 rows = min(banks, 2)
-                x_grp[piece, b] = work.tile([P, P * banks, 4], BF16, name="x_grp", tag="xgrp", bufs=3, align_bytes=64)
+                new_x_grp(piece, b)
                 nc.vector.tensor_copy(
                     out=x_grp[piece, b][:].rearrange("p (i g l) t -> p g t l i", i=rows, l=4 // rows),
                     in_=x_raw[b][:, :, first : first + P * banks].rearrange("p t (g l i) -> p g t l i", i=rows, l=4 // rows),
+                )
+
+            def x_interleave_side(piece, b):
+                first, banks = X_PIECES[piece]
+                new_x_grp(piece, b)
+                nc.gpsimd.tensor_scalar(
+                    out=x_grp[piece, b][:].rearrange("p (i g) t -> p i g t", i=min(banks, 2)),
+                    in0=x_raw[b][:, :, first : first + P * banks].rearrange("p t (g i) -> p i g t", i=min(banks, 2)),
+                    scalar1=1.0,
+                    scalar2=0.0,
+                    op0=MULT,
+                    op1=ADD,
                 )
 
             def x_quant(piece, b):
@@ -516,6 +545,7 @@ def tile_multilatentattention_pb_v_kernel(tc, x, wd, wu, rope_cos, rope_sin, g, 
                 )
 
             out1_res = {}
+            out1_done = set()
 
             def out1_copy(piece, n, engine="scalar", rows=2):
                 first = X_PIECES[piece][0] + 256 * (n // 2)
@@ -528,7 +558,8 @@ def tile_multilatentattention_pb_v_kernel(tc, x, wd, wu, rope_cos, rope_sin, g, 
                     res[:, n % 2, :].rearrange("p (m u e) -> p m u e", u=2, e=2),
                     lambda bank: bank[:].rearrange("p (u m e) -> p m u e", u=2, e=2),
                 )
-                if n % 2 == rows - 1:
+                out1_done.add((piece, n))
+                if all((piece, n - n % 2 + j) in out1_done for j in range(rows)):
                     nc.sync.dma_start(out=out_1[first : first + P * rows].rearrange("(p i) l -> p i l", i=rows), in_=res[:])
 
             def out1_bank(piece, n, engine="scalar", rows=2):
@@ -557,7 +588,6 @@ def tile_multilatentattention_pb_v_kernel(tc, x, wd, wu, rope_cos, rope_sin, g, 
             load_g(6)
             load_g(7)
             tables_negate()
-            tables_sort()
             new_products(0)
             plain_product(0, SIN, 0, 8)
             plain_product(0, COS, 0, 8)
@@ -583,154 +613,165 @@ def tile_multilatentattention_pb_v_kernel(tc, x, wd, wu, rope_cos, rope_sin, g, 
             wu_row(2)
             rope_window(2, 5)
             sort_content(2, "scalar")
-            rope_own(2, 5)
-            dz1_passes(0, 0, 4, cols=slice(0, 256))
+            rope_own(2, 4)
+            dz1_passes(0, 0, 0, 4)
             wu_bank(3, 0)
             wu_bank(3, 1)
-            dz1_passes(0, 4, 6, cols=slice(0, 256))
+            dz1_passes(0, 0, 4, 6)
             wu_bank(3, 2)
             wu_quant(1)
             for b in range(B):
                 load_x(b)
-            for c in range(3):
-                dz2_bank(1, c)
+            dz2_turns(1)
+            dz2_copies(1, (0, 1))
             wd_bank(0)
-            dz1_passes(0, cols=slice(256, 512))
+            dz1_passes(0, 1)
             sort_content(3, "scalar")
+            dz2_copies(1, (2,), "vector")
             dz2_quant(1, 0, 4)
             dz2_quant(1, 4, 6)
-            rope_window(3, 5)
+            rope_window(3, 4)
             wd_bank(1)
             dz1_copy(0)
             wd_bank(2)
-            dz1_passes(1, 0, 3)
-            wd_bank(3)
-            rope_window(4, 5)
-            for c in range(3):
-                dz2_bank(2, c)
-            dz1_passes(1, 3, 6)
-            dz1_transpose(0)
-            dz1_copy(1)
-            rope_own(3, 5)
-            wd_quant(0)
+            dz1_passes(1, 0)
+            sort_content(4, "scalar")
+            wd_turn(3)
+            rope_window(4, 4)
+            dz2_turns(2)
+            dz2_copies(2, (0, 1, 2))
+            wd_copy(3)
+            dz1_passes(1, 1)
+            rope_own(3, 4)
             dz2_quant(2, 0, 4)
             dz2_quant(2, 4, 6)
-            dz1f_quant(0)
+            rope_window(5, 3)
             wd_turn(4)
-            sort_content(4, "scalar")
+            dz2_turns(3)
+            dz1_copy(1)
             wd_copy(4)
-            for c in range(3):
-                dz2_turn(3, c)
-            dz2_copy(3, 0)
-            dz2_copy(3, 1)
-            wd_quant(1)
-            rope_window(5, 0)
-            dz2_copy(3, 2, "vector")
-            dz1_passes(2)
-            dz1_copy(2)
-            dz1_transpose(1)
-            sort_content(5)
-            dz1f_quant(1)
+            dz2_copies(3, (0, 1, 2))
+            dz1_turn(0)
+            wd_turn(5)
+            dz1f_copy(0, "vector")
+            rope_own(4, 3)
+            wd_quant(0)
+            dz1f_quant(0, 2)
             dz2_quant(3, 0, 4)
             dz2_quant(3, 4, 6)
-            wd_bank(5)
-            wd_bank(6)
-            out0(0, (0, 1))
-            for c in range(3):
-                dz2_turn(4, c)
-            dz2_copy(4, 0)
-            dz2_copy(4, 1)
+            wd_copy(5)
+            wd_quant(1)
+            dz1_passes(2, 0)
+            dz1_passes(2, 1)
+            wd_turn(6)
             rope_window(6, 0)
-            dz2_copy(4, 2, "vector")
-            dz1_transpose(2)
-            dz1_passes(3)
-            sort_content(6, "scalar")
-            dz1_copy(3)
-            wd_quant(2)
-            dz1f_quant(2)
+            sort_content(5, "scalar")
+            dz1_copy(2)
+            dz2_turns(4)
+            wd_copy(6)
+            dz2_copies(4, (0, 1, 2))
+            out0_passes(0, (0,))
+            out0_passes(1, (0,))
+            out0_copies(0, (0,), "vector")
+            out0_copies(1, (0,))
+            dz1_passes(3, 0)
+            dz1_passes(3, 1)
+            out0_passes(0, (1,))
+            out0_passes(1, (1,))
             dz2_quant(4, 0, 4)
             dz2_quant(4, 4, 6)
-            wd_bank(7)
-            out0(1, (0, 1))
-            for c in range(3):
-                dz2_turn(5, c)
-            dz2_copy(5, 0)
-            dz2_copy(5, 1)
+            wd_quant(2)
             rope_window(7, 0)
-            dz2_copy(5, 2, "vector")
-            dz1_transpose(3)
-            out0(2, (0, 1))
-            out0(0, (2,))
-            out0(1, (2,))
+            wd_turn(7)
+            dz2_turns(5)
+            sort_content(6, "scalar")
+            dz1_copy(3)
+            dz1_turn(1)
+            out0_copies(0, (1,))
+            out0_copies(1, (1,))
+            dz2_copies(5, (0, 1, 2))
             feat_passes(4)
-            feat_copy(4)
-            sort_content(7, "scalar")
+            dz1f_copy(1)
+            wd_copy(7, "vector")
+            dz1f_quant(2, 2)
+            rope_own(7, 7)
             wd_quant(3)
-            dz1f_quant(3)
+            out0_passes(0, (2,))
+            out0_passes(1, (2,))
             dz2_quant(5, 0, 4)
             dz2_quant(5, 4, 6)
-            for c in range(3):
-                dz2_turn(6, c)
-            rope_own(7, 7)
+            feat_copy(4)
+            out0_copies(0, (2,))
+            out0_copies(1, (2,))
+            dz2_turns(6)
+            sort_content(7, "scalar")
             rope_finish(7, nc.gpsimd, 7)
             free_banks.append(7)
-            for c in range(3):
-                dz2_copy(6, c, "vector")
-            out0(0, (3,))
-            out0(1, (3,))
-            out0(2, (2, 3))
-            out0(3, (0, 1))
-            feat_passes(5)
-            feat_copy(5)
-            dz1f_quant(4)
+            dz2_copies(6, (0, 1, 2), "vector")
+            out0_passes(2, (0, 1))
+            out0_passes(0, (3,))
+            out0_passes(1, (3,))
+            out0_copies(2, (0, 1))
+            out0_copies(0, (3,))
+            out0_copies(1, (3,))
+            feat_passes(5, 0, 2)
+            out0_passes(2, (2, 3))
+            feat_passes(5, 2, 4)
+            out0_copies(2, (2, 3))
+            x_interleave(0, 0)
             dz2_quant(6, 0, 4)
             dz2_quant(6, 4, 6)
-            x_interleave(0, 0)
-            for c in range(3):
-                dz2_bank(7, c)
+            dz2_turns(7)
+            feat_copy(5)
+            dz1f_quant(4, 2)
             dz1_interleave(0)
+            dz2_copies(7, (0, 1, 2))
+            out0_passes(3)
             x_quant(0, 0)
-            dz1f_quant(5)
-            out0(3, (2, 3))
-            out0(4, (0, 1))
-            feat_passes(6)
             dz2_quant(7, 0, 4)
             dz2_quant(7, 4, 6)
+            out0_copies(3)
+            feat_passes(6, 0, 2)
+            out0_passes(4, (0, 1))
+            feat_passes(6, 2, 4)
             dz1_quant(0)
             x_interleave(0, 1)
-            feat_copy(6)
-            out0(4, (2, 3))
-            out0(5, (0, 1))
-            feat_passes(7)
-            feat_copy(7)
-            dz1f_quant(6)
-            x_quant(0, 1)
             x_interleave(1, 0)
-            x_interleave(1, 1)
-            dz1f_quant(7)
-            out0(5, (2, 3))
-            for n in range(2):
-                out0_pass(6, n)
+            out0_copies(4, (0, 1))
+            feat_copy(6)
+            out0_passes(4, (2, 3))
+            out0_copies(4, (2, 3))
+            out0_passes(5, (0, 1))
+            feat_passes(7)
+            out0_copies(5, (0,))
+            dz1f_quant(6, 1)
+            x_quant(0, 1)
+            out0_copies(5, (1,))
+            feat_copy(7, "vector")
+            x_quant(1, 0)
+            dz1f_quant(7, 1)
+            out0_passes(5, (2, 3))
+            out0_copies(5, (2, 3))
+            out0_passes(6, (0, 1))
             for u in range(2):
                 feat_turn(1, u)
-            for n in range(2):
-                out0_copy(6, n)
+            out0_copies(6, (0, 1))
             dz1t_copy(1, 0, "vector")
+            x_interleave_side(2, 0)
             dz1t_copy(1, 1, "vector")
-            for n in (2, 3):
-                out0_pass(6, n)
-                out0_copy(6, n, "scalar")
-            x_quant(1, 0)
+            out0_passes(6, (2, 3))
+            out0_copies(6, (2, 3))
+            x_quant(2, 0)
             dz1_quant(1)
-            out0(7)
+            out0_passes(7)
+            out0_copies(7)
             for i in range(2):
                 out1_pass(0, i, 0)
-            x_interleave(2, 0)
-            x_quant(1, 1)
+            x_interleave(1, 1)
             x_interleave(2, 1)
-            x_quant(2, 0)
-            x_quant(2, 1)
+            x_quant(1, 1)
             x_interleave(3, 0)
+            x_quant(2, 1)
             x_interleave(3, 1)
             x_quant(3, 0)
             x_interleave(4, 0)
@@ -741,7 +782,11 @@ def tile_multilatentattention_pb_v_kernel(tc, x, wd, wu, rope_cos, rope_sin, g, 
             x_quant(4, 1)
             x_interleave(5, 1)
             x_quant(5, 0)
+            x_interleave(6, 0)
             x_quant(5, 1)
+            x_interleave(6, 1)
+            x_quant(6, 0)
+            x_quant(6, 1)
             for n, (first, rows) in enumerate(X_PIECES):
                 for i in range(rows):
-                    out1_bank(n, i, "vector" if n >= 4 else "scalar", min(rows, 2))
+                    out1_bank(n, i, "vector" if n in (5, 6) else "scalar", min(rows, 2))

from contextlib import ExitStack

import concourse.mybir as mybir
from concourse.masks import make_identity

B, S, D, H, DH, DL, DR = 2, 512, 2048, 16, 128, 512, 64
T = B * S
J = H * (DH + DR)
FLOPS = 2 * T * J * DL + 2 * T * DL * D + 2 * D * T * DL

F32 = mybir.dt.float32
BF16 = mybir.dt.bfloat16
U32 = mybir.dt.uint32
U8 = mybir.dt.uint8
E4M3 = mybir.dt.float8_e4m3fn_x4
E5M2 = mybir.dt.float8_e5m2_x4
MULT = mybir.AluOpType.mult
ADD = mybir.AluOpType.add

P = 128
PASSES = J // 512
TILES = T // P
GTILES = S // P
HF = DH + DR
KIB = 1024
COS, SIN = 0, 1
OWN_HEADS = 4
SORTED_SLOTS = 3
GRAD_SLOTS = 4
WHOLE_FROM = 8
X_PIECES = ((0, 4), (512, 4), (1024, 2), (1280, 2), (1536, 2), (1792, 1), (1920, 1))
RESULT_SLOTS = 10


def tile_multilatentattention_pb_v_kernel(tc, x, wd, wu, rope_cos, rope_sin, g, out_0, out_1):
    nc = tc.nc

    g_view = g.rearrange("b (p j) h f -> b p j h f", j=4)
    x_view = x.rearrange("b (p j) d -> b p j d", j=4)
    wu_view = wu.rearrange("(p r) f -> p r f", r=4)
    wd_view = wd.rearrange("(n p i) l -> p n i l", p=P, i=4)
    cos_view = rope_cos.rearrange("(p j) r -> p j r", j=4)
    sin_view = rope_sin.rearrange("(p j) r -> p j r", j=4)
    out0_view = out_0.rearrange("b (p j) d -> b p j d", j=4)

    with ExitStack() as ctx:
        keep = ctx.enter_context(tc.tile_pool(name="keep", bufs=1))
        arena = ctx.enter_context(tc.tile_pool(name="arena", bufs=1))
        work = ctx.enter_context(tc.tile_pool(name="work", bufs=2))
        psum = ctx.enter_context(tc.psum_pool(name="psum", bufs=1))

        ident = keep.tile([P, P], F32, name="ident", align_bytes=64)
        ident_first = keep.tile([P, P], F32, name="ident_first", align_bytes=64)
        make_identity(nc, ident_first[:])

        tables = keep.tile([P, 2, 4, DR], F32, name="tables", align_bytes=64)
        tables_t = arena.tile([P, 4, P], F32, name="tables_t", offset=66 * KIB, align_bytes=64)
        tables_psum = psum.tile([P, 2, 4, DR], F32, name="tables_psum", tag="bank7")
        wu_codes = keep.tile([P, 2, PASSES, DL // 2], U32, name="wu_codes", align_bytes=64)
        wu_scales = keep.tile([P, 2, PASSES, DL // 2], U8, name="wu_scales", align_bytes=64)
        wd_codes = keep.tile([P, D], U32, name="wd_codes", align_bytes=64)
        wd_scales = keep.tile([P, D], U8, name="wd_scales", align_bytes=64)
        x_codes = keep.tile([P, B, D], U32, name="x_codes", align_bytes=64)
        x_scales = keep.tile([P, B, D], U8, name="x_scales", align_bytes=64)

        with tc.manual_schedule():
            nc.scalar.copy(out=ident[:], in_=ident_first[:])

            wu_raw, g_raw, wd_raw, x_raw = {}, {}, {}, {}

            def load_tables():
                nc.sync.dma_start(out=tables[:, SIN], in_=sin_view)
                nc.sync.dma_start(out=tables[:, COS], in_=cos_view)

            def load_g(k):
                t = work.tile([P, H, HF], BF16, name=f"g{k}", tag="g", bufs=GRAD_SLOTS, align_bytes=64)
                nc.sync.dma_start(out=t[:], in_=g_view[k // GTILES][:, k % GTILES])
                g_raw[k] = [t]

            def load_first_g(half):
                t = arena.tile([P, H // 2, HF], BF16, name=f"g0_{half}", offset=KIB * (24 + 3 * half), align_bytes=64)
                nc.sync.dma_start(out=t[:], in_=g_view[0][:, 0, half * H // 2 : (half + 1) * H // 2])
                g_raw.setdefault(0, []).append(t)

            def load_wu(r, lo=0, hi=PASSES):
                t = arena.tile([P, 512 * (hi - lo)], BF16, name=f"wu{r}_{lo}", offset=KIB * (PASSES * r + lo), align_bytes=64)
                nc.sync.dma_start(out=t[:], in_=wu_view[:, r, 512 * lo : 512 * hi])
                for s in range(lo, hi):
                    wu_raw[r, s] = t[:, 512 * (s - lo) : 512 * (s - lo + 1)]

            def load_wd(c):
                t = arena.tile([P, 4, DL], BF16, name=f"wd{c}", offset=KIB * (24 + 4 * c), align_bytes=64)
                nc.sync.dma_start(out=t[:], in_=wd_view[:, c])
                wd_raw[c] = t

            def load_x(b, lo=0, hi=4):
                if b not in x_raw:
                    x_raw[b] = arena.tile([P, 4, D], BF16, name=f"x{b}", offset=KIB * (40 + 16 * b), align_bytes=64)
                nc.sync.dma_start(out=x_raw[b][:, lo:hi], in_=x_view[b][:, lo:hi])

            def copy(engine, out, in_):
                if engine == "vector":
                    nc.vector.tensor_copy(out=out, in_=in_)
                else:
                    nc.scalar.copy(out=out, in_=in_)

            free_banks = list(range(7))
            bank_of = {}

            def new_bank(key):
                n = free_banks.pop(0)
                bank_of[key] = (n, psum.tile([P, 512], F32, name=f"bank{n}", tag=f"bank{n}"))
                return bank_of[key][1]

            def empty_bank(key, engine, out, view):
                n, bank = bank_of.pop(key)
                copy(engine, out, view(bank))
                free_banks.append(n)

            def transpose_pairs(bank, rows):
                for i in range(2):
                    words = rows[i].bitcast(F32)
                    for u in range(2):
                        q = 2 * i + u
                        nc.tensor.transpose(bank[:, q * P : (q + 1) * P], words[:, u:256:2], ident[:])

            def tables_negate():
                nc.scalar.mul(out=tables[:, SIN, :, 0:32], in_=tables[:, SIN, :, 0:32], mul=-1.0)

            def tables_turn():
                bank = new_bank("tables")
                flat = tables[:].rearrange("p a j r -> p (a j r)")
                for q in (2, 3, 0, 1):
                    nc.tensor.transpose(bank[:, q * P : (q + 1) * P], flat[:, q * P : (q + 1) * P], ident[:])
                empty_bank("tables", "scalar", tables_t[:].rearrange("p j c -> p (j c)"), lambda bank: bank[:])

            def tables_turn_back():
                flat = tables_psum[:].rearrange("p a j r -> p (a j r)")
                for q in range(4):
                    nc.tensor.transpose(flat[:, q * P : (q + 1) * P], tables_t[:, q, :], ident[:])

            def rope_part(k, lo, hi):
                parts = g_raw[k]
                per = H // len(parts)
                return parts[lo // per][:, lo % per : lo % per + hi - lo, DH:HF]

            products = {}

            def new_products(k):
                products[k] = [work.tile([P, H * DR], F32, name=n, tag=n, bufs=2, align_bytes=64) for n in ("pc", "ps")]

            def plain_product(k, which, lo, hi):
                row = tables[:, which, k, :].rearrange("p (a j) -> p a j", a=2).unsqueeze(1).to_broadcast([P, hi - lo, 2, 32])
                out = products[k][which][:].rearrange("p (h a j) -> p h a j", h=H, a=2)[:, lo:hi]
                if which == SIN:
                    out = out[:, :, ::-1]
                rope = rope_part(k, lo, hi).rearrange("p h (a j) -> p h a j", a=2)
                nc.vector.tensor_tensor(out=out, in0=rope, in1=row, op=MULT)

            def plain_sum(k, lo, hi):
                pc, ps = [t[:].rearrange("p (h f) -> p h f", h=H)[:, lo:hi] for t in products[k]]
                nc.vector.tensor_tensor(out=rope_part(k, lo, hi), in0=pc, in1=ps, op=ADD)

            g_sorted = {}

            def new_sorted(k):
                if k not in g_sorted:
                    g_sorted[k] = work.tile([P, 2, H, HF // 4], F32, name="g_sorted", tag="gs", bufs=SORTED_SLOTS, align_bytes=64)
                return g_sorted[k]

            def sort_content(k, engine="vector"):
                t = new_sorted(k)
                words = g_raw[k][0][:].bitcast(F32)[:, :, : DH // 2]
                copy(
                    engine,
                    t[:, :, :, : DH // 4].rearrange("p u h (g l) -> p h g u l", l=4),
                    words.rearrange("p h (g l u) -> p h g u l", l=4, u=2),
                )

            def sorted_product(k, which, u, lo, hi):
                rope = rope_part(k, lo, hi).rearrange("p h (a m u e) -> p h a m u e", a=2, u=2, e=2)[:, :, :, :, u, :]
                row = tables_psum[:, which, k % 4, :].rearrange("p (a m u e) -> p a m u e", a=2, u=2, e=2)[:, :, :, u, :]
                out = products[k][which][:].rearrange("p (u h a m e) -> p u h a m e", u=2, h=H, a=2, e=2)[:, u, lo:hi]
                if which == SIN:
                    out = out[:, :, ::-1]
                nc.vector.tensor_tensor(out=out, in0=rope, in1=row.unsqueeze(1).to_broadcast([P, hi - lo, 2, 8, 2]), op=MULT)

            def sorted_sum(engine, k, lo, hi):
                pc, ps = [t[:].rearrange("p (u h f) -> p u h f", u=2, h=H)[:, :, lo:hi] for t in products[k]]
                out = new_sorted(k)[:].bitcast(BF16)[:, :, lo:hi, DH // 2 :]
                engine.tensor_tensor(out=out, in0=pc, in1=ps, op=ADD)

            def rope_products(k):
                new_products(k)
                sorted_product(k, COS, 0, 0, H)
                sorted_product(k, COS, 1, 0, H)
                sorted_product(k, SIN, 1, 0, H)
                sorted_product(k, SIN, 0, 0, H - 2)

            def rope_finish(k, engine, own=OWN_HEADS):
                sorted_product(k, SIN, 0, H - 2, H)
                sorted_sum(engine, k, own, H)

            def rope_window(k, own=OWN_HEADS):
                rope_finish(k - 1, nc.gpsimd, own)
                rope_products(k)

            def rope_own(k, own=OWN_HEADS):
                sorted_sum(nc.vector, k, 0, own)

            wu_grp = {}

            def wu_turn(r, c):
                transpose_pairs(new_bank(("wu", r, c)), [wu_raw[r, 2 * c + i] for i in range(2)])

            def wu_copy(r, c, engine="scalar"):
                if (r // 2, c) not in wu_grp:
                    offset = KIB * (40 + 4 * (3 * (r // 2) + c))
                    wu_grp[r // 2, c] = arena.tile([P, 2, 2, 512], BF16, name=f"wu_grp{r}_{c}", offset=offset, align_bytes=64)
                empty_bank(
                    ("wu", r, c),
                    engine,
                    wu_grp[r // 2, c][:, :, r % 2, :].bitcast(F32).rearrange("p i (m u) -> p i m u", u=2),
                    lambda bank: bank[:].rearrange("p (i u m) -> p i m u", i=2, u=2),
                )

            def wu_bank(r, c):
                wu_turn(r, c)
                wu_copy(r, c)

            def wu_row(r):
                for c in range(3):
                    wu_bank(r, c)

            def wu_quant(pair, lo=0, hi=3):
                for c in range(lo, hi):
                    nc.vector.quantize_mx(
                        out=wu_codes[:, pair, 2 * c : 2 * c + 2].rearrange("p s l -> p (s l)").bitcast(E4M3),
                        scales=wu_scales[:, pair, 2 * c : 2 * c + 2].rearrange("p s l -> p (s l)"),
                        in_=wu_grp[pair, c][:].rearrange("p s r c -> p (s r c)"),
                    )

            wd_grp = {}

            def wd_turn(n):
                c, half = n // 2, n % 2
                transpose_pairs(new_bank(("wd", n)), [wd_raw[c][:, 2 * half + i, :] for i in range(2)])

            def wd_copy(n, engine="scalar"):
                c, half = n // 2, n % 2
                if c not in wd_grp:
                    wd_grp[c] = work.tile([P, 2048], BF16, name="wd_grp", tag="xgrp", bufs=3, align_bytes=64)
                empty_bank(
                    ("wd", n),
                    engine,
                    wd_grp[c][:].bitcast(F32).rearrange("p (m i u) -> p m i u", i=4, u=2)[:, :, 2 * half : 2 * half + 2, :],
                    lambda bank: bank[:].rearrange("p (i u m) -> p m i u", i=2, u=2),
                )

            def wd_bank(n):
                wd_turn(n)
                wd_copy(n)

            def wd_quant(c):
                nc.vector.quantize_mx(
                    out=wd_codes[:, 512 * c : 512 * c + 512].bitcast(E4M3),
                    scales=wd_scales[:, 512 * c : 512 * c + 512],
                    in_=wd_grp[c][:],
                )

            def g_pass(k, s):
                parts = g_raw[k]
                per = PASSES // len(parts)
                flat = parts[s // per][:].rearrange("p h f -> p (h f)")
                return flat[:, 512 * (s % per) : 512 * (s % per) + 512]

            dz2_grp = {}

            def dz2_turn(k, c):
                bank = new_bank(("dz2", k, c))
                if k in g_sorted:
                    words = g_sorted[k][:].rearrange("p u h m -> p u (h m)")
                    for i in range(2):
                        for u in range(2):
                            q, s = 2 * i + u, 2 * c + i
                            nc.tensor.transpose(bank[:, q * P : (q + 1) * P], words[:, u, P * s : P * s + P], ident[:])
                else:
                    transpose_pairs(bank, [g_pass(k, 2 * c + i) for i in range(2)])

            def dz2_copy(k, c, engine="scalar"):
                if k not in dz2_grp:
                    dz2_grp[k] = work.tile([P, J], BF16, name="dz2_grp", tag="dz2g", bufs=2, align_bytes=64)
                empty_bank(
                    ("dz2", k, c),
                    engine,
                    dz2_grp[k][:, 1024 * c : 1024 * c + 1024].bitcast(F32).rearrange("p (i r u) -> p i r u", i=2, u=2),
                    lambda bank: bank[:].rearrange("p (i u r) -> p i r u", i=2, u=2),
                )

            def dz2_bank(k, c, engine="scalar"):
                dz2_turn(k, c)
                dz2_copy(k, c, engine)

            dz2 = {}

            def dz2_quant(k, lo, hi):
                if k not in dz2:
                    codes = work.tile([P, PASSES, P], U32, name="dz2_codes", tag="dz2c", bufs=3, align_bytes=64)
                    scales = work.tile([P, PASSES, P], U8, name="dz2_scales", tag="dz2s", bufs=3, align_bytes=64)
                    dz2[k] = (codes, scales)
                codes, scales = dz2[k]
                nc.vector.quantize_mx(
                    out=codes[:, lo:hi, :].rearrange("p s r -> p (s r)").bitcast(E5M2),
                    scales=scales[:, lo:hi, :].rearrange("p s r -> p (s r)"),
                    in_=dz2_grp[k][:, 512 * lo : 512 * hi],
                )

            dz1_tok = {}
            dz1_acc = {}

            def dz1_passes(k, half, lo=0, hi=PASSES):
                codes, scales = dz2[k]
                if k not in dz1_acc:
                    dz1_acc[k] = new_bank(("dz1", k))
                for s in range(lo, hi):
                    nc.tensor.matmul_mx(
                        out=dz1_acc[k][:, 256 * half : 256 * half + 256],
                        lhsT=codes[:, s, :].bitcast(E5M2),
                        lhsT_scale=scales[:, s, :],
                        rhs=wu_codes[:, half, s].bitcast(E4M3),
                        rhs_scale=wu_scales[:, half, s],
                        start=(s == 0),
                        stop=(s == PASSES - 1),
                    )

            def dz1_copy(k, engine="scalar"):
                if k % GTILES == 0:
                    dz1_tok[k // GTILES] = work.tile([P, GTILES, DL], BF16, name="dz1_tok", tag="dz1t", bufs=2, align_bytes=64)
                empty_bank(
                    ("dz1", k),
                    engine,
                    dz1_tok[k // GTILES][:, k % GTILES, :].rearrange("p (u m e) -> p u m e", u=2, e=2),
                    lambda bank: bank[:].rearrange("p (u e m) -> p u m e", u=2, e=2),
                )

            dz1f_grp = {}

            def dz1_turn(q):
                bank = new_bank(("dz1f", q))
                for j in range(2):
                    words = dz1_tok[0][:, 2 * q + j, :].bitcast(F32)
                    for u in range(2):
                        nc.tensor.transpose(bank[:, (2 * j + u) * P : (2 * j + u + 1) * P], words[:, u * P : (u + 1) * P], ident[:])

            def dz1f_copy(q, engine="scalar"):
                dz1f_grp[q] = work.tile([P, 2 * DL], BF16, name="dz1f_grp", tag="dz1fg", bufs=1, align_bytes=64)
                empty_bank(
                    ("dz1f", q),
                    engine,
                    dz1f_grp[q][:].bitcast(F32).rearrange("p (j r u) -> p j r u", j=2, u=2),
                    lambda bank: bank[:].rearrange("p (j u r) -> p j r u", j=2, u=2),
                )

            dz1f = {}

            dz1_feat = {}

            def feat_passes(k, lo=0, hi=4):
                codes, scales = dz2[k]
                if k not in dz1_acc:
                    dz1_acc[k] = new_bank(("dz1", k))
                for t in range(lo, hi):
                    for s in range(PASSES):
                        nc.tensor.matmul_mx(
                            out=dz1_acc[k][:, P * t : P * t + P],
                            lhsT=wu_codes[:, t // 2, s, P * (t % 2) : P * (t % 2) + P].bitcast(E4M3),
                            lhsT_scale=wu_scales[:, t // 2, s, P * (t % 2) : P * (t % 2) + P],
                            rhs=codes[:, s, :].bitcast(E5M2),
                            rhs_scale=scales[:, s, :],
                            start=(s == 0),
                            stop=(s == PASSES - 1),
                        )

            def feat_copy(k, engine="scalar"):
                if k % GTILES == 0:
                    dz1_feat[k // GTILES] = work.tile([P, GTILES, DL], BF16, name="dz1_feat", tag="dz1t", bufs=2, align_bytes=64)
                empty_bank(
                    ("dz1", k),
                    engine,
                    dz1_feat[k // GTILES][:, k % GTILES, :].rearrange("p (n t) -> p n t", t=4),
                    lambda bank: bank[:].rearrange("p (t n) -> p n t", t=4),
                )

            def dz1f_quant(k, n=1):
                codes = work.tile([P, n * P], U32, name="dz1f_codes", tag="dz1fc", bufs=3, align_bytes=64)
                scales = work.tile([P, n * P], U8, name="dz1f_scales", tag="dz1fs", bufs=3, align_bytes=64)
                if k < GTILES:
                    src = dz1f_grp[k // 2][:]
                else:
                    src = dz1_feat[1][:, k - GTILES : k - GTILES + n, :].rearrange("p j c -> p (j c)")
                nc.vector.quantize_mx(out=codes[:].bitcast(E5M2), scales=scales[:], in_=src)
                for j in range(n):
                    dz1f[k + j] = (codes[:, P * j : P * j + P], scales[:, P * j : P * j + P])

            results = []

            def new_result(banks):
                if banks == 4 and len(results) % 2 == 1:
                    results.append(None)
                slot = len(results) % RESULT_SLOTS
                t = arena.tile([P, banks, 512], F32, name=f"res{len(results)}", offset=4 * KIB * slot, align_bytes=64)
                results.extend([t] * ((banks + 1) // 2))
                return t

            def out0_pass(k, n):
                codes, scales = dz1f[k]
                nc.tensor.matmul_mx(
                    out=new_bank(("out0", k, n))[:],
                    lhsT=codes.bitcast(E5M2),
                    lhsT_scale=scales,
                    rhs=wd_codes[:, 512 * n : 512 * n + 512].bitcast(E4M3),
                    rhs_scale=wd_scales[:, 512 * n : 512 * n + 512],
                    start=True,
                    stop=True,
                )

            out0_res = {}
            out0_done = set()

            def out0_copy(k, n, engine="scalar"):
                banks = 4 if k >= WHOLE_FROM else 2
                part, i = divmod(n, banks)
                if (k, part) not in out0_res:
                    out0_res[k, part] = new_result(banks)
                res = out0_res[k, part]
                empty_bank(("out0", k, n), engine, res[:, i, :], lambda bank: bank[:])
                out0_done.add((k, n))
                if all((k, banks * part + j) in out0_done for j in range(banks)):
                    nc.sync.dma_start(
                        out=out0_view[k // GTILES][:, k % GTILES, 512 * banks * part : 512 * banks * (part + 1)],
                        in_=res[:].rearrange("p i c -> p (i c)"),
                    )

            def out0_passes(k, blocks=range(4)):
                for n in blocks:
                    out0_pass(k, n)

            def out0_copies(k, blocks=range(4), engine="scalar"):
                for n in blocks:
                    out0_copy(k, n, engine)

            def dz2_turns(k):
                for c in range(3):
                    dz2_turn(k, c)

            def dz2_copies(k, order=(1, 0, 2), engine="scalar"):
                for c in order:
                    dz2_copy(k, c, engine)

            dz1 = {}
            dz1_grp = {}

            def dz1_interleave(b):
                dz1_grp[b] = work.tile([P, DL, 4], BF16, name="dz1_grp", tag="xgrp", bufs=3, align_bytes=64)
                nc.vector.tensor_copy(
                    out=dz1_grp[b][:].rearrange("p (g l) t -> p g t l", l=4),
                    in_=dz1_tok[b][:].rearrange("p t (g l) -> p g t l", l=4),
                )

            def feat_turn(b, u, lo=0, hi=GTILES):
                bank = new_bank(("dz1t", b, u)) if lo == 0 else bank_of["dz1t", b, u][1]
                for j in range(lo, hi):
                    words = dz1_feat[b][:, j, :].bitcast(F32).rearrange("p (n u) -> p u n", u=2)
                    nc.tensor.transpose(bank[:, j * P : (j + 1) * P], words[:, u, :], ident[:])

            def dz1t_copy(b, u, engine="scalar"):
                if b not in dz1_grp:
                    dz1_grp[b] = work.tile([P, DL, 4], BF16, name="dz1_grp", tag="xgrp", bufs=3, align_bytes=64)
                empty_bank(
                    ("dz1t", b, u),
                    engine,
                    dz1_grp[b][:, 256 * u : 256 * u + 256, :],
                    lambda bank: bank[:].bitcast(BF16).rearrange("p (j c) -> p c j", j=4),
                )

            def dz1_quant(b):
                codes = keep.tile([P, DL], U32, name=f"dz1_codes{b}", align_bytes=64)
                scales = keep.tile([P, DL], U8, name=f"dz1_scales{b}", align_bytes=64)
                nc.vector.quantize_mx(
                    out=codes[:].bitcast(E5M2), scales=scales[:], in_=dz1_grp[b][:].rearrange("p c t -> p (c t)")
                )
                dz1[b] = (codes, scales)

            x_grp = {}

            def new_x_grp(piece, b):
                tag, bufs = ("xside", 1) if (piece, b) in ((1, 0), (2, 0)) else ("xgrp", 3)
                x_grp[piece, b] = work.tile([P, P * X_PIECES[piece][1], 4], BF16, name="x_grp", tag=tag, bufs=bufs, align_bytes=64)

            def x_interleave(piece, b):
                first, banks = X_PIECES[piece]
                rows = min(banks, 2)
                new_x_grp(piece, b)
                nc.vector.tensor_copy(
                    out=x_grp[piece, b][:].rearrange("p (i g l) t -> p g t l i", i=rows, l=4 // rows),
                    in_=x_raw[b][:, :, first : first + P * banks].rearrange("p t (g l i) -> p g t l i", i=rows, l=4 // rows),
                )

            def x_interleave_side(piece, b):
                first, banks = X_PIECES[piece]
                new_x_grp(piece, b)
                nc.gpsimd.tensor_scalar(
                    out=x_grp[piece, b][:].rearrange("p (i g) t -> p i g t", i=min(banks, 2)),
                    in0=x_raw[b][:, :, first : first + P * banks].rearrange("p t (g i) -> p i g t", i=min(banks, 2)),
                    scalar1=1.0,
                    scalar2=0.0,
                    op0=MULT,
                    op1=ADD,
                )

            def x_quant(piece, b):
                first, banks = X_PIECES[piece]
                nc.vector.quantize_mx(
                    out=x_codes[:, b, first : first + P * banks].bitcast(E4M3),
                    scales=x_scales[:, b, first : first + P * banks],
                    in_=x_grp[piece, b][:].rearrange("p c t -> p (c t)"),
                )

            out1_acc = {}

            def out1_pass(piece, n, b):
                if b == 0:
                    out1_acc[piece, n] = new_bank(("out1", piece, n))
                codes, scales = dz1[b]
                first, banks = X_PIECES[piece]
                col = first + P * (n // 2 + banks // 2 * (n % 2))
                nc.tensor.matmul_mx(
                    out=out1_acc[piece, n][:],
                    lhsT=x_codes[:, b, col : col + P].bitcast(E4M3),
                    lhsT_scale=x_scales[:, b, col : col + P],
                    rhs=codes[:].bitcast(E5M2),
                    rhs_scale=scales[:],
                    start=(b == 0),
                    stop=(b == B - 1),
                )

            out1_res = {}
            out1_done = set()

            def out1_copy(piece, n, engine="scalar", rows=2):
                first = X_PIECES[piece][0] + 256 * (n // 2)
                if (piece, n // 2) not in out1_res:
                    out1_res[piece, n // 2] = new_result(rows)
                res = out1_res[piece, n // 2]
                empty_bank(
                    ("out1", piece, n),
                    engine,
                    res[:, n % 2, :].rearrange("p (m u e) -> p m u e", u=2, e=2),
                    lambda bank: bank[:].rearrange("p (u m e) -> p m u e", u=2, e=2),
                )
                out1_done.add((piece, n))
                if all((piece, n - n % 2 + j) in out1_done for j in range(rows)):
                    nc.sync.dma_start(out=out_1[first : first + P * rows].rearrange("(p i) l -> p i l", i=rows), in_=res[:])

            def out1_bank(piece, n, engine="scalar", rows=2):
                if (piece, n) not in out1_acc:
                    out1_pass(piece, n, 0)
                out1_pass(piece, n, 1)
                out1_copy(piece, n, engine, rows)

            load_tables()
            load_first_g(0)
            load_wu(0, 0, 2)
            load_first_g(1)
            load_wu(0, 2, PASSES)
            load_g(1)
            load_wu(1)
            load_wu(2)
            load_g(2)
            load_wu(3)
            load_wd(0)
            load_g(3)
            load_wd(1)
            load_g(4)
            load_wd(2)
            load_g(5)
            load_wd(3)
            load_g(6)
            load_g(7)
            tables_negate()
            new_products(0)
            plain_product(0, SIN, 0, 8)
            plain_product(0, COS, 0, 8)
            plain_sum(0, 0, 8)
            plain_product(0, COS, 8, H)
            plain_product(0, SIN, 8, H)
            tables_turn()
            wu_bank(0, 0)
            plain_sum(0, 8, H)
            tables_turn_back()
            dz2_bank(0, 0)
            wu_bank(0, 1)
            wu_bank(0, 2)
            rope_products(1)
            dz2_bank(0, 1)
            dz2_bank(0, 2)
            sort_content(1, "scalar")
            wu_row(1)
            dz2_quant(0, 0, 4)
            rope_own(1, 5)
            dz2_quant(0, 4, 6)
            wu_quant(0)
            wu_row(2)
            rope_window(2, 5)
            sort_content(2, "scalar")
            rope_own(2, 4)
            dz1_passes(0, 0, 0, 4)
            wu_bank(3, 0)
            wu_bank(3, 1)
            dz1_passes(0, 0, 4, 6)
            wu_bank(3, 2)
            wu_quant(1)
            for b in range(B):
                load_x(b)
            dz2_turns(1)
            dz2_copies(1, (0, 1))
            wd_bank(0)
            dz1_passes(0, 1)
            sort_content(3, "scalar")
            dz2_copies(1, (2,), "vector")
            dz2_quant(1, 0, 4)
            dz2_quant(1, 4, 6)
            rope_window(3, 4)
            wd_bank(1)
            dz1_copy(0)
            wd_bank(2)
            dz1_passes(1, 0)
            sort_content(4, "scalar")
            wd_turn(3)
            rope_window(4, 4)
            dz2_turns(2)
            dz2_copies(2, (0, 1, 2))
            wd_copy(3)
            dz1_passes(1, 1)
            rope_own(3, 4)
            dz2_quant(2, 0, 4)
            dz2_quant(2, 4, 6)
            rope_window(5, 3)
            wd_turn(4)
            dz2_turns(3)
            dz1_copy(1)
            wd_copy(4)
            dz2_copies(3, (0, 1, 2))
            dz1_turn(0)
            wd_turn(5)
            dz1f_copy(0, "vector")
            rope_own(4, 3)
            wd_quant(0)
            dz1f_quant(0, 2)
            dz2_quant(3, 0, 4)
            dz2_quant(3, 4, 6)
            wd_copy(5)
            wd_quant(1)
            dz1_passes(2, 0)
            dz1_passes(2, 1)
            wd_turn(6)
            rope_window(6, 0)
            sort_content(5, "scalar")
            dz1_copy(2)
            dz2_turns(4)
            wd_copy(6)
            dz2_copies(4, (0, 1, 2))
            out0_passes(0, (0,))
            out0_passes(1, (0,))
            out0_copies(0, (0,), "vector")
            out0_copies(1, (0,))
            dz1_passes(3, 0)
            dz1_passes(3, 1)
            out0_passes(0, (1,))
            out0_passes(1, (1,))
            dz2_quant(4, 0, 4)
            dz2_quant(4, 4, 6)
            wd_quant(2)
            rope_window(7, 0)
            wd_turn(7)
            dz2_turns(5)
            sort_content(6, "scalar")
            dz1_copy(3)
            dz1_turn(1)
            out0_copies(0, (1,))
            out0_copies(1, (1,))
            dz2_copies(5, (0, 1, 2))
            feat_passes(4)
            dz1f_copy(1)
            wd_copy(7, "vector")
            dz1f_quant(2, 2)
            rope_own(7, 7)
            wd_quant(3)
            out0_passes(0, (2,))
            out0_passes(1, (2,))
            dz2_quant(5, 0, 4)
            dz2_quant(5, 4, 6)
            feat_copy(4)
            out0_copies(0, (2,))
            out0_copies(1, (2,))
            dz2_turns(6)
            sort_content(7, "scalar")
            rope_finish(7, nc.gpsimd, 7)
            free_banks.append(7)
            dz2_copies(6, (0, 1, 2), "vector")
            out0_passes(2, (0, 1))
            out0_passes(0, (3,))
            out0_passes(1, (3,))
            out0_copies(2, (0, 1))
            out0_copies(0, (3,))
            out0_copies(1, (3,))
            feat_passes(5, 0, 2)
            out0_passes(2, (2, 3))
            feat_passes(5, 2, 4)
            out0_copies(2, (2, 3))
            x_interleave(0, 0)
            dz2_quant(6, 0, 4)
            dz2_quant(6, 4, 6)
            dz2_turns(7)
            feat_copy(5)
            dz1f_quant(4, 2)
            dz1_interleave(0)
            dz2_copies(7, (0, 1, 2))
            out0_passes(3)
            x_quant(0, 0)
            dz2_quant(7, 0, 4)
            dz2_quant(7, 4, 6)
            out0_copies(3)
            feat_passes(6, 0, 2)
            out0_passes(4, (0, 1))
            feat_passes(6, 2, 4)
            dz1_quant(0)
            x_interleave(0, 1)
            x_interleave(1, 0)
            out0_copies(4, (0, 1))
            feat_copy(6)
            out0_passes(4, (2, 3))
            out0_copies(4, (2, 3))
            out0_passes(5, (0, 1))
            feat_passes(7)
            out0_copies(5, (0,))
            dz1f_quant(6, 1)
            x_quant(0, 1)
            out0_copies(5, (1,))
            feat_copy(7, "vector")
            x_quant(1, 0)
            dz1f_quant(7, 1)
            out0_passes(5, (2, 3))
            out0_copies(5, (2, 3))
            out0_passes(6, (0, 1))
            for u in range(2):
                feat_turn(1, u)
            out0_copies(6, (0, 1))
            dz1t_copy(1, 0, "vector")
            x_interleave_side(2, 0)
            dz1t_copy(1, 1, "vector")
            out0_passes(6, (2, 3))
            out0_copies(6, (2, 3))
            x_quant(2, 0)
            dz1_quant(1)
            out0_passes(7)
            out0_copies(7)
            for i in range(2):
                out1_pass(0, i, 0)
            x_interleave(1, 1)
            x_interleave(2, 1)
            x_quant(1, 1)
            x_interleave(3, 0)
            x_quant(2, 1)
            x_interleave(3, 1)
            x_quant(3, 0)
            x_interleave(4, 0)
            x_quant(3, 1)
            x_interleave(4, 1)
            x_quant(4, 0)
            x_interleave(5, 0)
            x_quant(4, 1)
            x_interleave(5, 1)
            x_quant(5, 0)
            x_interleave(6, 0)
            x_quant(5, 1)
            x_interleave(6, 1)
            x_quant(6, 0)
            x_quant(6, 1)
            for n, (first, rows) in enumerate(X_PIECES):
                for i in range(rows):
                    out1_bank(n, i, "vector" if n in (5, 6) else "scalar", min(rows, 2))
